import numpy as np
import ml_dtypes


def mxq(x, axis, fmt="e4m3"):
    dtype, down = {"e4m3": (ml_dtypes.float8_e4m3fn, 7), "e5m2": (ml_dtypes.float8_e5m2, 14)}[fmt]
    v = np.moveaxis(np.asarray(x, np.float32).astype(ml_dtypes.bfloat16).astype(np.float64), axis, -1)
    blocks = v.reshape(v.shape[:-1] + (-1, 32))
    amax = np.abs(blocks).max(-1, keepdims=True)
    byte = np.maximum(np.where(amax > 0, np.frexp(amax)[1] - 1 + 127, 0) - down, 1)
    scale = np.exp2(byte - 127.0)
    codes = (blocks / scale).astype(np.float32).astype(dtype).astype(np.float64)
    return np.moveaxis((codes * scale).reshape(v.shape), -1, axis)


WIDE = False


def mx_kscale(k):
    if not WIDE:
        return np.ones(k)
    levels = np.array([10, -10, 5, -5, 0])
    a = np.random.permutation(np.resize(levels, k // 512 * 4)).reshape(k // 512, 4)
    idx = np.arange(k)
    return np.exp2(a[idx // 512, idx % 128 // 32])


BF16 = ml_dtypes.bfloat16


def bf(x):
    return np.asarray(x, np.float32).astype(BF16)


def f64(x):
    return np.asarray(x).astype(np.float64)


E2M1 = np.array([0.0, 0.5, 1.0, 1.5, 2.0, 3.0, 4.0, 6.0, -0.0, -0.5, -1.0, -1.5, -2.0, -3.0, -4.0, -6.0])


def pack_weight(w, fmt):
    k, n = w.shape
    w = f64(bf(w)).reshape(k // 32, 32, n)
    amax = np.abs(w).max(1)
    if fmt == "e4m3":
        byte = np.frexp(amax)[1] - 1 + 127 - 7
    else:
        mant, ex = np.frexp(amax / 6.0)
        byte = np.where(mant > 0.5, ex, ex - 1) + 127
    byte = np.clip(np.where(amax > 0, byte, 1), 1, 254)
    scaled = (w * np.exp2(127.0 - byte)[:, None, :]).reshape(k, n).astype(np.float32)
    by_word = np.ascontiguousarray(scaled.reshape(k // 512, 128, 4, n).transpose(0, 1, 3, 2))
    if fmt == "e4m3":
        words = by_word.astype(ml_dtypes.float8_e4m3fn).view(np.uint8)
    else:
        c = by_word.astype(ml_dtypes.float4_e2m1fn).view(np.uint8) & 0xF
        words = c[..., 0::2] | (c[..., 1::2] << 4)
    return np.ascontiguousarray(words), np.ascontiguousarray(byte.astype(np.uint8).reshape(k // 512, 16, n))


def unpack_weight(words, scales, fmt):
    g, p, n, _ = words.shape
    if fmt == "e4m3":
        vals = np.ascontiguousarray(words).view(ml_dtypes.float8_e4m3fn).astype(np.float64)
    else:
        nib = np.empty((g, p, n, 4), np.uint8)
        nib[..., 0::2] = words & 0xF
        nib[..., 1::2] = words >> 4
        vals = E2M1[nib]
    vals = vals * np.repeat(np.exp2(scales.astype(np.float64) - 127.0), 8, axis=1)[..., None]
    return vals.transpose(0, 1, 3, 2).reshape(g * 512, n)

def pack4(w):
    words, scales = pack_weight(w, "e2m1")
    return words.reshape(words.shape[0], 128, -1), scales


def unpack4(words, scales):
    return unpack_weight(words.reshape(words.shape[0], 128, -1, 2), scales, "e2m1")


B, S, D = 32, 256, 512
NB = 2
W = 2 * NB + 1
LN_EPS = 1e-5


def setup_inputs():
    s = mx_kscale(D)
    u = s / s.max()
    pos = np.arange(S)[:, None] + np.arange(W)[None, :] - NB
    e = np.exp(np.random.standard_normal((B, S, W))) * ((pos >= 0) & (pos < S))
    x = bf(np.random.standard_normal((B, S, D)) * u)
    wv = np.random.standard_normal((D, D)) / np.sqrt(D) / u[None, :]
    words, scales = pack4(wv.T)
    return {"x": x,
            "Wv_words": words,
            "Wv_scales": scales,
            "bv": bf(0.2 + 0.2 * np.random.standard_normal(D)),
            "attn_band": bf(e / e.sum(-1, keepdims=True)),
            "gamma": bf(1.0 + 0.1 * np.random.standard_normal(D)),
            "beta": bf(0.2 * np.random.standard_normal(D))}


def reference(x, Wv_words, Wv_scales, bv, attn_band, gamma, beta):
    xf, a = f64(x), f64(attn_band)
    v = (mxq(xf, 2, "e4m3") @ unpack4(Wv_words, Wv_scales)) + f64(bv)
    mix = np.zeros_like(xf)
    for j in range(W):
        o = j - NB
        lo, hi = max(0, -o), S - max(0, o)
        mix[:, lo:hi] += a[:, lo:hi, j:j + 1] * v[:, lo + o:hi + o]
    out = mix + xf
    mu = out.mean(-1, keepdims=True)
    var = out.var(-1, keepdims=True)
    return (out - mu) / np.sqrt(var + LN_EPS) * f64(gamma) + f64(beta)

@@ -1,0 +1,215 @@
+import concourse.mybir as mybir
+from concourse.masks import make_identity
+
+F32 = mybir.dt.float32
+BF16 = mybir.dt.bfloat16
+I32 = mybir.dt.int32
+U32 = mybir.dt.uint32
+U8 = mybir.dt.uint8
+FP8X4 = mybir.dt.float8_e4m3fn_x4
+FP4X4 = mybir.dt.float4_e2m1fn_x4
+ACT = mybir.ActivationFunctionType
+ALU = mybir.AluOpType
+
+P = 128
+D = 512
+ROWS = 32 * 256
+TILES = ROWS // P
+NB = 2
+TAPS = 2 * NB + 1
+GROUP = 4
+SRC_GROUPS = (TILES + 2 * NB) // GROUP
+OUT_GROUPS = TILES // GROUP
+CHUNKS = D // P
+LN_EPS = 1e-5
+
+FLOPS = 2 * ROWS * D * D
+
+
+def tile_crosssliceattention_pb_t_kernel(tc, x, Wv_words, Wv_scales, bv, attn_band, gamma, beta, out):
+    nc = tc.nc
+    x_rows = x.flatten_outer_dims().rearrange("(p t) d -> p t d", t=TILES)
+    out_rows = out.flatten_outer_dims().rearrange("(p t) d -> p t d", t=TILES)
+    band_rows = attn_band.flatten_outer_dims().rearrange("(p t) j -> p (t j)", t=TILES)
+
+    with (
+        tc.tile_pool(name="const", bufs=1) as const,
+        tc.tile_pool(name="stage", bufs=2) as stage,
+        tc.tile_pool(name="result", bufs=3) as result,
+        tc.tile_pool(name="small", bufs=3) as small,
+        tc.psum_pool(name="psum_front", bufs=2) as psum_front,
+        tc.psum_pool(name="psum_v", bufs=TAPS + 1) as psum_v,
+    ):
+        ident = const.tile([P, P], F32)
+        make_identity(nc, ident[:])
+        eps_col = const.tile([P, 1], F32)
+        nc.vector.memset(eps_col[:], LN_EPS)
+
+        w_words = const.tile([P, 2 * D], U8, align_bytes=64)
+        nc.sync.dma_start(out=w_words[:].bitcast(I32), in_=Wv_words[0].bitcast(I32))
+        w_scales = const.tile([P, D], U8, align_bytes=64)
+        nc.vector.memset(w_scales[:].bitcast(I32), 0)
+        for quadrant in range(4):
+            nc.sync.dma_start(
+                out=w_scales[32 * quadrant : 32 * quadrant + 4, :].bitcast(I32),
+                in_=Wv_scales[0, 4 * quadrant : 4 * quadrant + 4, :].bitcast(I32),
+            )
+
+        x_src = [const.tile([P, GROUP, D], BF16, name="x_src%d" % g) for g in range(SRC_GROUPS)]
+        last = SRC_GROUPS - 1
+        nc.vector.memset(x_src[0][:, 0:NB, :], 0.0)
+        nc.vector.memset(x_src[last][:, NB:GROUP, :], 0.0)
+        for lo, hi in ((1, 65), (65, P)):
+            nc.sync.dma_start(out=x_src[0][lo:hi, 0:NB, :], in_=x_rows[lo - 1 : hi - 1, TILES - NB : TILES, :])
+        nc.sync.dma_start(out=x_src[0][:, NB:GROUP, :], in_=x_rows[:, 0:NB, :])
+
+        band_bf = const.tile([P, TILES * TAPS], BF16)
+        nc.sync.dma_start(out=band_bf[:], in_=band_rows)
+        band = const.tile([P, TILES * TAPS], F32)
+        nc.vector.tensor_copy(out=band[:], in_=band_bf[:])
+
+        bv_bf = const.tile([P, CHUNKS], BF16)
+        with nc.allow_non_contiguous_dma(reason="512 bias values, one to a partition for each chunk of n"):
+            nc.sync.dma_start(out=bv_bf[:], in_=bv.rearrange("(c n) -> n c", n=P))
+        bv_col = const.tile([P, CHUNKS], F32)
+        nc.vector.tensor_copy(out=bv_col[:], in_=bv_bf[:])
+
+        for g in range(1, last):
+            nc.sync.dma_start(out=x_src[g][:], in_=x_rows[:, GROUP * g - NB : GROUP * g + NB, :])
+        nc.sync.dma_start(out=x_src[last][:, 0:NB, :], in_=x_rows[:, TILES - NB : TILES, :])
+        for lo, hi in ((0, 64), (64, P - 1)):
+            nc.sync.dma_start(out=x_src[last][lo:hi, NB:GROUP, :], in_=x_rows[lo + 1 : hi + 1, 0:NB, :])
+
+        gamma_all = const.tile([P, D], BF16)
+        nc.sync.dma_start(out=gamma_all[:], in_=gamma.partition_broadcast(P))
+        beta_all = const.tile([P, D], BF16)
+        nc.sync.dma_start(out=beta_all[:], in_=beta.partition_broadcast(P))
+
+        def transpose_and_quantise(g):
+            grouped = stage.tile([P, GROUP * P * 4], BF16, align_bytes=64)
+            grouped_words = grouped[:].bitcast(F32)
+            for half in range(2):
+                planes = psum_front.tile([P, D], F32, tag="front")
+                for i in range(2):
+                    words = x_src[g][:, 2 * half + i, :].bitcast(F32)
+                    for u in range(2):
+                        col = (2 * i + u) * P
+                        nc.tensor.transpose(planes[:, col : col + P], words[:, u : D // 2 : 2], ident[:])
+                nc.scalar.copy(
+                    out=grouped_words[:, half * D : (half + 1) * D].rearrange("q (i p u) -> q i p u", i=2, u=2),
+                    in_=planes[:].rearrange("q (i u p) -> q i p u", i=2, u=2),
+                )
+            codes = stage.tile([P, GROUP * P], U32, align_bytes=64)
+            scales = stage.tile([P, GROUP * P], U8, align_bytes=64)
+            nc.vector.quantize_mx(out=codes[:].bitcast(FP8X4), scales=scales[:], in_=grouped[:])
+            return codes, scales
+
+        def project(codes, scales):
+            v_by_feature = stage.tile([P, CHUNKS, GROUP * P], F32)
+            for c in range(CHUNKS):
+                product = psum_front.tile([P, GROUP * P], F32, tag="front")
+                nc.tensor.matmul_mx(
+                    out=product[:],
+                    lhsT=w_words[:, 2 * P * c : 2 * P * (c + 1)].bitcast(FP4X4),
+                    lhsT_scale=w_scales[:, P * c : P * (c + 1)],
+                    rhs=codes[:].bitcast(FP8X4),
+                    rhs_scale=scales[:],
+                    start=True,
+                    stop=True,
+                )
+                nc.scalar.activation(
+                    out=v_by_feature[:, c, :], in_=product[:], func=ACT.Identity, bias=bv_col[:, c : c + 1], scale=1.0
+                )
+            return v_by_feature
+
+        def restore_rows(v_by_feature, i):
+            v_rows = psum_v.tile([P, D], F32, tag="v")
+            for c in range(CHUNKS):
+                nc.tensor.transpose(v_rows[:, P * c : P * (c + 1)], v_by_feature[:, c, P * i : P * (i + 1)], ident[:])
+            return v_rows
+
+        def mix_pair(t0, v_src, mixed, row_sum):
+            for j in range(TAPS):
+                for t in (t0, t0 + 1):
+                    acc = mixed[:, t % GROUP, :]
+                    residual = x_src[(t + NB) // GROUP][:, (t + NB) % GROUP, :]
+                    nc.vector.scalar_tensor_tensor(
+                        out=acc,
+                        in0=v_src[t + j][:],
+                        scalar=band[:, TAPS * t + j : TAPS * t + j + 1],
+                        in1=residual if j == 0 else acc,
+                        op0=ALU.mult,
+                        op1=ALU.add,
+                        accum_out=row_sum[:, t % GROUP : t % GROUP + 1] if j == TAPS - 1 else None,
+                    )
+
+        def start_statistics(mixed, row_sum):
+            neg_mean = small.tile([P, GROUP], F32)
+            nc.vector.tensor_scalar_mul(out=neg_mean[:], in0=row_sum[:], scalar1=-1.0 / D)
+            normed = result.tile([P, GROUP, D], F32)
+            square_sum = small.tile([P, GROUP], F32)
+            for i in range(GROUP):
+                nc.scalar.activation(
+                    out=normed[:, i, :],
+                    in_=mixed[:, i, :],
+                    func=ACT.Square,
+                    bias=neg_mean[:, i : i + 1],
+                    scale=1.0,
+                    accum_out=square_sum[:, i : i + 1],
+                )
+            std = small.tile([P, GROUP], F32)
+            nc.scalar.activation(out=std[:], in_=square_sum[:], func=ACT.Sqrt, bias=eps_col[:, 0:1], scale=1.0 / D)
+            return neg_mean, std, normed
+
+        def finish_statistics(neg_mean, std):
+            rstd = small.tile([P, GROUP], F32)
+            nc.vector.reciprocal(out=rstd[:], in_=std[:])
+            shift = small.tile([P, GROUP], F32)
+            nc.vector.tensor_mul(out=shift[:], in0=neg_mean[:], in1=rstd[:])
+            return rstd, shift
+
+        def normalise_and_store(og, mixed, normed, rstd, shift):
+            for i in range(GROUP):
+                nc.scalar.activation(
+                    out=normed[:, i, :],
+                    in_=mixed[:, i, :],
+                    func=ACT.Identity,
+                    bias=shift[:, i : i + 1],
+                    scale=rstd[:, i : i + 1],
+                )
+            nc.gpsimd.tensor_mul(out=normed[:], in0=normed[:], in1=gamma_all[:].unsqueeze(1).to_broadcast([P, GROUP, D]))
+            nc.gpsimd.tensor_add(out=normed[:], in0=normed[:], in1=beta_all[:].unsqueeze(1).to_broadcast([P, GROUP, D]))
+            nc.sync.dma_start(out=out_rows[:, GROUP * og : GROUP * (og + 1), :], in_=normed[:])
+
+        quantised = {}
+        projected = {}
+        v_src = {}
+        quantised[0] = transpose_and_quantise(0)
+        quantised[1] = transpose_and_quantise(1)
+        projected[0] = project(*quantised[0])
+        quantised[2] = transpose_and_quantise(2)
+        projected[1] = project(*quantised[1])
+        for i in range(GROUP):
+            v_src[i] = restore_rows(projected[0], i)
+
+        waiting = None
+        for og in range(OUT_GROUPS):
+            mixed = result.tile([P, GROUP, D], F32)
+            row_sum = small.tile([P, GROUP], F32)
+            for i in (0, 1):
+                v_src[GROUP * (og + 1) + i] = restore_rows(projected[og + 1], i)
+            mix_pair(GROUP * og, v_src, mixed, row_sum)
+            if waiting is not None:
+                scalars = finish_statistics(waiting[2], waiting[3])
+            if og + 2 < SRC_GROUPS:
+                projected[og + 2] = project(*quantised[og + 2])
+            if waiting is not None:
+                normalise_and_store(waiting[0], waiting[1], waiting[4], *scalars)
+            for i in (2, 3):
+                v_src[GROUP * (og + 1) + i] = restore_rows(projected[og + 1], i)
+            mix_pair(GROUP * og + 2, v_src, mixed, row_sum)
+            if og + 3 < SRC_GROUPS:
+                quantised[og + 3] = transpose_and_quantise(og + 3)
+            waiting = (og, mixed) + start_statistics(mixed, row_sum)
+        scalars = finish_statistics(waiting[2], waiting[3])
+        normalise_and_store(waiting[0], waiting[1], waiting[4], *scalars)

@@ -39,6 +39,7 @@ def tile_crosssliceattention_pb_t_kernel(tc, x, Wv_words, Wv_scales, bv, attn_ba
         tc.tile_pool(name="small", bufs=3) as small,
         tc.psum_pool(name="psum_front", bufs=2) as psum_front,
         tc.psum_pool(name="psum_v", bufs=TAPS + 1) as psum_v,
+        tc.manual_schedule(),
     ):
         ident = const.tile([P, P], F32)
         make_identity(nc, ident[:])

@@ -86,8 +86,8 @@ def tile_crosssliceattention_pb_t_kernel(tc, x, Wv_words, Wv_scales, bv, attn_ba
         beta_all = const.tile([P, D], BF16)
         nc.sync.dma_start(out=beta_all[:], in_=beta.partition_broadcast(P))
 
-        def transpose_and_quantise(g):
-            grouped = stage.tile([P, GROUP * P * 4], BF16, align_bytes=64)
+        def transpose_rows(g):
+            grouped = stage.tile([P, GROUP * P * 4], BF16, align_bytes=64, bufs=3)
             grouped_words = grouped[:].bitcast(F32)
             for half in range(2):
                 planes = psum_front.tile([P, D], F32, tag="front")
@@ -100,6 +100,9 @@ def tile_crosssliceattention_pb_t_kernel(tc, x, Wv_words, Wv_scales, bv, attn_ba
                     out=grouped_words[:, half * D : (half + 1) * D].rearrange("q (i p u) -> q i p u", i=2, u=2),
                     in_=planes[:].rearrange("q (i u p) -> q i p u", i=2, u=2),
                 )
+            return grouped
+
+        def quantise(grouped):
             codes = stage.tile([P, GROUP * P], U32, align_bytes=64)
             scales = stage.tile([P, GROUP * P], U8, align_bytes=64)
             nc.vector.quantize_mx(out=codes[:].bitcast(FP8X4), scales=scales[:], in_=grouped[:])
@@ -182,16 +185,21 @@ def tile_crosssliceattention_pb_t_kernel(tc, x, Wv_words, Wv_scales, bv, attn_ba
             nc.gpsimd.tensor_add(out=normed[:], in0=normed[:], in1=beta_all[:].unsqueeze(1).to_broadcast([P, GROUP, D]))
             nc.sync.dma_start(out=out_rows[:, GROUP * og : GROUP * (og + 1), :], in_=normed[:])
 
+        transposed = {}
         quantised = {}
         projected = {}
         v_src = {}
-        quantised[0] = transpose_and_quantise(0)
-        quantised[1] = transpose_and_quantise(1)
+        transposed[0] = transpose_rows(0)
+        transposed[1] = transpose_rows(1)
+        quantised[0] = quantise(transposed[0])
+        quantised[1] = quantise(transposed[1])
         projected[0] = project(*quantised[0])
-        quantised[2] = transpose_and_quantise(2)
+        transposed[2] = transpose_rows(2)
+        quantised[2] = quantise(transposed[2])
         projected[1] = project(*quantised[1])
         for i in range(GROUP):
             v_src[i] = restore_rows(projected[0], i)
+        transposed[3] = transpose_rows(3)
 
         waiting = None
         for og in range(OUT_GROUPS):
@@ -209,8 +217,10 @@ def tile_crosssliceattention_pb_t_kernel(tc, x, Wv_words, Wv_scales, bv, attn_ba
             for i in (2, 3):
                 v_src[GROUP * (og + 1) + i] = restore_rows(projected[og + 1], i)
             mix_pair(GROUP * og + 2, v_src, mixed, row_sum)
+            if og + 4 < SRC_GROUPS:
+                transposed[og + 4] = transpose_rows(og + 4)
             if og + 3 < SRC_GROUPS:
-                quantised[og + 3] = transpose_and_quantise(og + 3)
+                quantised[og + 3] = quantise(transposed[og + 3])
             waiting = (og, mixed) + start_statistics(mixed, row_sum)
         scalars = finish_statistics(waiting[2], waiting[3])
         normalise_and_store(waiting[0], waiting[1], waiting[4], *scalars)

@@ -174,12 +174,13 @@ def tile_crosssliceattention_pb_t_kernel(tc, x, Wv_words, Wv_scales, bv, attn_ba
 
         def normalise_and_store(og, mixed, normed, rstd, shift):
             for i in range(GROUP):
-                nc.scalar.activation(
+                nc.vector.tensor_scalar(
                     out=normed[:, i, :],
-                    in_=mixed[:, i, :],
-                    func=ACT.Identity,
-                    bias=shift[:, i : i + 1],
-                    scale=rstd[:, i : i + 1],
+                    in0=mixed[:, i, :],
+                    scalar1=rstd[:, i : i + 1],
+                    scalar2=shift[:, i : i + 1],
+                    op0=ALU.mult,
+                    op1=ALU.add,
                 )
             nc.gpsimd.tensor_mul(out=normed[:], in0=normed[:], in1=gamma_all[:].unsqueeze(1).to_broadcast([P, GROUP, D]))
             nc.gpsimd.tensor_add(out=normed[:], in0=normed[:], in1=beta_all[:].unsqueeze(1).to_broadcast([P, GROUP, D]))

@@ -103,8 +103,8 @@ def tile_crosssliceattention_pb_t_kernel(tc, x, Wv_words, Wv_scales, bv, attn_ba
             return grouped
 
         def quantise(grouped):
-            codes = stage.tile([P, GROUP * P], U32, align_bytes=64)
-            scales = stage.tile([P, GROUP * P], U8, align_bytes=64)
+            codes = stage.tile([P, GROUP * P], U32, align_bytes=64, bufs=3)
+            scales = stage.tile([P, GROUP * P], U8, align_bytes=64, bufs=3)
             nc.vector.quantize_mx(out=codes[:].bitcast(FP8X4), scales=scales[:], in_=grouped[:])
             return codes, scales
 
@@ -147,9 +147,9 @@ def tile_crosssliceattention_pb_t_kernel(tc, x, Wv_words, Wv_scales, bv, attn_ba
                         accum_out=row_sum[:, t % GROUP : t % GROUP + 1] if j == TAPS - 1 else None,
                     )
 
-        def start_statistics(mixed, row_sum):
+        def layer_norm_and_store(og, mixed, row_sum, affine_engine):
             neg_mean = small.tile([P, GROUP], F32)
-            nc.vector.tensor_scalar_mul(out=neg_mean[:], in0=row_sum[:], scalar1=-1.0 / D)
+            nc.scalar.mul(out=neg_mean[:], in_=row_sum[:], mul=-1.0 / D)
             normed = result.tile([P, GROUP, D], F32)
             square_sum = small.tile([P, GROUP], F32)
             for i in range(GROUP):
@@ -161,67 +161,63 @@ def tile_crosssliceattention_pb_t_kernel(tc, x, Wv_words, Wv_scales, bv, attn_ba
                     scale=1.0,
                     accum_out=square_sum[:, i : i + 1],
                 )
-            std = small.tile([P, GROUP], F32)
-            nc.scalar.activation(out=std[:], in_=square_sum[:], func=ACT.Sqrt, bias=eps_col[:, 0:1], scale=1.0 / D)
-            return neg_mean, std, normed
-
-        def finish_statistics(neg_mean, std):
             rstd = small.tile([P, GROUP], F32)
-            nc.vector.reciprocal(out=rstd[:], in_=std[:])
+            nc.scalar.activation(
+                out=rstd[:], in_=square_sum[:], func=ACT.Abs_reciprocal_sqrt, bias=eps_col[:, 0:1], scale=1.0 / D
+            )
             shift = small.tile([P, GROUP], F32)
-            nc.vector.tensor_mul(out=shift[:], in0=neg_mean[:], in1=rstd[:])
-            return rstd, shift
-
-        def normalise_and_store(og, mixed, normed, rstd, shift):
             for i in range(GROUP):
-                nc.vector.tensor_scalar(
-                    out=normed[:, i, :],
-                    in0=mixed[:, i, :],
-                    scalar1=rstd[:, i : i + 1],
-                    scalar2=shift[:, i : i + 1],
-                    op0=ALU.mult,
-                    op1=ALU.add,
+                nc.scalar.activation(
+                    out=shift[:, i : i + 1], in_=neg_mean[:, i : i + 1], func=ACT.Copy, scale=rstd[:, i : i + 1]
                 )
-            nc.gpsimd.tensor_mul(out=normed[:], in0=normed[:], in1=gamma_all[:].unsqueeze(1).to_broadcast([P, GROUP, D]))
-            nc.gpsimd.tensor_add(out=normed[:], in0=normed[:], in1=beta_all[:].unsqueeze(1).to_broadcast([P, GROUP, D]))
-            nc.sync.dma_start(out=out_rows[:, GROUP * og : GROUP * (og + 1), :], in_=normed[:])
+            for i in range(GROUP):
+                nc.scalar.activation(
+                    out=normed[:, i, :],
+                    in_=mixed[:, i, :],
+                    func=ACT.Identity,
+                    bias=shift[:, i : i + 1],
+                    scale=rstd[:, i : i + 1],
+                )
+            for first in (0, 2):
+                pair = (first, first + 1)
+                for i in pair:
+                    affine_engine.tensor_mul(out=normed[:, i, :], in0=normed[:, i, :], in1=gamma_all[:])
+                for i in pair:
+                    affine_engine.tensor_add(out=normed[:, i, :], in0=normed[:, i, :], in1=beta_all[:])
+                t = GROUP * og + first
+                nc.sync.dma_start(out=out_rows[:, t : t + 2, :], in_=normed[:, first : first + 2, :])
 
         transposed = {}
         quantised = {}
         projected = {}
         v_src = {}
-        transposed[0] = transpose_rows(0)
-        transposed[1] = transpose_rows(1)
-        quantised[0] = quantise(transposed[0])
-        quantised[1] = quantise(transposed[1])
+        for g in range(3):
+            transposed[g] = transpose_rows(g)
+        for g in range(3):
+            quantised[g] = quantise(transposed[g])
         projected[0] = project(*quantised[0])
-        transposed[2] = transpose_rows(2)
-        quantised[2] = quantise(transposed[2])
-        projected[1] = project(*quantised[1])
         for i in range(GROUP):
             v_src[i] = restore_rows(projected[0], i)
+        projected[1] = project(*quantised[1])
         transposed[3] = transpose_rows(3)
 
-        waiting = None
+        pending = None
         for og in range(OUT_GROUPS):
             mixed = result.tile([P, GROUP, D], F32)
             row_sum = small.tile([P, GROUP], F32)
             for i in (0, 1):
                 v_src[GROUP * (og + 1) + i] = restore_rows(projected[og + 1], i)
             mix_pair(GROUP * og, v_src, mixed, row_sum)
-            if waiting is not None:
-                scalars = finish_statistics(waiting[2], waiting[3])
             if og + 2 < SRC_GROUPS:
                 projected[og + 2] = project(*quantised[og + 2])
-            if waiting is not None:
-                normalise_and_store(waiting[0], waiting[1], waiting[4], *scalars)
             for i in (2, 3):
                 v_src[GROUP * (og + 1) + i] = restore_rows(projected[og + 1], i)
+            if pending is not None:
+                layer_norm_and_store(*pending, nc.gpsimd)
             mix_pair(GROUP * og + 2, v_src, mixed, row_sum)
             if og + 4 < SRC_GROUPS:
                 transposed[og + 4] = transpose_rows(og + 4)
             if og + 3 < SRC_GROUPS:
                 quantised[og + 3] = quantise(transposed[og + 3])
-            waiting = (og, mixed) + start_statistics(mixed, row_sum)
-        scalars = finish_statistics(waiting[2], waiting[3])
-        normalise_and_store(waiting[0], waiting[1], waiting[4], *scalars)
+            pending = (og, mixed, row_sum)
+        layer_norm_and_store(*pending, nc.vector)

@@ -18,6 +18,7 @@ TILES = ROWS // P
 NB = 2
 TAPS = 2 * NB + 1
 GROUP = 4
+PAIR = 2
 SRC_GROUPS = (TILES + 2 * NB) // GROUP
 OUT_GROUPS = TILES // GROUP
 CHUNKS = D // P
@@ -132,60 +133,61 @@ def tile_crosssliceattention_pb_t_kernel(tc, x, Wv_words, Wv_scales, bv, attn_ba
                 nc.tensor.transpose(v_rows[:, P * c : P * (c + 1)], v_by_feature[:, c, P * i : P * (i + 1)], ident[:])
             return v_rows
 
-        def mix_pair(t0, v_src, mixed, row_sum):
+        def mix_pair(t0, v_src):
+            mixed = result.tile([P, PAIR, D], F32, bufs=4)
+            row_sum = small.tile([P, PAIR], F32)
+            partial = stage.tile([P, PAIR, 2, D], F32)
             for j in range(TAPS):
-                for t in (t0, t0 + 1):
-                    acc = mixed[:, t % GROUP, :]
+                for e in range(PAIR):
+                    t = t0 + e
                     residual = x_src[(t + NB) // GROUP][:, (t + NB) % GROUP, :]
                     nc.vector.scalar_tensor_tensor(
-                        out=acc,
+                        out=mixed[:, e, :] if j == TAPS - 1 else partial[:, e, j % 2, :],
                         in0=v_src[t + j][:],
                         scalar=band[:, TAPS * t + j : TAPS * t + j + 1],
-                        in1=residual if j == 0 else acc,
+                        in1=residual if j == 0 else partial[:, e, (j - 1) % 2, :],
                         op0=ALU.mult,
                         op1=ALU.add,
-                        accum_out=row_sum[:, t % GROUP : t % GROUP + 1] if j == TAPS - 1 else None,
+                        accum_out=row_sum[:, e : e + 1] if j == TAPS - 1 else None,
                     )
+            return t0, mixed, row_sum
 
-        def layer_norm_and_store(og, mixed, row_sum, affine_engine):
-            neg_mean = small.tile([P, GROUP], F32)
+        def layer_norm_and_store(t0, mixed, row_sum, affine_engine):
+            neg_mean = small.tile([P, PAIR], F32)
             nc.scalar.mul(out=neg_mean[:], in_=row_sum[:], mul=-1.0 / D)
-            normed = result.tile([P, GROUP, D], F32)
-            square_sum = small.tile([P, GROUP], F32)
-            for i in range(GROUP):
+            normed = result.tile([P, PAIR, D], F32, bufs=5)
+            square_sum = small.tile([P, PAIR], F32)
+            for e in range(PAIR):
                 nc.scalar.activation(
-                    out=normed[:, i, :],
-                    in_=mixed[:, i, :],
+                    out=normed[:, e, :],
+                    in_=mixed[:, e, :],
                     func=ACT.Square,
-                    bias=neg_mean[:, i : i + 1],
+                    bias=neg_mean[:, e : e + 1],
                     scale=1.0,
-                    accum_out=square_sum[:, i : i + 1],
+                    accum_out=square_sum[:, e : e + 1],
                 )
-            rstd = small.tile([P, GROUP], F32)
+            rstd = small.tile([P, PAIR], F32)
             nc.scalar.activation(
                 out=rstd[:], in_=square_sum[:], func=ACT.Abs_reciprocal_sqrt, bias=eps_col[:, 0:1], scale=1.0 / D
             )
-            shift = small.tile([P, GROUP], F32)
-            for i in range(GROUP):
+            shift = small.tile([P, PAIR], F32)
+            for e in range(PAIR):
                 nc.scalar.activation(
-                    out=shift[:, i : i + 1], in_=neg_mean[:, i : i + 1], func=ACT.Copy, scale=rstd[:, i : i + 1]
+                    out=shift[:, e : e + 1], in_=neg_mean[:, e : e + 1], func=ACT.Copy, scale=rstd[:, e : e + 1]
                 )
-            for i in range(GROUP):
+            for e in range(PAIR):
                 nc.scalar.activation(
-                    out=normed[:, i, :],
-                    in_=mixed[:, i, :],
+                    out=normed[:, e, :],
+                    in_=mixed[:, e, :],
                     func=ACT.Identity,
-                    bias=shift[:, i : i + 1],
-                    scale=rstd[:, i : i + 1],
+                    bias=shift[:, e : e + 1],
+                    scale=rstd[:, e : e + 1],
                 )
-            for first in (0, 2):
-                pair = (first, first + 1)
-                for i in pair:
-                    affine_engine.tensor_mul(out=normed[:, i, :], in0=normed[:, i, :], in1=gamma_all[:])
-                for i in pair:
-                    affine_engine.tensor_add(out=normed[:, i, :], in0=normed[:, i, :], in1=beta_all[:])
-                t = GROUP * og + first
-                nc.sync.dma_start(out=out_rows[:, t : t + 2, :], in_=normed[:, first : first + 2, :])
+            for e in range(PAIR):
+                affine_engine.tensor_mul(out=normed[:, e, :], in0=normed[:, e, :], in1=gamma_all[:])
+            for e in range(PAIR):
+                affine_engine.tensor_add(out=normed[:, e, :], in0=normed[:, e, :], in1=beta_all[:])
+            nc.sync.dma_start(out=out_rows[:, t0 : t0 + PAIR, :], in_=normed[:])
 
         transposed = {}
         quantised = {}
@@ -203,21 +205,19 @@ def tile_crosssliceattention_pb_t_kernel(tc, x, Wv_words, Wv_scales, bv, attn_ba
 
         pending = None
         for og in range(OUT_GROUPS):
-            mixed = result.tile([P, GROUP, D], F32)
-            row_sum = small.tile([P, GROUP], F32)
             for i in (0, 1):
                 v_src[GROUP * (og + 1) + i] = restore_rows(projected[og + 1], i)
-            mix_pair(GROUP * og, v_src, mixed, row_sum)
+            first_pair = mix_pair(GROUP * og, v_src)
             if og + 2 < SRC_GROUPS:
                 projected[og + 2] = project(*quantised[og + 2])
-            for i in (2, 3):
-                v_src[GROUP * (og + 1) + i] = restore_rows(projected[og + 1], i)
             if pending is not None:
                 layer_norm_and_store(*pending, nc.gpsimd)
-            mix_pair(GROUP * og + 2, v_src, mixed, row_sum)
+            for i in (2, 3):
+                v_src[GROUP * (og + 1) + i] = restore_rows(projected[og + 1], i)
+            pending = mix_pair(GROUP * og + PAIR, v_src)
+            layer_norm_and_store(*first_pair, nc.gpsimd)
             if og + 4 < SRC_GROUPS:
                 transposed[og + 4] = transpose_rows(og + 4)
             if og + 3 < SRC_GROUPS:
                 quantised[og + 3] = quantise(transposed[og + 3])
-            pending = (og, mixed, row_sum)
         layer_norm_and_store(*pending, nc.vector)

@@ -14,43 +14,71 @@ ALU = mybir.AluOpType
 P = 128
 D = 512
 ROWS = 32 * 256
-TILES = ROWS // P
 NB = 2
 TAPS = 2 * NB + 1
 GROUP = 4
 PAIR = 2
-SRC_GROUPS = (TILES + 2 * NB) // GROUP
-OUT_GROUPS = TILES // GROUP
 CHUNKS = D // P
 LN_EPS = 1e-5
+
+BAND_TILES = 25
+BAND_STEP = P - 2 * NB - 1
+BAND_ROWS = 24 * P
+COEF = BAND_ROWS // P
+PITCH = 136
+WIDTH = PITCH - 1
+SCRATCH_ROWS = 832
+SUMS_AT = 820 * D
+TAIL = 8
+AHEAD = 4
+V_BUFS = AHEAD + 1
+VECTOR_EVERY = 2
+
+TILES = (ROWS - BAND_ROWS) // P
+SRC_TILES = TILES + 2 * NB
+SRC_GROUPS = SRC_TILES // GROUP
+OUT_GROUPS = TILES // GROUP
+SLOTS = TILES // PAIR
+FIRST_BAND_SLOT = 2
+LAST_BAND_SLOT = SLOTS - 2
 
 FLOPS = 2 * ROWS * D * D
 
 
 def tile_crosssliceattention_pb_t_kernel(tc, x, Wv_words, Wv_scales, bv, attn_band, gamma, beta, out):
     nc = tc.nc
-    x_rows = x.flatten_outer_dims().rearrange("(p t) d -> p t d", t=TILES)
-    out_rows = out.flatten_outer_dims().rearrange("(p t) d -> p t d", t=TILES)
-    band_rows = attn_band.flatten_outer_dims().rearrange("(p t) j -> p (t j)", t=TILES)
+    x_all = x.flatten_outer_dims()
+    out_all = out.flatten_outer_dims()
+    band_all = attn_band.flatten_outer_dims()
+    x_rows = x_all[BAND_ROWS:ROWS, :].rearrange("(p t) d -> p t d", t=TILES)
+    x_from_halo = x_all[BAND_ROWS - NB : ROWS - NB, :].rearrange("(p t) d -> p t d", t=TILES)
+    out_rows = out_all[BAND_ROWS:ROWS, :].rearrange("(p t) d -> p t d", t=TILES)
+    band_rows = band_all[BAND_ROWS:ROWS, :].rearrange("(p t) j -> p (t j)", t=TILES)
+    scratch = out_all[BAND_ROWS - SCRATCH_ROWS : BAND_ROWS, :].rearrange("r d -> (r d)")
 
     with (
         tc.tile_pool(name="const", bufs=1) as const,
         tc.tile_pool(name="stage", bufs=2) as stage,
         tc.tile_pool(name="result", bufs=3) as result,
-        tc.tile_pool(name="small", bufs=3) as small,
-        tc.psum_pool(name="psum_front", bufs=2) as psum_front,
-        tc.psum_pool(name="psum_v", bufs=TAPS + 1) as psum_v,
+        tc.tile_pool(name="small", bufs=6) as small,
+        tc.psum_pool(name="psum_front", bufs=3) as psum_front,
+        tc.psum_pool(name="psum_v", bufs=TAPS) as psum_v,
         tc.manual_schedule(),
     ):
         ident = const.tile([P, P], F32)
         make_identity(nc, ident[:])
-        eps_col = const.tile([P, 1], F32)
-        nc.vector.memset(eps_col[:], LN_EPS)
-
         w_words = const.tile([P, 2 * D], U8, align_bytes=64)
         nc.sync.dma_start(out=w_words[:].bitcast(I32), in_=Wv_words[0].bitcast(I32))
         w_scales = const.tile([P, D], U8, align_bytes=64)
         nc.vector.memset(w_scales[:].bitcast(I32), 0)
+        eps_col = const.tile([P, 1], F32)
+        nc.vector.memset(eps_col[:], LN_EPS)
+        zero = const.tile([1, TAIL * PITCH], F32)
+        nc.vector.memset(zero[:], 0.0)
+        coef_before = const.tile([P, NB, TAPS], BF16)
+        nc.gpsimd.memset(coef_before[:], 0.0)
+        weights = const.tile([P, COEF, PITCH], F32)
+        nc.gpsimd.memset(weights[:], 0.0)
         for quadrant in range(4):
             nc.sync.dma_start(
                 out=w_scales[32 * quadrant : 32 * quadrant + 4, :].bitcast(I32),
@@ -59,58 +87,137 @@ def tile_crosssliceattention_pb_t_kernel(tc, x, Wv_words, Wv_scales, bv, attn_ba
 
         x_src = [const.tile([P, GROUP, D], BF16, name="x_src%d" % g) for g in range(SRC_GROUPS)]
         last = SRC_GROUPS - 1
-        nc.vector.memset(x_src[0][:, 0:NB, :], 0.0)
         nc.vector.memset(x_src[last][:, NB:GROUP, :], 0.0)
-        for lo, hi in ((1, 65), (65, P)):
-            nc.sync.dma_start(out=x_src[0][lo:hi, 0:NB, :], in_=x_rows[lo - 1 : hi - 1, TILES - NB : TILES, :])
-        nc.sync.dma_start(out=x_src[0][:, NB:GROUP, :], in_=x_rows[:, 0:NB, :])
+        x_band = [const.tile([P, D], BF16, name="x_band%d" % i) for i in range(BAND_TILES)]
+        nc.vector.memset(x_band[0][0:NB, :], 0.0)
 
+        def load_src(g):
+            if g < last:
+                nc.sync.dma_start(out=x_src[g][:], in_=x_from_halo[:, GROUP * g : GROUP * (g + 1), :])
+            else:
+                nc.sync.dma_start(out=x_src[last][:, 0:NB, :], in_=x_rows[:, TILES - NB : TILES, :])
+                for lo, hi in ((0, 64), (64, P - 1)):
+                    nc.sync.dma_start(out=x_src[last][lo:hi, NB:GROUP, :], in_=x_rows[lo + 1 : hi + 1, 0:NB, :])
+
+        def load_band(i):
+            if i == 0:
+                nc.sync.dma_start(out=x_band[0][NB:P, :], in_=x_all[0 : P - NB, :])
+            else:
+                nc.sync.dma_start(out=x_band[i][:], in_=x_all[BAND_STEP * i - NB : BAND_STEP * i - NB + P, :])
+
+        coef_main = const.tile([P, COEF, TAPS], BF16)
+        coef_after = const.tile([P, NB, TAPS], BF16)
+        nc.sync.dma_start(out=coef_main[:], in_=band_all[0:BAND_ROWS, :].rearrange("(p l) j -> p l j", l=COEF))
+        before = band_all[COEF - NB : COEF - NB + COEF * (P - 1), :].rearrange("(p l) j -> p l j", l=COEF)
+        for lo, hi in ((1, 65), (65, P)):
+            nc.sync.dma_start(out=coef_before[lo:hi, :, :], in_=before[lo - 1 : hi - 1, 0:NB, :])
+        nc.sync.dma_start(
+            out=coef_after[:],
+            in_=band_all[COEF : COEF + BAND_ROWS, :].rearrange("(p l) j -> p l j", l=COEF)[:, 0:NB, :],
+        )
+        bv_stage = const.tile([P, D], BF16)
+        nc.sync.dma_start(out=bv_stage[96:P, :], in_=bv.partition_broadcast(32))
+        load_src(0)
+        load_src(1)
+        v_band = [const.tile([P, D], F32, name="v_band%d" % k) for k in range(V_BUFS)]
+        for k in range(V_BUFS):
+            nc.vector.tensor_copy(out=v_band[k][96:P, :], in_=bv_stage[96:P, :])
         band_bf = const.tile([P, TILES * TAPS], BF16)
         nc.sync.dma_start(out=band_bf[:], in_=band_rows)
         band = const.tile([P, TILES * TAPS], F32)
         nc.vector.tensor_copy(out=band[:], in_=band_bf[:])
-
         bv_bf = const.tile([P, CHUNKS], BF16)
         with nc.allow_non_contiguous_dma(reason="512 bias values, one to a partition for each chunk of n"):
             nc.sync.dma_start(out=bv_bf[:], in_=bv.rearrange("(c n) -> n c", n=P))
         bv_col = const.tile([P, CHUNKS], F32)
         nc.vector.tensor_copy(out=bv_col[:], in_=bv_bf[:])
 
-        for g in range(1, last):
-            nc.sync.dma_start(out=x_src[g][:], in_=x_rows[:, GROUP * g - NB : GROUP * g + NB, :])
-        nc.sync.dma_start(out=x_src[last][:, 0:NB, :], in_=x_rows[:, TILES - NB : TILES, :])
-        for lo, hi in ((0, 64), (64, P - 1)):
-            nc.sync.dma_start(out=x_src[last][lo:hi, NB:GROUP, :], in_=x_rows[lo + 1 : hi + 1, 0:NB, :])
-
+        nc.sync.dma_start(out=scratch[0 : NB * PITCH].rearrange("(o z) -> o z", o=1), in_=zero[:, 0 : NB * PITCH])
+        nc.sync.dma_start(
+            out=scratch[(NB + BAND_ROWS) * PITCH : (NB + BAND_ROWS + TAIL) * PITCH].rearrange("(o z) -> o z", o=1),
+            in_=zero[:],
+        )
         gamma_all = const.tile([P, D], BF16)
         nc.sync.dma_start(out=gamma_all[:], in_=gamma.partition_broadcast(P))
         beta_all = const.tile([P, D], BF16)
         nc.sync.dma_start(out=beta_all[:], in_=beta.partition_broadcast(P))
+        load_src(2)
 
-        def transpose_rows(g):
-            grouped = stage.tile([P, GROUP * P * 4], BF16, align_bytes=64, bufs=3)
+        coef = const.tile([P, COEF + 2 * NB, TAPS], F32)
+        nc.gpsimd.tensor_copy(out=coef[:, 0:NB, :], in_=coef_before[:])
+        nc.gpsimd.tensor_copy(out=coef[:, NB : NB + COEF, :], in_=coef_main[:])
+        nc.gpsimd.tensor_copy(out=coef[:, NB + COEF : 2 * NB + COEF, :], in_=coef_after[:])
+        for i in range(TAPS):
+            nc.gpsimd.tensor_copy(out=weights[:, :, i], in_=coef[:, i : i + COEF, TAPS - 1 - i])
+        weight_sum = const.tile([P, COEF], F32)
+        nc.gpsimd.tensor_tensor(
+            out=weight_sum[:], in0=coef[:, NB : NB + COEF, 0], in1=coef[:, NB : NB + COEF, 1], op=ALU.add
+        )
+        for j in range(2, TAPS):
+            nc.gpsimd.tensor_tensor(out=weight_sum[:], in0=weight_sum[:], in1=coef[:, NB : NB + COEF, j], op=ALU.add)
+
+        nc.sync.dma_start(
+            out=scratch[NB * PITCH : (NB + BAND_ROWS) * PITCH].rearrange("(p l w) -> p l w", l=COEF, w=PITCH),
+            in_=weights[:],
+        )
+        nc.sync.dma_start(
+            out=scratch[SUMS_AT : SUMS_AT + BAND_ROWS].rearrange("(p l) -> p l", l=COEF), in_=weight_sum[:]
+        )
+        for i in range(4):
+            load_band(i)
+        load_src(3)
+        for i in range(4, 8):
+            load_band(i)
+        load_src(4)
+        band_t = const.tile([P, BAND_TILES, P], F32)
+        for i in range(BAND_TILES):
+            start = BAND_STEP * i * PITCH + NB
+            nc.sync.dma_start(
+                out=band_t[:, i, :],
+                in_=scratch[start : start + P * WIDTH].rearrange("(c w) -> c w", w=WIDTH)[:, 0:P],
+            )
+        whole = BAND_TILES - 1
+        nc.sync.dma_start(
+            out=band_t[P - 1 : P, 0:whole, NB : NB + BAND_STEP],
+            in_=scratch[SUMS_AT : SUMS_AT + whole * BAND_STEP].rearrange("(o i m) -> o i m", o=1, m=BAND_STEP),
+        )
+        nc.sync.dma_start(
+            out=band_t[P - 1 : P, whole, NB : NB + BAND_ROWS - whole * BAND_STEP],
+            in_=scratch[SUMS_AT + whole * BAND_STEP : SUMS_AT + BAND_ROWS].rearrange("(o m) -> o m", o=1),
+        )
+        for g in range(5, SRC_GROUPS):
+            load_src(g)
+            for i in range(3 * g - 7, min(3 * g - 4, BAND_TILES)):
+                load_band(i)
+
+        def transpose_tiles(sources, tag, bufs):
+            grouped = stage.tile([P, len(sources) * P * 4], BF16, align_bytes=64, bufs=bufs, tag=tag)
             grouped_words = grouped[:].bitcast(F32)
-            for half in range(2):
+            for first in range(0, len(sources), 2):
+                some = sources[first : first + 2]
+                n = len(some)
                 planes = psum_front.tile([P, D], F32, tag="front")
-                for i in range(2):
-                    words = x_src[g][:, 2 * half + i, :].bitcast(F32)
+                for i in range(n):
+                    words = some[i].bitcast(F32)
                     for u in range(2):
                         col = (2 * i + u) * P
                         nc.tensor.transpose(planes[:, col : col + P], words[:, u : D // 2 : 2], ident[:])
                 nc.scalar.copy(
-                    out=grouped_words[:, half * D : (half + 1) * D].rearrange("q (i p u) -> q i p u", i=2, u=2),
-                    in_=planes[:].rearrange("q (i u p) -> q i p u", i=2, u=2),
+                    out=grouped_words[:, first * 2 * P : (first + n) * 2 * P].rearrange(
+                        "q (i p u) -> q i p u", i=n, u=2
+                    ),
+                    in_=planes[:, 0 : n * 2 * P].rearrange("q (i u p) -> q i p u", i=n, u=2),
                 )
             return grouped
 
-        def quantise(grouped):
-            codes = stage.tile([P, GROUP * P], U32, align_bytes=64, bufs=3)
-            scales = stage.tile([P, GROUP * P], U8, align_bytes=64, bufs=3)
+        def quantise(grouped, n, tag, bufs):
+            codes = stage.tile([P, n * P], U32, align_bytes=64, bufs=bufs, tag="codes" + tag)
+            scales = stage.tile([P, n * P], U8, align_bytes=64, bufs=bufs, tag="scales" + tag)
             nc.vector.quantize_mx(out=codes[:].bitcast(FP8X4), scales=scales[:], in_=grouped[:])
             return codes, scales
 
         def project(codes, scales):
-            v_by_feature = stage.tile([P, CHUNKS, GROUP * P], F32)
+            v_by_feature = stage.tile([P, CHUNKS, GROUP * P], F32, tag="v_by_feature")
             for c in range(CHUNKS):
                 product = psum_front.tile([P, GROUP * P], F32, tag="front")
                 nc.tensor.matmul_mx(
@@ -127,16 +234,25 @@ def tile_crosssliceattention_pb_t_kernel(tc, x, Wv_words, Wv_scales, bv, attn_ba
                 )
             return v_by_feature
 
-        def restore_rows(v_by_feature, i):
+        projected = {}
+        v_src = {}
+
+        def restore(s):
+            if s >= SRC_TILES:
+                return
             v_rows = psum_v.tile([P, D], F32, tag="v")
             for c in range(CHUNKS):
-                nc.tensor.transpose(v_rows[:, P * c : P * (c + 1)], v_by_feature[:, c, P * i : P * (i + 1)], ident[:])
-            return v_rows
+                nc.tensor.transpose(
+                    v_rows[:, P * c : P * (c + 1)],
+                    projected[s // GROUP][:, c, P * (s % GROUP) : P * (s % GROUP + 1)],
+                    ident[:],
+                )
+            v_src[s] = v_rows
 
-        def mix_pair(t0, v_src):
-            mixed = result.tile([P, PAIR, D], F32, bufs=4)
-            row_sum = small.tile([P, PAIR], F32)
-            partial = stage.tile([P, PAIR, 2, D], F32)
+        def mix_pair(t0, after_restores, late):
+            mixed = result.tile([P, PAIR, D], F32, bufs=6, tag="mixed")
+            row_sum = small.tile([P, PAIR], F32, tag="row_sum")
+            partial = stage.tile([P, PAIR, 2, D], F32, tag="partial")
             for j in range(TAPS):
                 for e in range(PAIR):
                     t = t0 + e
@@ -150,14 +266,24 @@ def tile_crosssliceattention_pb_t_kernel(tc, x, Wv_words, Wv_scales, bv, attn_ba
                         op1=ALU.add,
                         accum_out=row_sum[:, e : e + 1] if j == TAPS - 1 else None,
                     )
-            return t0, mixed, row_sum
+                    if e == 0 and j < PAIR:
+                        restore(t0 + j + TAPS)
+                        if j == PAIR - 1:
+                            after_restores()
+                    if e == PAIR - 1 and j == TAPS - 2:
+                        late()
 
-        def layer_norm_and_store(t0, mixed, row_sum, affine_engine):
-            neg_mean = small.tile([P, PAIR], F32)
-            nc.scalar.mul(out=neg_mean[:], in_=row_sum[:], mul=-1.0 / D)
-            normed = result.tile([P, PAIR, D], F32, bufs=5)
-            square_sum = small.tile([P, PAIR], F32)
-            for e in range(PAIR):
+            def store(normed):
+                nc.sync.dma_start(out=out_rows[:, t0 : t0 + PAIR, :], in_=normed[:])
+
+            return mixed, row_sum, PAIR, store
+
+        def statistics(mixed, row_sum, n):
+            neg_mean = small.tile([P, PAIR], F32, tag="neg_mean")
+            nc.scalar.mul(out=neg_mean[:, 0:n], in_=row_sum[:, 0:n], mul=-1.0 / D)
+            normed = result.tile([P, PAIR, D], F32, bufs=5, tag="normed")
+            square_sum = small.tile([P, PAIR], F32, tag="square_sum")
+            for e in range(n):
                 nc.scalar.activation(
                     out=normed[:, e, :],
                     in_=mixed[:, e, :],
@@ -166,16 +292,20 @@ def tile_crosssliceattention_pb_t_kernel(tc, x, Wv_words, Wv_scales, bv, attn_ba
                     scale=1.0,
                     accum_out=square_sum[:, e : e + 1],
                 )
-            rstd = small.tile([P, PAIR], F32)
+            rstd = small.tile([P, PAIR], F32, tag="rstd")
             nc.scalar.activation(
-                out=rstd[:], in_=square_sum[:], func=ACT.Abs_reciprocal_sqrt, bias=eps_col[:, 0:1], scale=1.0 / D
+                out=rstd[:, 0:n], in_=square_sum[:, 0:n], func=ACT.Abs_reciprocal_sqrt, bias=eps_col[:, 0:1], scale=1.0 / D
             )
-            shift = small.tile([P, PAIR], F32)
-            for e in range(PAIR):
+            return neg_mean, rstd, normed
+
+        def finish_on_gpsimd(mixed, row_sum, n, store):
+            neg_mean, rstd, normed = statistics(mixed, row_sum, n)
+            shift = small.tile([P, PAIR], F32, tag="shift")
+            for e in range(n):
                 nc.scalar.activation(
                     out=shift[:, e : e + 1], in_=neg_mean[:, e : e + 1], func=ACT.Copy, scale=rstd[:, e : e + 1]
                 )
-            for e in range(PAIR):
+            for e in range(n):
                 nc.scalar.activation(
                     out=normed[:, e, :],
                     in_=mixed[:, e, :],
@@ -183,41 +313,195 @@ def tile_crosssliceattention_pb_t_kernel(tc, x, Wv_words, Wv_scales, bv, attn_ba
                     bias=shift[:, e : e + 1],
                     scale=rstd[:, e : e + 1],
                 )
-            for e in range(PAIR):
-                affine_engine.tensor_mul(out=normed[:, e, :], in0=normed[:, e, :], in1=gamma_all[:])
-            for e in range(PAIR):
-                affine_engine.tensor_add(out=normed[:, e, :], in0=normed[:, e, :], in1=beta_all[:])
-            nc.sync.dma_start(out=out_rows[:, t0 : t0 + PAIR, :], in_=normed[:])
+            for e in range(n):
+                nc.gpsimd.tensor_mul(out=normed[:, e, :], in0=normed[:, e, :], in1=gamma_all[:])
+            for e in range(n):
+                nc.gpsimd.tensor_add(out=normed[:, e, :], in0=normed[:, e, :], in1=beta_all[:])
+            store(normed)
+
+        def finish_on_vector(mixed, n, store, neg_mean, rstd, normed):
+            for e in range(n):
+                nc.vector.scalar_tensor_tensor(
+                    out=normed[:, e, :],
+                    in0=mixed[:, e, :],
+                    scalar=neg_mean[:, e : e + 1],
+                    in1=gamma_all[:],
+                    op0=ALU.add,
+                    op1=ALU.mult,
+                )
+            final = result.tile([P, PAIR, D], F32, bufs=5, tag="normed")
+            for e in range(n):
+                nc.vector.scalar_tensor_tensor(
+                    out=final[:, e, :],
+                    in0=normed[:, e, :],
+                    scalar=rstd[:, e : e + 1],
+                    in1=beta_all[:],
+                    op0=ALU.mult,
+                    op1=ALU.add,
+                )
+            store(final)
+
+        band_grouped = {}
+        band_codes = {}
+        band_groups = (BAND_TILES + GROUP - 1) // GROUP
+
+        def band_front(h):
+            if h < band_groups:
+                band_grouped[h] = transpose_tiles([t[:] for t in x_band[GROUP * h : GROUP * (h + 1)]], "band_grouped", 2)
+
+        def band_quantise(h):
+            if h < band_groups:
+                band_codes[h] = quantise(band_grouped[h], min(GROUP, BAND_TILES - GROUP * h), "_band", 3)
+
+        def band_project(i):
+            if i >= BAND_TILES:
+                return
+            codes, scales = band_codes[i // GROUP]
+            e = i % GROUP
+            product = psum_front.tile([P, D], F32, tag="front")
+            nc.tensor.matmul_mx(
+                out=product[:],
+                lhsT=codes[:, P * e : P * (e + 1)].bitcast(FP8X4),
+                lhsT_scale=scales[:, P * e : P * (e + 1)],
+                rhs=w_words[:].bitcast(FP4X4),
+                rhs_scale=w_scales[:],
+                start=True,
+                stop=True,
+            )
+            nc.scalar.copy(out=v_band[i % V_BUFS][0 : P - 1, :], in_=product[0 : P - 1, :])
+
+        band_sums = {}
+
+        def band_matmul(i):
+            summed = psum_front.tile([P, D], F32, tag="front")
+            nc.tensor.matmul(out=summed[:], lhsT=band_t[:, i, :], rhs=v_band[i % V_BUFS][:], start=True, stop=True)
+            band_sums[i] = summed
+
+        def band_add(i, mixed, row_sum):
+            e = i % PAIR
+            nc.vector.scalar_tensor_tensor(
+                out=mixed[:, e, :],
+                in0=band_sums[i][:],
+                scalar=1.0,
+                in1=x_band[i][:],
+                op0=ALU.mult,
+                op1=ALU.add,
+                accum_out=row_sum[:, e : e + 1],
+            )
+
+        def band_store(i0, n):
+            rows = min(BAND_STEP, BAND_ROWS - BAND_STEP * (i0 + n - 1))
+            target = out_all[BAND_STEP * i0 : BAND_STEP * (i0 + n - 1) + rows, :].rearrange("(e m) d -> m e d", e=n)
+
+            def store(normed):
+                for lo, hi in ((0, 64), (64, 112), (112, rows)):
+                    nc.sync.dma_start(out=target[lo:hi, :, :], in_=normed[NB + lo : NB + hi, 0:n, :])
+
+            return store
+
+        band_state = {"open": None, "ready": [], "vector": []}
+
+        def band_due(slot):
+            span = LAST_BAND_SLOT - FIRST_BAND_SLOT + 1
+
+            def upto(k):
+                return min(BAND_TILES, max(0, ((k - FIRST_BAND_SLOT + 1) * BAND_TILES + span - 1) // span))
+
+            return list(range(upto(slot - 1), upto(slot)))
+
+        def band_norms():
+            for mixed, row_sum, n, store, pair in band_state["ready"]:
+                if pair % VECTOR_EVERY == VECTOR_EVERY - 1:
+                    band_state["vector"].append((mixed, n, store) + statistics(mixed, row_sum, n))
+                else:
+                    finish_on_gpsimd(mixed, row_sum, n, store)
+            band_state["ready"] = []
+
+        def band_adds(due):
+            for job in band_state["vector"]:
+                finish_on_vector(*job)
+            band_state["vector"] = []
+            for i in due:
+                if i % PAIR == 0:
+                    mixed = result.tile([P, PAIR, D], F32, bufs=6, tag="mixed")
+                    row_sum = small.tile([P, PAIR], F32, tag="row_sum")
+                    band_state["open"] = (mixed, row_sum)
+                mixed, row_sum = band_state["open"]
+                band_add(i, mixed, row_sum)
+                if i % PAIR == PAIR - 1 or i == BAND_TILES - 1:
+                    n = i % PAIR + 1
+                    band_state["ready"].append((mixed, row_sum, n, band_store(i + 1 - n, n), i // PAIR))
 
         transposed = {}
         quantised = {}
-        projected = {}
-        v_src = {}
-        for g in range(3):
-            transposed[g] = transpose_rows(g)
-        for g in range(3):
-            quantised[g] = quantise(transposed[g])
+
+        def front(g):
+            if g < SRC_GROUPS:
+                transposed[g] = transpose_tiles([x_src[g][:, i, :] for i in range(GROUP)], "grouped", 3)
+
+        def quantise_src(g):
+            if g < SRC_GROUPS:
+                quantised[g] = quantise(transposed[g], GROUP, "", 2)
+
+        front(0)
+        front(1)
+        quantise_src(0)
         projected[0] = project(*quantised[0])
-        for i in range(GROUP):
-            v_src[i] = restore_rows(projected[0], i)
+        quantise_src(1)
         projected[1] = project(*quantised[1])
-        transposed[3] = transpose_rows(3)
+        for s in range(TAPS):
+            restore(s)
+        front(2)
+        band_front(0)
+        front(3)
+        band_front(1)
 
         pending = None
-        for og in range(OUT_GROUPS):
-            for i in (0, 1):
-                v_src[GROUP * (og + 1) + i] = restore_rows(projected[og + 1], i)
-            first_pair = mix_pair(GROUP * og, v_src)
-            if og + 2 < SRC_GROUPS:
-                projected[og + 2] = project(*quantised[og + 2])
+        for slot in range(SLOTS):
+            og = slot // 2
+            due = band_due(slot)
+
+            def quantising():
+                if slot % 2 == 0:
+                    quantise_src(og + 2)
+                if slot == 0:
+                    band_quantise(0)
+                if slot == 1:
+                    band_quantise(1)
+                for i in due:
+                    if i % GROUP == 0:
+                        band_quantise(i // GROUP + 2)
+
+            def band_matmuls():
+                for i in due:
+                    band_matmul(i)
+
+            summed_pair = mix_pair(PAIR * slot, band_matmuls, quantising)
+            band_adds(due)
+            band_norms_ready = band_state["ready"]
+            band_state["ready"] = band_state.get("late", [])
+            band_norms()
+            band_state["late"] = band_norms_ready
             if pending is not None:
-                layer_norm_and_store(*pending, nc.gpsimd)
-            for i in (2, 3):
-                v_src[GROUP * (og + 1) + i] = restore_rows(projected[og + 1], i)
-            pending = mix_pair(GROUP * og + PAIR, v_src)
-            layer_norm_and_store(*first_pair, nc.gpsimd)
-            if og + 4 < SRC_GROUPS:
-                transposed[og + 4] = transpose_rows(og + 4)
-            if og + 3 < SRC_GROUPS:
-                quantised[og + 3] = quantise(transposed[og + 3])
-        layer_norm_and_store(*pending, nc.vector)
+                finish_on_gpsimd(*pending)
+            pending = summed_pair
+            if slot % 2 == 0:
+                if og + 2 < SRC_GROUPS:
+                    projected[og + 2] = project(*quantised[og + 2])
+            else:
+                front(og + 4)
+            if slot == 0:
+                band_front(2)
+            if slot == 1:
+                for i in range(AHEAD):
+                    band_project(i)
+            for i in due:
+                band_project(i + AHEAD)
+                if i % GROUP == 1:
+                    band_front(i // GROUP + 3)
+        band_state["ready"] = band_state["late"]
+        band_norms()
+        for job in band_state["vector"]:
+            finish_on_vector(*job)
+        mixed, row_sum, n, store = pending
+        finish_on_vector(mixed, n, store, *statistics(mixed, row_sum, n))

@@ -39,7 +39,7 @@ SRC_TILES = TILES + 2 * NB
 SRC_GROUPS = SRC_TILES // GROUP
 OUT_GROUPS = TILES // GROUP
 SLOTS = TILES // PAIR
-FIRST_BAND_SLOT = 2
+FIRST_BAND_SLOT = 3
 LAST_BAND_SLOT = SLOTS - 2
 
 FLOPS = 2 * ROWS * D * D
@@ -68,7 +68,6 @@ def tile_crosssliceattention_pb_t_kernel(tc, x, Wv_words, Wv_scales, bv, attn_ba
         ident = const.tile([P, P], F32)
         make_identity(nc, ident[:])
         w_words = const.tile([P, 2 * D], U8, align_bytes=64)
-        nc.sync.dma_start(out=w_words[:].bitcast(I32), in_=Wv_words[0].bitcast(I32))
         w_scales = const.tile([P, D], U8, align_bytes=64)
         nc.vector.memset(w_scales[:].bitcast(I32), 0)
         eps_col = const.tile([P, 1], F32)
@@ -79,11 +78,6 @@ def tile_crosssliceattention_pb_t_kernel(tc, x, Wv_words, Wv_scales, bv, attn_ba
         nc.gpsimd.memset(coef_before[:], 0.0)
         weights = const.tile([P, COEF, PITCH], F32)
         nc.gpsimd.memset(weights[:], 0.0)
-        for quadrant in range(4):
-            nc.sync.dma_start(
-                out=w_scales[32 * quadrant : 32 * quadrant + 4, :].bitcast(I32),
-                in_=Wv_scales[0, 4 * quadrant : 4 * quadrant + 4, :].bitcast(I32),
-            )
 
         x_src = [const.tile([P, GROUP, D], BF16, name="x_src%d" % g) for g in range(SRC_GROUPS)]
         last = SRC_GROUPS - 1
@@ -105,6 +99,24 @@ def tile_crosssliceattention_pb_t_kernel(tc, x, Wv_words, Wv_scales, bv, attn_ba
             else:
                 nc.sync.dma_start(out=x_band[i][:], in_=x_all[BAND_STEP * i - NB : BAND_STEP * i - NB + P, :])
 
+        nc.sync.dma_start(out=x_src[0][:, 0:PAIR, :], in_=x_from_halo[:, 0:PAIR, :])
+        nc.sync.dma_start(out=x_src[0][:, PAIR:GROUP, :], in_=x_from_halo[:, PAIR:GROUP, :])
+        nc.sync.dma_start(out=w_words[:].bitcast(I32), in_=Wv_words[0].bitcast(I32))
+        for quadrant in range(4):
+            nc.sync.dma_start(
+                out=w_scales[32 * quadrant : 32 * quadrant + 4, :].bitcast(I32),
+                in_=Wv_scales[0, 4 * quadrant : 4 * quadrant + 4, :].bitcast(I32),
+            )
+        bv_bf = const.tile([P, CHUNKS], BF16)
+        with nc.allow_non_contiguous_dma(reason="512 bias values, one to a partition for each chunk of n"):
+            nc.sync.dma_start(out=bv_bf[:], in_=bv.rearrange("(c n) -> n c", n=P))
+        bv_col = const.tile([P, CHUNKS], F32)
+        nc.vector.tensor_copy(out=bv_col[:], in_=bv_bf[:])
+        load_src(1)
+        band_bf = const.tile([P, TILES * TAPS], BF16)
+        nc.sync.dma_start(out=band_bf[:], in_=band_rows)
+        band = const.tile([P, TILES * TAPS], F32)
+
         coef_main = const.tile([P, COEF, TAPS], BF16)
         coef_after = const.tile([P, NB, TAPS], BF16)
         nc.sync.dma_start(out=coef_main[:], in_=band_all[0:BAND_ROWS, :].rearrange("(p l) j -> p l j", l=COEF))
@@ -115,33 +127,19 @@ def tile_crosssliceattention_pb_t_kernel(tc, x, Wv_words, Wv_scales, bv, attn_ba
             out=coef_after[:],
             in_=band_all[COEF : COEF + BAND_ROWS, :].rearrange("(p l) j -> p l j", l=COEF)[:, 0:NB, :],
         )
-        bv_stage = const.tile([P, D], BF16)
-        nc.sync.dma_start(out=bv_stage[96:P, :], in_=bv.partition_broadcast(32))
-        load_src(0)
-        load_src(1)
-        v_band = [const.tile([P, D], F32, name="v_band%d" % k) for k in range(V_BUFS)]
-        for k in range(V_BUFS):
-            nc.vector.tensor_copy(out=v_band[k][96:P, :], in_=bv_stage[96:P, :])
-        band_bf = const.tile([P, TILES * TAPS], BF16)
-        nc.sync.dma_start(out=band_bf[:], in_=band_rows)
-        band = const.tile([P, TILES * TAPS], F32)
-        nc.vector.tensor_copy(out=band[:], in_=band_bf[:])
-        bv_bf = const.tile([P, CHUNKS], BF16)
-        with nc.allow_non_contiguous_dma(reason="512 bias values, one to a partition for each chunk of n"):
-            nc.sync.dma_start(out=bv_bf[:], in_=bv.rearrange("(c n) -> n c", n=P))
-        bv_col = const.tile([P, CHUNKS], F32)
-        nc.vector.tensor_copy(out=bv_col[:], in_=bv_bf[:])
-
         nc.sync.dma_start(out=scratch[0 : NB * PITCH].rearrange("(o z) -> o z", o=1), in_=zero[:, 0 : NB * PITCH])
         nc.sync.dma_start(
             out=scratch[(NB + BAND_ROWS) * PITCH : (NB + BAND_ROWS + TAIL) * PITCH].rearrange("(o z) -> o z", o=1),
             in_=zero[:],
         )
+        load_src(2)
         gamma_all = const.tile([P, D], BF16)
         nc.sync.dma_start(out=gamma_all[:], in_=gamma.partition_broadcast(P))
         beta_all = const.tile([P, D], BF16)
         nc.sync.dma_start(out=beta_all[:], in_=beta.partition_broadcast(P))
-        load_src(2)
+        for i in range(4):
+            load_band(i)
+        load_src(3)
 
         coef = const.tile([P, COEF + 2 * NB, TAPS], F32)
         nc.gpsimd.tensor_copy(out=coef[:, 0:NB, :], in_=coef_before[:])
@@ -163,12 +161,12 @@ def tile_crosssliceattention_pb_t_kernel(tc, x, Wv_words, Wv_scales, bv, attn_ba
         nc.sync.dma_start(
             out=scratch[SUMS_AT : SUMS_AT + BAND_ROWS].rearrange("(p l) -> p l", l=COEF), in_=weight_sum[:]
         )
-        for i in range(4):
-            load_band(i)
-        load_src(3)
+        bv_stage = const.tile([P, D], BF16)
+        nc.sync.dma_start(out=bv_stage[96:P, :], in_=bv.partition_broadcast(32))
+        v_band = [const.tile([P, D], F32, name="v_band%d" % k) for k in range(V_BUFS)]
+        load_src(4)
         for i in range(4, 8):
             load_band(i)
-        load_src(4)
         band_t = const.tile([P, BAND_TILES, P], F32)
         for i in range(BAND_TILES):
             start = BAND_STEP * i * PITCH + NB
@@ -190,7 +188,7 @@ def tile_crosssliceattention_pb_t_kernel(tc, x, Wv_words, Wv_scales, bv, attn_ba
             for i in range(3 * g - 7, min(3 * g - 4, BAND_TILES)):
                 load_band(i)
 
-        def transpose_tiles(sources, tag, bufs):
+        def transpose_tiles(sources, tag, bufs, vector_helps=False):
             grouped = stage.tile([P, len(sources) * P * 4], BF16, align_bytes=64, bufs=bufs, tag=tag)
             grouped_words = grouped[:].bitcast(F32)
             for first in range(0, len(sources), 2):
@@ -202,7 +200,8 @@ def tile_crosssliceattention_pb_t_kernel(tc, x, Wv_words, Wv_scales, bv, attn_ba
                     for u in range(2):
                         col = (2 * i + u) * P
                         nc.tensor.transpose(planes[:, col : col + P], words[:, u : D // 2 : 2], ident[:])
-                nc.scalar.copy(
+                copy = nc.vector.tensor_copy if vector_helps and first > 0 else nc.scalar.copy
+                copy(
                     out=grouped_words[:, first * 2 * P : (first + n) * 2 * P].rearrange(
                         "q (i p u) -> q i p u", i=n, u=2
                     ),
@@ -216,7 +215,7 @@ def tile_crosssliceattention_pb_t_kernel(tc, x, Wv_words, Wv_scales, bv, attn_ba
             nc.vector.quantize_mx(out=codes[:].bitcast(FP8X4), scales=scales[:], in_=grouped[:])
             return codes, scales
 
-        def project(codes, scales):
+        def project(codes, scales, vector_helps=False):
             v_by_feature = stage.tile([P, CHUNKS, GROUP * P], F32, tag="v_by_feature")
             for c in range(CHUNKS):
                 product = psum_front.tile([P, GROUP * P], F32, tag="front")
@@ -229,9 +228,18 @@ def tile_crosssliceattention_pb_t_kernel(tc, x, Wv_words, Wv_scales, bv, attn_ba
                     start=True,
                     stop=True,
                 )
-                nc.scalar.activation(
-                    out=v_by_feature[:, c, :], in_=product[:], func=ACT.Identity, bias=bv_col[:, c : c + 1], scale=1.0
-                )
+                if vector_helps and c % 2 == 1:
+                    nc.vector.tensor_scalar(
+                        out=v_by_feature[:, c, :], in0=product[:], scalar1=bv_col[:, c : c + 1], scalar2=None, op0=ALU.add
+                    )
+                else:
+                    nc.scalar.activation(
+                        out=v_by_feature[:, c, :],
+                        in_=product[:],
+                        func=ACT.Identity,
+                        bias=bv_col[:, c : c + 1],
+                        scale=1.0,
+                    )
             return v_by_feature
 
         projected = {}
@@ -409,13 +417,12 @@ def tile_crosssliceattention_pb_t_kernel(tc, x, Wv_words, Wv_scales, bv, attn_ba
 
             return list(range(upto(slot - 1), upto(slot)))
 
-        def band_norms():
-            for mixed, row_sum, n, store, pair in band_state["ready"]:
+        def band_norms(pairs):
+            for mixed, row_sum, n, store, pair in pairs:
                 if pair % VECTOR_EVERY == VECTOR_EVERY - 1:
                     band_state["vector"].append((mixed, n, store) + statistics(mixed, row_sum, n))
                 else:
                     finish_on_gpsimd(mixed, row_sum, n, store)
-            band_state["ready"] = []
 
         def band_adds(due):
             for job in band_state["vector"]:
@@ -435,53 +442,56 @@ def tile_crosssliceattention_pb_t_kernel(tc, x, Wv_words, Wv_scales, bv, attn_ba
         transposed = {}
         quantised = {}
 
-        def front(g):
+        def front(g, vector_helps=False):
             if g < SRC_GROUPS:
-                transposed[g] = transpose_tiles([x_src[g][:, i, :] for i in range(GROUP)], "grouped", 3)
+                transposed[g] = transpose_tiles([x_src[g][:, i, :] for i in range(GROUP)], "grouped", 3, vector_helps)
 
         def quantise_src(g):
             if g < SRC_GROUPS:
                 quantised[g] = quantise(transposed[g], GROUP, "", 2)
 
-        front(0)
-        front(1)
+        front(0, True)
         quantise_src(0)
-        projected[0] = project(*quantised[0])
+        front(1, True)
+        projected[0] = project(*quantised[0], True)
         quantise_src(1)
+        nc.vector.tensor_copy(out=band[:], in_=band_bf[:])
+        restore(0)
+        restore(1)
         projected[1] = project(*quantised[1])
-        for s in range(TAPS):
-            restore(s)
+        restore(2)
+        restore(3)
         front(2)
-        band_front(0)
-        front(3)
-        band_front(1)
+        restore(GROUP)
+        if FIRST_BAND_SLOT == 2:
+            band_front(0)
 
         pending = None
         for slot in range(SLOTS):
             og = slot // 2
             due = band_due(slot)
 
+            def tensor_work():
+                for i in due:
+                    band_matmul(i)
+
             def quantising():
                 if slot % 2 == 0:
                     quantise_src(og + 2)
                 if slot == 0:
-                    band_quantise(0)
-                if slot == 1:
-                    band_quantise(1)
+                    for k in range(V_BUFS):
+                        nc.vector.tensor_copy(out=v_band[k][96:P, :], in_=bv_stage[96:P, :])
+                if FIRST_BAND_SLOT - 2 <= slot < FIRST_BAND_SLOT:
+                    band_quantise(slot - FIRST_BAND_SLOT + 2)
                 for i in due:
                     if i % GROUP == 0:
                         band_quantise(i // GROUP + 2)
 
-            def band_matmuls():
-                for i in due:
-                    band_matmul(i)
-
-            summed_pair = mix_pair(PAIR * slot, band_matmuls, quantising)
+            summed_pair = mix_pair(PAIR * slot, tensor_work, quantising)
+            summed_before = band_state["ready"]
+            band_state["ready"] = []
             band_adds(due)
-            band_norms_ready = band_state["ready"]
-            band_state["ready"] = band_state.get("late", [])
-            band_norms()
-            band_state["late"] = band_norms_ready
+            band_norms(summed_before)
             if pending is not None:
                 finish_on_gpsimd(*pending)
             pending = summed_pair
@@ -491,16 +501,17 @@ def tile_crosssliceattention_pb_t_kernel(tc, x, Wv_words, Wv_scales, bv, attn_ba
             else:
                 front(og + 4)
             if slot == 0:
-                band_front(2)
-            if slot == 1:
-                for i in range(AHEAD):
-                    band_project(i)
+                front(3)
+            if FIRST_BAND_SLOT - 3 <= slot < FIRST_BAND_SLOT:
+                band_front(slot - FIRST_BAND_SLOT + 3)
+            if FIRST_BAND_SLOT - 2 <= slot < FIRST_BAND_SLOT:
+                band_project(2 * (slot - FIRST_BAND_SLOT + 2))
+                band_project(2 * (slot - FIRST_BAND_SLOT + 2) + 1)
             for i in due:
                 band_project(i + AHEAD)
                 if i % GROUP == 1:
                     band_front(i // GROUP + 3)
-        band_state["ready"] = band_state["late"]
-        band_norms()
+        band_norms(band_state["ready"])
         for job in band_state["vector"]:
             finish_on_vector(*job)
         mixed, row_sum, n, store = pending

@@ -133,10 +133,10 @@ def tile_crosssliceattention_pb_t_kernel(tc, x, Wv_words, Wv_scales, bv, attn_ba
             in_=zero[:],
         )
         load_src(2)
-        gamma_all = const.tile([P, D], BF16)
-        nc.sync.dma_start(out=gamma_all[:], in_=gamma.partition_broadcast(P))
-        beta_all = const.tile([P, D], BF16)
-        nc.sync.dma_start(out=beta_all[:], in_=beta.partition_broadcast(P))
+        gamma_bf = const.tile([P, D], BF16)
+        nc.sync.dma_start(out=gamma_bf[:], in_=gamma.partition_broadcast(P))
+        beta_bf = const.tile([P, D], BF16)
+        nc.sync.dma_start(out=beta_bf[:], in_=beta.partition_broadcast(P))
         for i in range(4):
             load_band(i)
         load_src(3)
@@ -153,6 +153,11 @@ def tile_crosssliceattention_pb_t_kernel(tc, x, Wv_words, Wv_scales, bv, attn_ba
         )
         for j in range(2, TAPS):
             nc.gpsimd.tensor_tensor(out=weight_sum[:], in0=weight_sum[:], in1=coef[:, NB : NB + COEF, j], op=ALU.add)
+
+        gamma_all = const.tile([P, D], F32)
+        nc.gpsimd.tensor_copy(out=gamma_all[:], in_=gamma_bf[:])
+        beta_all = const.tile([P, D], F32)
+        nc.gpsimd.tensor_copy(out=beta_all[:], in_=beta_bf[:])
 
         nc.sync.dma_start(
             out=scratch[NB * PITCH : (NB + BAND_ROWS) * PITCH].rearrange("(p l w) -> p l w", l=COEF, w=PITCH),

@@ -154,10 +154,11 @@ def tile_crosssliceattention_pb_t_kernel(tc, x, Wv_words, Wv_scales, bv, attn_ba
         for j in range(2, TAPS):
             nc.gpsimd.tensor_tensor(out=weight_sum[:], in0=weight_sum[:], in1=coef[:, NB : NB + COEF, j], op=ALU.add)
 
-        gamma_all = const.tile([P, D], F32)
-        nc.gpsimd.tensor_copy(out=gamma_all[:], in_=gamma_bf[:])
-        beta_all = const.tile([P, D], F32)
-        nc.gpsimd.tensor_copy(out=beta_all[:], in_=beta_bf[:])
+        gamma_pair = const.tile([P, PAIR, D], F32)
+        beta_pair = const.tile([P, PAIR, D], F32)
+        for e in range(PAIR):
+            nc.gpsimd.tensor_copy(out=gamma_pair[:, e, :], in_=gamma_bf[:])
+            nc.gpsimd.tensor_copy(out=beta_pair[:, e, :], in_=beta_bf[:])
 
         nc.sync.dma_start(
             out=scratch[NB * PITCH : (NB + BAND_ROWS) * PITCH].rearrange("(p l w) -> p l w", l=COEF, w=PITCH),
@@ -265,7 +266,7 @@ def tile_crosssliceattention_pb_t_kernel(tc, x, Wv_words, Wv_scales, bv, attn_ba
         def mix_pair(t0, after_restores, late):
             mixed = result.tile([P, PAIR, D], F32, bufs=6, tag="mixed")
             row_sum = small.tile([P, PAIR], F32, tag="row_sum")
-            partial = stage.tile([P, PAIR, 2, D], F32, tag="partial")
+            partial = stage.tile([P, PAIR, 2, D], F32, tag="partial", bufs=1)
             for j in range(TAPS):
                 for e in range(PAIR):
                     t = t0 + e
@@ -326,10 +327,8 @@ def tile_crosssliceattention_pb_t_kernel(tc, x, Wv_words, Wv_scales, bv, attn_ba
                     bias=shift[:, e : e + 1],
                     scale=rstd[:, e : e + 1],
                 )
-            for e in range(n):
-                nc.gpsimd.tensor_mul(out=normed[:, e, :], in0=normed[:, e, :], in1=gamma_all[:])
-            for e in range(n):
-                nc.gpsimd.tensor_add(out=normed[:, e, :], in0=normed[:, e, :], in1=beta_all[:])
+            nc.gpsimd.tensor_mul(out=normed[:, 0:n, :], in0=normed[:, 0:n, :], in1=gamma_pair[:, 0:n, :])
+            nc.gpsimd.tensor_add(out=normed[:, 0:n, :], in0=normed[:, 0:n, :], in1=beta_pair[:, 0:n, :])
             store(normed)
 
         def finish_on_vector(mixed, n, store, neg_mean, rstd, normed):
@@ -338,7 +337,7 @@ def tile_crosssliceattention_pb_t_kernel(tc, x, Wv_words, Wv_scales, bv, attn_ba
                     out=normed[:, e, :],
                     in0=mixed[:, e, :],
                     scalar=neg_mean[:, e : e + 1],
-                    in1=gamma_all[:],
+                    in1=gamma_pair[:, 0, :],
                     op0=ALU.add,
                     op1=ALU.mult,
                 )
@@ -348,7 +347,7 @@ def tile_crosssliceattention_pb_t_kernel(tc, x, Wv_words, Wv_scales, bv, attn_ba
                     out=final[:, e, :],
                     in0=normed[:, e, :],
                     scalar=rstd[:, e : e + 1],
-                    in1=beta_all[:],
+                    in1=beta_pair[:, 0, :],
                     op0=ALU.mult,
                     op1=ALU.add,
                 )

@@ -22,6 +22,7 @@ CHUNKS = D // P
 LN_EPS = 1e-5
 
 BAND_TILES = 25
+BAND_GROUPS = (BAND_TILES + GROUP - 1) // GROUP
 BAND_STEP = P - 2 * NB - 1
 BAND_ROWS = 24 * P
 COEF = BAND_ROWS // P
@@ -30,17 +31,20 @@ WIDTH = PITCH - 1
 SCRATCH_ROWS = 832
 SUMS_AT = 820 * D
 TAIL = 8
-AHEAD = 4
-V_BUFS = AHEAD + 1
-VECTOR_EVERY = 2
+AHEAD = 2
+V_BUFS = 2 * AHEAD
 
 TILES = (ROWS - BAND_ROWS) // P
 SRC_TILES = TILES + 2 * NB
 SRC_GROUPS = SRC_TILES // GROUP
-OUT_GROUPS = TILES // GROUP
-SLOTS = TILES // PAIR
-FIRST_BAND_SLOT = 3
-LAST_BAND_SLOT = SLOTS - 2
+V_BANKS = 3
+SLOTS = SRC_TILES // PAIR
+FIRST_BAND_SLOT = 4
+LAST_BAND_SLOT = 19
+FIRST_JOINT = 3
+VECTOR_EVERY = 4
+LAST_ON_VECTOR = 3
+LONE_SLOT = 2 * (BAND_GROUPS - 1 + FIRST_JOINT) - 3
 
 FLOPS = 2 * ROWS * D * D
 
@@ -61,12 +65,15 @@ def tile_crosssliceattention_pb_t_kernel(tc, x, Wv_words, Wv_scales, bv, attn_ba
         tc.tile_pool(name="stage", bufs=2) as stage,
         tc.tile_pool(name="result", bufs=3) as result,
         tc.tile_pool(name="small", bufs=6) as small,
-        tc.psum_pool(name="psum_front", bufs=3) as psum_front,
-        tc.psum_pool(name="psum_v", bufs=TAPS) as psum_v,
+        tc.psum_pool(name="psum_front", bufs=4) as psum_front,
+        tc.psum_pool(name="psum_v", bufs=V_BANKS) as psum_v,
+        tc.psum_pool(name="psum_const", bufs=1) as psum_const,
         tc.manual_schedule(),
     ):
         ident = const.tile([P, P], F32)
         make_identity(nc, ident[:])
+        ident_bf = const.tile([P, P], BF16)
+        make_identity(nc, ident_bf[:])
         w_words = const.tile([P, 2 * D], U8, align_bytes=64)
         w_scales = const.tile([P, D], U8, align_bytes=64)
         nc.vector.memset(w_scales[:].bitcast(I32), 0)
@@ -133,13 +140,13 @@ def tile_crosssliceattention_pb_t_kernel(tc, x, Wv_words, Wv_scales, bv, attn_ba
             in_=zero[:],
         )
         load_src(2)
-        gamma_bf = const.tile([P, D], BF16)
-        nc.sync.dma_start(out=gamma_bf[:], in_=gamma.partition_broadcast(P))
-        beta_bf = const.tile([P, D], BF16)
-        nc.sync.dma_start(out=beta_bf[:], in_=beta.partition_broadcast(P))
+        gamma_pair = const.tile([P, PAIR, D], BF16)
+        nc.sync.dma_start(out=gamma_pair[:, 0, :], in_=gamma.partition_broadcast(P))
+        beta_pair = const.tile([P, PAIR, D], BF16)
+        nc.sync.dma_start(out=beta_pair[:, 0, :], in_=beta.partition_broadcast(P))
+        load_src(3)
         for i in range(4):
             load_band(i)
-        load_src(3)
 
         coef = const.tile([P, COEF + 2 * NB, TAPS], F32)
         nc.gpsimd.tensor_copy(out=coef[:, 0:NB, :], in_=coef_before[:])
@@ -153,12 +160,8 @@ def tile_crosssliceattention_pb_t_kernel(tc, x, Wv_words, Wv_scales, bv, attn_ba
         )
         for j in range(2, TAPS):
             nc.gpsimd.tensor_tensor(out=weight_sum[:], in0=weight_sum[:], in1=coef[:, NB : NB + COEF, j], op=ALU.add)
-
-        gamma_pair = const.tile([P, PAIR, D], F32)
-        beta_pair = const.tile([P, PAIR, D], F32)
-        for e in range(PAIR):
-            nc.gpsimd.tensor_copy(out=gamma_pair[:, e, :], in_=gamma_bf[:])
-            nc.gpsimd.tensor_copy(out=beta_pair[:, e, :], in_=beta_bf[:])
+        nc.gpsimd.tensor_copy(out=gamma_pair[:, 1, :], in_=gamma_pair[:, 0, :])
+        nc.gpsimd.tensor_copy(out=beta_pair[:, 1, :], in_=beta_pair[:, 0, :])
 
         nc.sync.dma_start(
             out=scratch[NB * PITCH : (NB + BAND_ROWS) * PITCH].rearrange("(p l w) -> p l w", l=COEF, w=PITCH),
@@ -170,6 +173,8 @@ def tile_crosssliceattention_pb_t_kernel(tc, x, Wv_words, Wv_scales, bv, attn_ba
         bv_stage = const.tile([P, D], BF16)
         nc.sync.dma_start(out=bv_stage[96:P, :], in_=bv.partition_broadcast(32))
         v_band = [const.tile([P, D], F32, name="v_band%d" % k) for k in range(V_BUFS)]
+        for k in range(V_BUFS):
+            nc.gpsimd.tensor_copy(out=v_band[k][96:P, :], in_=bv_stage[96:P, :])
         load_src(4)
         for i in range(4, 8):
             load_band(i)
@@ -194,9 +199,7 @@ def tile_crosssliceattention_pb_t_kernel(tc, x, Wv_words, Wv_scales, bv, attn_ba
             for i in range(3 * g - 7, min(3 * g - 4, BAND_TILES)):
                 load_band(i)
 
-        def transpose_tiles(sources, tag, bufs, vector_helps=False):
-            grouped = stage.tile([P, len(sources) * P * 4], BF16, align_bytes=64, bufs=bufs, tag=tag)
-            grouped_words = grouped[:].bitcast(F32)
+        def transpose_tiles(sources, grouped_words, vector_helps=False):
             for first in range(0, len(sources), 2):
                 some = sources[first : first + 2]
                 n = len(some)
@@ -213,15 +216,42 @@ def tile_crosssliceattention_pb_t_kernel(tc, x, Wv_words, Wv_scales, bv, attn_ba
                     ),
                     in_=planes[:, 0 : n * 2 * P].rearrange("q (i u p) -> q i p u", i=n, u=2),
                 )
-            return grouped
 
-        def quantise(grouped, n, tag, bufs):
-            codes = stage.tile([P, n * P], U32, align_bytes=64, bufs=bufs, tag="codes" + tag)
-            scales = stage.tile([P, n * P], U8, align_bytes=64, bufs=bufs, tag="scales" + tag)
-            nc.vector.quantize_mx(out=codes[:].bitcast(FP8X4), scales=scales[:], in_=grouped[:])
-            return codes, scales
+        grouped = {}
+        quantised = {}
 
-        def project(codes, scales, vector_helps=False):
+        def joint_band_group(g):
+            h = g - FIRST_JOINT
+            return h if 0 <= h < BAND_GROUPS else None
+
+        def band_tiles_of(h):
+            return range(GROUP * h, min(GROUP * (h + 1), BAND_TILES))
+
+        def front(g, vector_helps=False):
+            if g >= SRC_GROUPS:
+                return
+            h = joint_band_group(g)
+            tiles = GROUP if h is None or len(band_tiles_of(h)) < GROUP else 2 * GROUP
+            columns = stage.tile([P, tiles * P * 4], BF16, align_bytes=64, bufs=2, tag="grouped")
+            grouped[g] = columns
+            words = columns[:].bitcast(F32)
+            transpose_tiles([x_src[g][:, i, :] for i in range(GROUP)], words[:, 0 : GROUP * 2 * P], vector_helps)
+            if tiles == 2 * GROUP:
+                transpose_tiles([x_band[i][:] for i in band_tiles_of(h)], words[:, GROUP * 2 * P : tiles * 2 * P])
+
+        def quantise(g):
+            if g >= SRC_GROUPS:
+                return
+            columns = grouped[g][:].shape[1] // 4
+            codes = stage.tile([P, columns], U32, align_bytes=64, bufs=3, tag="codes")
+            scales = stage.tile([P, columns], U8, align_bytes=64, bufs=3, tag="scales")
+            nc.vector.quantize_mx(out=codes[:].bitcast(FP8X4), scales=scales[:], in_=grouped[g][:])
+            quantised[g] = (codes, scales)
+
+        def project(g, vector_helps=False):
+            if g >= SRC_GROUPS:
+                return
+            codes, scales = quantised[g]
             v_by_feature = stage.tile([P, CHUNKS, GROUP * P], F32, tag="v_by_feature")
             for c in range(CHUNKS):
                 product = psum_front.tile([P, GROUP * P], F32, tag="front")
@@ -229,8 +259,8 @@ def tile_crosssliceattention_pb_t_kernel(tc, x, Wv_words, Wv_scales, bv, attn_ba
                     out=product[:],
                     lhsT=w_words[:, 2 * P * c : 2 * P * (c + 1)].bitcast(FP4X4),
                     lhsT_scale=w_scales[:, P * c : P * (c + 1)],
-                    rhs=codes[:].bitcast(FP8X4),
-                    rhs_scale=scales[:],
+                    rhs=codes[:, 0 : GROUP * P].bitcast(FP8X4),
+                    rhs_scale=scales[:, 0 : GROUP * P],
                     start=True,
                     stop=True,
                 )
@@ -246,7 +276,7 @@ def tile_crosssliceattention_pb_t_kernel(tc, x, Wv_words, Wv_scales, bv, attn_ba
                         bias=bv_col[:, c : c + 1],
                         scale=1.0,
                     )
-            return v_by_feature
+            projected[g] = v_by_feature
 
         projected = {}
         v_src = {}
@@ -263,34 +293,38 @@ def tile_crosssliceattention_pb_t_kernel(tc, x, Wv_words, Wv_scales, bv, attn_ba
                 )
             v_src[s] = v_rows
 
-        def mix_pair(t0, after_restores, late):
-            mixed = result.tile([P, PAIR, D], F32, bufs=6, tag="mixed")
-            row_sum = small.tile([P, PAIR], F32, tag="row_sum")
-            partial = stage.tile([P, PAIR, 2, D], F32, tag="partial", bufs=1)
-            for j in range(TAPS):
-                for e in range(PAIR):
-                    t = t0 + e
-                    residual = x_src[(t + NB) // GROUP][:, (t + NB) % GROUP, :]
-                    nc.vector.scalar_tensor_tensor(
-                        out=mixed[:, e, :] if j == TAPS - 1 else partial[:, e, j % 2, :],
-                        in0=v_src[t + j][:],
-                        scalar=band[:, TAPS * t + j : TAPS * t + j + 1],
-                        in1=residual if j == 0 else partial[:, e, (j - 1) % 2, :],
-                        op0=ALU.mult,
-                        op1=ALU.add,
-                        accum_out=row_sum[:, e : e + 1] if j == TAPS - 1 else None,
-                    )
-                    if e == 0 and j < PAIR:
-                        restore(t0 + j + TAPS)
-                        if j == PAIR - 1:
-                            after_restores()
-                    if e == PAIR - 1 and j == TAPS - 2:
-                        late()
+        sums = {}
+        pairs = {}
 
+        def spread(s):
+            for j in range(TAPS - 1, -1, -1):
+                t = s - j
+                if t < 0 or t >= TILES:
+                    continue
+                if j == 0:
+                    fresh = stage.tile([P, D], F32, tag="sums", bufs=TAPS + 1)
+                    sums[t] = fresh
+                if j == TAPS - 1 and t % PAIR == 0:
+                    mixed = result.tile([P, PAIR, D], F32, bufs=6, tag="mixed")
+                    row_sum = small.tile([P, PAIR], F32, tag="row_sum")
+                    pairs[t // PAIR] = (mixed, row_sum)
+                e = t % PAIR
+                nc.vector.scalar_tensor_tensor(
+                    out=pairs[t // PAIR][0][:, e, :] if j == TAPS - 1 else sums[t][:],
+                    in0=v_src[s][:],
+                    scalar=band[:, TAPS * t + j : TAPS * t + j + 1],
+                    in1=x_src[(t + NB) // GROUP][:, (t + NB) % GROUP, :] if j == 0 else sums[t][:],
+                    op0=ALU.mult,
+                    op1=ALU.add,
+                    accum_out=pairs[t // PAIR][1][:, e : e + 1] if j == TAPS - 1 else None,
+                )
+            restore(s + V_BANKS)
+
+        def store_pair(pair):
             def store(normed):
-                nc.sync.dma_start(out=out_rows[:, t0 : t0 + PAIR, :], in_=normed[:])
+                nc.sync.dma_start(out=out_rows[:, PAIR * pair : PAIR * (pair + 1), :], in_=normed[:])
 
-            return mixed, row_sum, PAIR, store
+            return store
 
         def statistics(mixed, row_sum, n):
             neg_mean = small.tile([P, PAIR], F32, tag="neg_mean")
@@ -331,13 +365,26 @@ def tile_crosssliceattention_pb_t_kernel(tc, x, Wv_words, Wv_scales, bv, attn_ba
             nc.gpsimd.tensor_add(out=normed[:, 0:n, :], in0=normed[:, 0:n, :], in1=beta_pair[:, 0:n, :])
             store(normed)
 
+        affine = psum_const.tile([P, 2, D], BF16)
+
+        def fill_affine():
+            turned = psum_front.tile([P, 2, D], BF16, tag="front")
+            for i, rows in enumerate((gamma_pair, beta_pair)):
+                for c in range(CHUNKS):
+                    nc.tensor.transpose(turned[:, i, P * c : P * (c + 1)], rows[:, 0, P * c : P * (c + 1)], ident_bf[:])
+            columns = stage.tile([P, 2, D], BF16, tag="columns", bufs=1)
+            nc.scalar.copy(out=columns[:], in_=turned[:])
+            for i in range(2):
+                for c in range(CHUNKS):
+                    nc.tensor.transpose(affine[:, i, P * c : P * (c + 1)], columns[:, i, P * c : P * (c + 1)], ident_bf[:])
+
         def finish_on_vector(mixed, n, store, neg_mean, rstd, normed):
             for e in range(n):
                 nc.vector.scalar_tensor_tensor(
                     out=normed[:, e, :],
                     in0=mixed[:, e, :],
                     scalar=neg_mean[:, e : e + 1],
-                    in1=gamma_pair[:, 0, :],
+                    in1=affine[:, 0, :],
                     op0=ALU.add,
                     op1=ALU.mult,
                 )
@@ -347,34 +394,39 @@ def tile_crosssliceattention_pb_t_kernel(tc, x, Wv_words, Wv_scales, bv, attn_ba
                     out=final[:, e, :],
                     in0=normed[:, e, :],
                     scalar=rstd[:, e : e + 1],
-                    in1=beta_pair[:, 0, :],
+                    in1=affine[:, 1, :],
                     op0=ALU.mult,
                     op1=ALU.add,
                 )
             store(final)
 
-        band_grouped = {}
-        band_codes = {}
-        band_groups = (BAND_TILES + GROUP - 1) // GROUP
+        lone = {}
 
-        def band_front(h):
-            if h < band_groups:
-                band_grouped[h] = transpose_tiles([t[:] for t in x_band[GROUP * h : GROUP * (h + 1)]], "band_grouped", 2)
+        def lone_front():
+            columns = stage.tile([P, P * 4], BF16, align_bytes=64, bufs=1, tag="lone_grouped")
+            lone["grouped"] = columns
+            transpose_tiles([x_band[BAND_TILES - 1][:]], columns[:].bitcast(F32))
 
-        def band_quantise(h):
-            if h < band_groups:
-                band_codes[h] = quantise(band_grouped[h], min(GROUP, BAND_TILES - GROUP * h), "_band", 3)
+        def lone_quantise():
+            codes = stage.tile([P, P], U32, align_bytes=64, bufs=1, tag="lone_codes")
+            scales = stage.tile([P, P], U8, align_bytes=64, bufs=1, tag="lone_scales")
+            nc.vector.quantize_mx(out=codes[:].bitcast(FP8X4), scales=scales[:], in_=lone["grouped"][:])
+            lone["quantised"] = (codes, scales)
 
         def band_project(i):
             if i >= BAND_TILES:
                 return
-            codes, scales = band_codes[i // GROUP]
-            e = i % GROUP
+            if i == BAND_TILES - 1:
+                codes, scales = lone["quantised"]
+                at = 0
+            else:
+                codes, scales = quantised[i // GROUP + FIRST_JOINT]
+                at = P * (GROUP + i % GROUP)
             product = psum_front.tile([P, D], F32, tag="front")
             nc.tensor.matmul_mx(
                 out=product[:],
-                lhsT=codes[:, P * e : P * (e + 1)].bitcast(FP8X4),
-                lhsT_scale=scales[:, P * e : P * (e + 1)],
+                lhsT=codes[:, at : at + P].bitcast(FP8X4),
+                lhsT_scale=scales[:, at : at + P],
                 rhs=w_words[:].bitcast(FP4X4),
                 rhs_scale=w_scales[:],
                 start=True,
@@ -411,8 +463,6 @@ def tile_crosssliceattention_pb_t_kernel(tc, x, Wv_words, Wv_scales, bv, attn_ba
 
             return store
 
-        band_state = {"open": None, "ready": [], "vector": []}
-
         def band_due(slot):
             span = LAST_BAND_SLOT - FIRST_BAND_SLOT + 1
 
@@ -421,102 +471,78 @@ def tile_crosssliceattention_pb_t_kernel(tc, x, Wv_words, Wv_scales, bv, attn_ba
 
             return list(range(upto(slot - 1), upto(slot)))
 
-        def band_norms(pairs):
-            for mixed, row_sum, n, store, pair in pairs:
-                if pair % VECTOR_EVERY == VECTOR_EVERY - 1:
-                    band_state["vector"].append((mixed, n, store) + statistics(mixed, row_sum, n))
+        def joined_before(i, slot):
+            return 2 * (i // GROUP + FIRST_JOINT) - 3 < slot
+
+        front(0, True)
+        quantise(0)
+        front(1, True)
+        project(0, True)
+        quantise(1)
+        nc.vector.tensor_copy(out=band[:], in_=band_bf[:])
+        for s in range(V_BANKS):
+            restore(s)
+        project(1)
+        front(2)
+
+        band_open = None
+        summed = []
+        for_vector = []
+        for slot in range(SLOTS):
+            due = band_due(slot)
+            g = (slot + 3) // 2
+            for i in due:
+                band_matmul(i)
+            for mixed, row_sum, n, store, on_vector in summed:
+                if on_vector:
+                    for_vector.append((mixed, n, store) + statistics(mixed, row_sum, n))
                 else:
                     finish_on_gpsimd(mixed, row_sum, n, store)
-
-        def band_adds(due):
-            for job in band_state["vector"]:
-                finish_on_vector(*job)
-            band_state["vector"] = []
+            summed = []
+            for i in due:
+                if joined_before(i + AHEAD, slot):
+                    band_project(i + AHEAD)
+            if slot % 2 == 0 and slot > 0:
+                front(g + 1)
+            if slot == LONE_SLOT - 1:
+                lone_front()
+            if slot == FIRST_BAND_SLOT:
+                fill_affine()
+            spread(PAIR * slot)
+            if slot % 2 == 1:
+                quantise(g)
+            if slot == LONE_SLOT:
+                lone_quantise()
+            for i in due:
+                if not joined_before(i + AHEAD, slot):
+                    band_project(i + AHEAD)
+            if slot == FIRST_BAND_SLOT - 1:
+                for i in range(AHEAD):
+                    band_project(i)
+            if slot % 2 == 1:
+                project(g)
+            spread(PAIR * slot + 1)
+            ready_for_vector = for_vector
+            for_vector = []
+            pair = slot - NB
+            if pair >= 0:
+                mixed, row_sum = pairs[pair]
+                if pair >= TILES // PAIR - LAST_ON_VECTOR:
+                    for_vector.append((mixed, PAIR, store_pair(pair)) + statistics(mixed, row_sum, PAIR))
+                else:
+                    finish_on_gpsimd(mixed, row_sum, PAIR, store_pair(pair))
             for i in due:
                 if i % PAIR == 0:
                     mixed = result.tile([P, PAIR, D], F32, bufs=6, tag="mixed")
                     row_sum = small.tile([P, PAIR], F32, tag="row_sum")
-                    band_state["open"] = (mixed, row_sum)
-                mixed, row_sum = band_state["open"]
-                band_add(i, mixed, row_sum)
+                    band_open = (mixed, row_sum)
+                band_add(i, *band_open)
                 if i % PAIR == PAIR - 1 or i == BAND_TILES - 1:
                     n = i % PAIR + 1
-                    band_state["ready"].append((mixed, row_sum, n, band_store(i + 1 - n, n), i // PAIR))
-
-        transposed = {}
-        quantised = {}
-
-        def front(g, vector_helps=False):
-            if g < SRC_GROUPS:
-                transposed[g] = transpose_tiles([x_src[g][:, i, :] for i in range(GROUP)], "grouped", 3, vector_helps)
-
-        def quantise_src(g):
-            if g < SRC_GROUPS:
-                quantised[g] = quantise(transposed[g], GROUP, "", 2)
-
-        front(0, True)
-        quantise_src(0)
-        front(1, True)
-        projected[0] = project(*quantised[0], True)
-        quantise_src(1)
-        nc.vector.tensor_copy(out=band[:], in_=band_bf[:])
-        restore(0)
-        restore(1)
-        projected[1] = project(*quantised[1])
-        restore(2)
-        restore(3)
-        front(2)
-        restore(GROUP)
-        if FIRST_BAND_SLOT == 2:
-            band_front(0)
-
-        pending = None
-        for slot in range(SLOTS):
-            og = slot // 2
-            due = band_due(slot)
-
-            def tensor_work():
-                for i in due:
-                    band_matmul(i)
-
-            def quantising():
-                if slot % 2 == 0:
-                    quantise_src(og + 2)
-                if slot == 0:
-                    for k in range(V_BUFS):
-                        nc.vector.tensor_copy(out=v_band[k][96:P, :], in_=bv_stage[96:P, :])
-                if FIRST_BAND_SLOT - 2 <= slot < FIRST_BAND_SLOT:
-                    band_quantise(slot - FIRST_BAND_SLOT + 2)
-                for i in due:
-                    if i % GROUP == 0:
-                        band_quantise(i // GROUP + 2)
-
-            summed_pair = mix_pair(PAIR * slot, tensor_work, quantising)
-            summed_before = band_state["ready"]
-            band_state["ready"] = []
-            band_adds(due)
-            band_norms(summed_before)
-            if pending is not None:
-                finish_on_gpsimd(*pending)
-            pending = summed_pair
-            if slot % 2 == 0:
-                if og + 2 < SRC_GROUPS:
-                    projected[og + 2] = project(*quantised[og + 2])
-            else:
-                front(og + 4)
-            if slot == 0:
-                front(3)
-            if FIRST_BAND_SLOT - 3 <= slot < FIRST_BAND_SLOT:
-                band_front(slot - FIRST_BAND_SLOT + 3)
-            if FIRST_BAND_SLOT - 2 <= slot < FIRST_BAND_SLOT:
-                band_project(2 * (slot - FIRST_BAND_SLOT + 2))
-                band_project(2 * (slot - FIRST_BAND_SLOT + 2) + 1)
-            for i in due:
-                band_project(i + AHEAD)
-                if i % GROUP == 1:
-                    band_front(i // GROUP + 3)
-        band_norms(band_state["ready"])
-        for job in band_state["vector"]:
+                    on_vector = (i // PAIR) % VECTOR_EVERY == VECTOR_EVERY - 1
+                    summed.append(band_open + (n, band_store(i + 1 - n, n), on_vector))
+            for job in ready_for_vector:
+                finish_on_vector(*job)
+        assert not summed
+        for job in for_vector:
             finish_on_vector(*job)
-        mixed, row_sum, n, store = pending
-        finish_on_vector(mixed, n, store, *statistics(mixed, row_sum, n))

@@ -40,7 +40,7 @@ SRC_GROUPS = SRC_TILES // GROUP
 V_BANKS = 3
 SLOTS = SRC_TILES // PAIR
 FIRST_BAND_SLOT = 4
-LAST_BAND_SLOT = 19
+LAST_BAND_SLOT = 20
 FIRST_JOINT = 3
 VECTOR_EVERY = 4
 LAST_ON_VECTOR = 3
@@ -77,20 +77,23 @@ def tile_crosssliceattention_pb_t_kernel(tc, x, Wv_words, Wv_scales, bv, attn_ba
         w_words = const.tile([P, 2 * D], U8, align_bytes=64)
         w_scales = const.tile([P, D], U8, align_bytes=64)
         nc.vector.memset(w_scales[:].bitcast(I32), 0)
+        weights = const.tile([P, COEF, PITCH], F32)
+        nc.vector.memset(weights[:], 0.0)
         eps_col = const.tile([P, 1], F32)
         nc.vector.memset(eps_col[:], LN_EPS)
         zero = const.tile([1, TAIL * PITCH], F32)
         nc.vector.memset(zero[:], 0.0)
         coef_before = const.tile([P, NB, TAPS], BF16)
         nc.gpsimd.memset(coef_before[:], 0.0)
-        weights = const.tile([P, COEF, PITCH], F32)
-        nc.gpsimd.memset(weights[:], 0.0)
 
         x_src = [const.tile([P, GROUP, D], BF16, name="x_src%d" % g) for g in range(SRC_GROUPS)]
         last = SRC_GROUPS - 1
         nc.vector.memset(x_src[last][:, NB:GROUP, :], 0.0)
         x_band = [const.tile([P, D], BF16, name="x_band%d" % i) for i in range(BAND_TILES)]
         nc.vector.memset(x_band[0][0:NB, :], 0.0)
+
+        def gpsimd_copy(target, source):
+            nc.gpsimd.tensor_scalar(out=target, in0=source, scalar1=1.0, scalar2=0.0, op0=ALU.mult, op1=ALU.add)
 
         def load_src(g):
             if g < last:
@@ -118,7 +121,7 @@ def tile_crosssliceattention_pb_t_kernel(tc, x, Wv_words, Wv_scales, bv, attn_ba
         with nc.allow_non_contiguous_dma(reason="512 bias values, one to a partition for each chunk of n"):
             nc.sync.dma_start(out=bv_bf[:], in_=bv.rearrange("(c n) -> n c", n=P))
         bv_col = const.tile([P, CHUNKS], F32)
-        nc.vector.tensor_copy(out=bv_col[:], in_=bv_bf[:])
+        nc.scalar.copy(out=bv_col[:], in_=bv_bf[:])
         load_src(1)
         band_bf = const.tile([P, TILES * TAPS], BF16)
         nc.sync.dma_start(out=band_bf[:], in_=band_rows)
@@ -160,8 +163,8 @@ def tile_crosssliceattention_pb_t_kernel(tc, x, Wv_words, Wv_scales, bv, attn_ba
         )
         for j in range(2, TAPS):
             nc.gpsimd.tensor_tensor(out=weight_sum[:], in0=weight_sum[:], in1=coef[:, NB : NB + COEF, j], op=ALU.add)
-        nc.gpsimd.tensor_copy(out=gamma_pair[:, 1, :], in_=gamma_pair[:, 0, :])
-        nc.gpsimd.tensor_copy(out=beta_pair[:, 1, :], in_=beta_pair[:, 0, :])
+        for rows in (gamma_pair, beta_pair):
+            gpsimd_copy(rows[:, 1, :], rows[:, 0, :])
 
         nc.sync.dma_start(
             out=scratch[NB * PITCH : (NB + BAND_ROWS) * PITCH].rearrange("(p l w) -> p l w", l=COEF, w=PITCH),
@@ -174,7 +177,7 @@ def tile_crosssliceattention_pb_t_kernel(tc, x, Wv_words, Wv_scales, bv, attn_ba
         nc.sync.dma_start(out=bv_stage[96:P, :], in_=bv.partition_broadcast(32))
         v_band = [const.tile([P, D], F32, name="v_band%d" % k) for k in range(V_BUFS)]
         for k in range(V_BUFS):
-            nc.gpsimd.tensor_copy(out=v_band[k][96:P, :], in_=bv_stage[96:P, :])
+            gpsimd_copy(v_band[k][96:P, :], bv_stage[96:P, :])
         load_src(4)
         for i in range(4, 8):
             load_band(i)
@@ -479,7 +482,7 @@ def tile_crosssliceattention_pb_t_kernel(tc, x, Wv_words, Wv_scales, bv, attn_ba
         front(1, True)
         project(0, True)
         quantise(1)
-        nc.vector.tensor_copy(out=band[:], in_=band_bf[:])
+        nc.scalar.copy(out=band[:], in_=band_bf[:])
         for s in range(V_BANKS):
             restore(s)
         project(1)
@@ -506,7 +509,7 @@ def tile_crosssliceattention_pb_t_kernel(tc, x, Wv_words, Wv_scales, bv, attn_ba
                 front(g + 1)
             if slot == LONE_SLOT - 1:
                 lone_front()
-            if slot == FIRST_BAND_SLOT:
+            if slot == 1:
                 fill_affine()
             spread(PAIR * slot)
             if slot % 2 == 1:

@@ -35,18 +35,36 @@ AHEAD = 2
 V_BUFS = 2 * AHEAD
 
 TILES = (ROWS - BAND_ROWS) // P
-SRC_TILES = TILES + 2 * NB
-SRC_GROUPS = SRC_TILES // GROUP
+SRC_GROUPS = TILES // GROUP
+SOURCES = list(range(TILES + NB)) + list(range(-NB, 0))
 V_BANKS = 3
-SLOTS = SRC_TILES // PAIR
-FIRST_BAND_SLOT = 4
-LAST_BAND_SLOT = 20
-FIRST_JOINT = 3
-VECTOR_EVERY = 4
-LAST_ON_VECTOR = 3
-LONE_SLOT = 2 * (BAND_GROUPS - 1 + FIRST_JOINT) - 3
+SLOTS = len(SOURCES) // PAIR
+FIRST_BAND_SLOT = 3
+LAST_BAND_SLOT = 19
+SHARED = 5
+MIXED_BUFS = 16
+LAG = 2
+VECTOR_FROM = 18
+TURN_FROM = 17
+ALPHA = 2
+ALPHA_OF = 5
+FRONT_BUFS = 5
+CODES_BUFS = 2
+BAND_FRONTS = 2
 
 FLOPS = 2 * ROWS * D * D
+
+
+def band_slot(i):
+    return FIRST_BAND_SLOT + i * (LAST_BAND_SLOT - FIRST_BAND_SLOT + 1) // BAND_TILES
+
+
+def project_slot(i):
+    return FIRST_BAND_SLOT - 1 if i < AHEAD else band_slot(i - AHEAD)
+
+
+def quantise_slot(g):
+    return 2 * g - 3
 
 
 def tile_crosssliceattention_pb_t_kernel(tc, x, Wv_words, Wv_scales, bv, attn_band, gamma, beta, out):
@@ -55,7 +73,6 @@ def tile_crosssliceattention_pb_t_kernel(tc, x, Wv_words, Wv_scales, bv, attn_ba
     out_all = out.flatten_outer_dims()
     band_all = attn_band.flatten_outer_dims()
     x_rows = x_all[BAND_ROWS:ROWS, :].rearrange("(p t) d -> p t d", t=TILES)
-    x_from_halo = x_all[BAND_ROWS - NB : ROWS - NB, :].rearrange("(p t) d -> p t d", t=TILES)
     out_rows = out_all[BAND_ROWS:ROWS, :].rearrange("(p t) d -> p t d", t=TILES)
     band_rows = band_all[BAND_ROWS:ROWS, :].rearrange("(p t) j -> p (t j)", t=TILES)
     scratch = out_all[BAND_ROWS - SCRATCH_ROWS : BAND_ROWS, :].rearrange("r d -> (r d)")
@@ -63,11 +80,10 @@ def tile_crosssliceattention_pb_t_kernel(tc, x, Wv_words, Wv_scales, bv, attn_ba
     with (
         tc.tile_pool(name="const", bufs=1) as const,
         tc.tile_pool(name="stage", bufs=2) as stage,
-        tc.tile_pool(name="result", bufs=3) as result,
-        tc.tile_pool(name="small", bufs=6) as small,
-        tc.psum_pool(name="psum_front", bufs=4) as psum_front,
+        tc.tile_pool(name="result", bufs=MIXED_BUFS) as result,
+        tc.tile_pool(name="small", bufs=8) as small,
+        tc.psum_pool(name="psum_front", bufs=FRONT_BUFS) as psum_front,
         tc.psum_pool(name="psum_v", bufs=V_BANKS) as psum_v,
-        tc.psum_pool(name="psum_const", bufs=1) as psum_const,
         tc.manual_schedule(),
     ):
         ident = const.tile([P, P], F32)
@@ -77,18 +93,23 @@ def tile_crosssliceattention_pb_t_kernel(tc, x, Wv_words, Wv_scales, bv, attn_ba
         w_words = const.tile([P, 2 * D], U8, align_bytes=64)
         w_scales = const.tile([P, D], U8, align_bytes=64)
         nc.vector.memset(w_scales[:].bitcast(I32), 0)
-        weights = const.tile([P, COEF, PITCH], F32)
+        weights = stage.tile([P, COEF, PITCH], F32, tag="weights", bufs=1)
         nc.vector.memset(weights[:], 0.0)
         eps_col = const.tile([P, 1], F32)
         nc.vector.memset(eps_col[:], LN_EPS)
-        zero = const.tile([1, TAIL * PITCH], F32)
+        zero = const.tile([TAIL, PITCH], F32)
         nc.vector.memset(zero[:], 0.0)
         coef_before = const.tile([P, NB, TAPS], BF16)
         nc.gpsimd.memset(coef_before[:], 0.0)
 
-        x_src = [const.tile([P, GROUP, D], BF16, name="x_src%d" % g) for g in range(SRC_GROUPS)]
-        last = SRC_GROUPS - 1
-        nc.vector.memset(x_src[last][:, NB:GROUP, :], 0.0)
+        x_src = []
+        for g in range(SRC_GROUPS):
+            if g < SHARED:
+                early_tile = result.tile([P, GROUP, D], BF16, tag="mixed")
+                x_src.append(early_tile)
+            else:
+                late_tile = const.tile([P, GROUP, D], BF16, name="x_src%d" % g)
+                x_src.append(late_tile)
         x_band = [const.tile([P, D], BF16, name="x_band%d" % i) for i in range(BAND_TILES)]
         nc.vector.memset(x_band[0][0:NB, :], 0.0)
 
@@ -96,12 +117,7 @@ def tile_crosssliceattention_pb_t_kernel(tc, x, Wv_words, Wv_scales, bv, attn_ba
             nc.gpsimd.tensor_scalar(out=target, in0=source, scalar1=1.0, scalar2=0.0, op0=ALU.mult, op1=ALU.add)
 
         def load_src(g):
-            if g < last:
-                nc.sync.dma_start(out=x_src[g][:], in_=x_from_halo[:, GROUP * g : GROUP * (g + 1), :])
-            else:
-                nc.sync.dma_start(out=x_src[last][:, 0:NB, :], in_=x_rows[:, TILES - NB : TILES, :])
-                for lo, hi in ((0, 64), (64, P - 1)):
-                    nc.sync.dma_start(out=x_src[last][lo:hi, NB:GROUP, :], in_=x_rows[lo + 1 : hi + 1, 0:NB, :])
+            nc.sync.dma_start(out=x_src[g][:], in_=x_rows[:, GROUP * g : GROUP * (g + 1), :])
 
         def load_band(i):
             if i == 0:
@@ -109,8 +125,8 @@ def tile_crosssliceattention_pb_t_kernel(tc, x, Wv_words, Wv_scales, bv, attn_ba
             else:
                 nc.sync.dma_start(out=x_band[i][:], in_=x_all[BAND_STEP * i - NB : BAND_STEP * i - NB + P, :])
 
-        nc.sync.dma_start(out=x_src[0][:, 0:PAIR, :], in_=x_from_halo[:, 0:PAIR, :])
-        nc.sync.dma_start(out=x_src[0][:, PAIR:GROUP, :], in_=x_from_halo[:, PAIR:GROUP, :])
+        nc.sync.dma_start(out=x_src[0][:, 0:PAIR, :], in_=x_rows[:, 0:PAIR, :])
+        nc.sync.dma_start(out=x_src[0][:, PAIR:GROUP, :], in_=x_rows[:, PAIR:GROUP, :])
         nc.sync.dma_start(out=w_words[:].bitcast(I32), in_=Wv_words[0].bitcast(I32))
         for quadrant in range(4):
             nc.sync.dma_start(
@@ -137,9 +153,9 @@ def tile_crosssliceattention_pb_t_kernel(tc, x, Wv_words, Wv_scales, bv, attn_ba
             out=coef_after[:],
             in_=band_all[COEF : COEF + BAND_ROWS, :].rearrange("(p l) j -> p l j", l=COEF)[:, 0:NB, :],
         )
-        nc.sync.dma_start(out=scratch[0 : NB * PITCH].rearrange("(o z) -> o z", o=1), in_=zero[:, 0 : NB * PITCH])
+        nc.sync.dma_start(out=scratch[0 : NB * PITCH].rearrange("(o z) -> o z", o=NB), in_=zero[0:NB, :])
         nc.sync.dma_start(
-            out=scratch[(NB + BAND_ROWS) * PITCH : (NB + BAND_ROWS + TAIL) * PITCH].rearrange("(o z) -> o z", o=1),
+            out=scratch[(NB + BAND_ROWS) * PITCH : (NB + BAND_ROWS + TAIL) * PITCH].rearrange("(o z) -> o z", o=TAIL),
             in_=zero[:],
         )
         load_src(2)
@@ -147,13 +163,13 @@ def tile_crosssliceattention_pb_t_kernel(tc, x, Wv_words, Wv_scales, bv, attn_ba
         nc.sync.dma_start(out=gamma_pair[:, 0, :], in_=gamma.partition_broadcast(P))
         beta_pair = const.tile([P, PAIR, D], BF16)
         nc.sync.dma_start(out=beta_pair[:, 0, :], in_=beta.partition_broadcast(P))
-        load_src(3)
-        for i in range(4):
+        for i in range(8):
             load_band(i)
+        load_src(3)
 
         coef = const.tile([P, COEF + 2 * NB, TAPS], F32)
-        nc.gpsimd.tensor_copy(out=coef[:, 0:NB, :], in_=coef_before[:])
         nc.gpsimd.tensor_copy(out=coef[:, NB : NB + COEF, :], in_=coef_main[:])
+        nc.gpsimd.tensor_copy(out=coef[:, 0:NB, :], in_=coef_before[:])
         nc.gpsimd.tensor_copy(out=coef[:, NB + COEF : 2 * NB + COEF, :], in_=coef_after[:])
         for i in range(TAPS):
             nc.gpsimd.tensor_copy(out=weights[:, :, i], in_=coef[:, i : i + COEF, TAPS - 1 - i])
@@ -178,29 +194,34 @@ def tile_crosssliceattention_pb_t_kernel(tc, x, Wv_words, Wv_scales, bv, attn_ba
         v_band = [const.tile([P, D], F32, name="v_band%d" % k) for k in range(V_BUFS)]
         for k in range(V_BUFS):
             gpsimd_copy(v_band[k][96:P, :], bv_stage[96:P, :])
-        load_src(4)
-        for i in range(4, 8):
+        for i in range(8, 16):
             load_band(i)
+        load_src(4)
         band_t = const.tile([P, BAND_TILES, P], F32)
-        for i in range(BAND_TILES):
-            start = BAND_STEP * i * PITCH + NB
-            nc.sync.dma_start(
-                out=band_t[:, i, :],
-                in_=scratch[start : start + P * WIDTH].rearrange("(c w) -> c w", w=WIDTH)[:, 0:P],
-            )
         whole = BAND_TILES - 1
-        nc.sync.dma_start(
-            out=band_t[P - 1 : P, 0:whole, NB : NB + BAND_STEP],
-            in_=scratch[SUMS_AT : SUMS_AT + whole * BAND_STEP].rearrange("(o i m) -> o i m", o=1, m=BAND_STEP),
-        )
+        for i0, i1 in ((0, GROUP), (GROUP, BAND_TILES)):
+            for i in range(i0, i1):
+                start = BAND_STEP * i * PITCH + NB
+                nc.sync.dma_start(
+                    out=band_t[:, i, :],
+                    in_=scratch[start : start + P * WIDTH].rearrange("(c w) -> c w", w=WIDTH)[:, 0:P],
+                )
+            if i0 == 0:
+                for i in range(16, BAND_TILES):
+                    load_band(i)
+            i1 = min(i1, whole)
+            nc.sync.dma_start(
+                out=band_t[P - 1 : P, i0:i1, NB : NB + BAND_STEP],
+                in_=scratch[SUMS_AT + i0 * BAND_STEP : SUMS_AT + i1 * BAND_STEP].rearrange(
+                    "(o i m) -> o i m", o=1, m=BAND_STEP
+                ),
+            )
         nc.sync.dma_start(
             out=band_t[P - 1 : P, whole, NB : NB + BAND_ROWS - whole * BAND_STEP],
             in_=scratch[SUMS_AT + whole * BAND_STEP : SUMS_AT + BAND_ROWS].rearrange("(o m) -> o m", o=1),
         )
         for g in range(5, SRC_GROUPS):
             load_src(g)
-            for i in range(3 * g - 7, min(3 * g - 4, BAND_TILES)):
-                load_band(i)
 
         def transpose_tiles(sources, grouped_words, vector_helps=False):
             for first in range(0, len(sources), 2):
@@ -222,40 +243,41 @@ def tile_crosssliceattention_pb_t_kernel(tc, x, Wv_words, Wv_scales, bv, attn_ba
 
         grouped = {}
         quantised = {}
-
-        def joint_band_group(g):
-            h = g - FIRST_JOINT
-            return h if 0 <= h < BAND_GROUPS else None
-
-        def band_tiles_of(h):
-            return range(GROUP * h, min(GROUP * (h + 1), BAND_TILES))
+        band_codes = const.tile([P, BAND_TILES * P], U32, align_bytes=64)
+        band_scales = const.tile([P, BAND_TILES * P], U8, align_bytes=64)
 
         def front(g, vector_helps=False):
-            if g >= SRC_GROUPS:
-                return
-            h = joint_band_group(g)
-            tiles = GROUP if h is None or len(band_tiles_of(h)) < GROUP else 2 * GROUP
-            columns = stage.tile([P, tiles * P * 4], BF16, align_bytes=64, bufs=2, tag="grouped")
+            columns = stage.tile([P, GROUP * P * 4], BF16, align_bytes=64, bufs=4, tag="grouped")
             grouped[g] = columns
-            words = columns[:].bitcast(F32)
-            transpose_tiles([x_src[g][:, i, :] for i in range(GROUP)], words[:, 0 : GROUP * 2 * P], vector_helps)
-            if tiles == 2 * GROUP:
-                transpose_tiles([x_band[i][:] for i in band_tiles_of(h)], words[:, GROUP * 2 * P : tiles * 2 * P])
+            transpose_tiles([x_src[g][:, i, :] for i in range(GROUP)], columns[:].bitcast(F32), vector_helps)
 
         def quantise(g):
-            if g >= SRC_GROUPS:
-                return
-            columns = grouped[g][:].shape[1] // 4
-            codes = stage.tile([P, columns], U32, align_bytes=64, bufs=3, tag="codes")
-            scales = stage.tile([P, columns], U8, align_bytes=64, bufs=3, tag="scales")
+            codes = stage.tile([P, GROUP * P], U32, align_bytes=64, bufs=CODES_BUFS, tag="codes")
+            scales = stage.tile([P, GROUP * P], U8, align_bytes=64, bufs=CODES_BUFS, tag="scales")
             nc.vector.quantize_mx(out=codes[:].bitcast(FP8X4), scales=scales[:], in_=grouped[g][:])
             quantised[g] = (codes, scales)
 
+        def band_front(h):
+            tiles = range(GROUP * h, min(GROUP * (h + 1), BAND_TILES))
+            columns = stage.tile([P, GROUP * P * 4], BF16, align_bytes=64, bufs=4, tag="grouped")
+            grouped[-1 - h] = columns[:, 0 : len(tiles) * P * 4]
+            transpose_tiles([x_band[i][:] for i in tiles], grouped[-1 - h].bitcast(F32))
+
+        def band_quantise(h):
+            lo, hi = P * GROUP * h, P * min(GROUP * (h + 1), BAND_TILES)
+            nc.vector.quantize_mx(
+                out=band_codes[:, lo:hi].bitcast(FP8X4), scales=band_scales[:, lo:hi], in_=grouped[-1 - h]
+            )
+
+        projected = {}
+        v_src = {}
+
         def project(g, vector_helps=False):
-            if g >= SRC_GROUPS:
-                return
             codes, scales = quantised[g]
-            v_by_feature = stage.tile([P, CHUNKS, GROUP * P], F32, tag="v_by_feature")
+            if g == 0:
+                v_by_feature = const.tile([P, CHUNKS, GROUP * P], F32, name="v_by_feature_0")
+            else:
+                v_by_feature = stage.tile([P, CHUNKS, GROUP * P], F32, tag="v_by_feature")
             for c in range(CHUNKS):
                 product = psum_front.tile([P, GROUP * P], F32, tag="front")
                 nc.tensor.matmul_mx(
@@ -281,47 +303,51 @@ def tile_crosssliceattention_pb_t_kernel(tc, x, Wv_words, Wv_scales, bv, attn_ba
                     )
             projected[g] = v_by_feature
 
-        projected = {}
-        v_src = {}
-
-        def restore(s):
-            if s >= SRC_TILES:
+        def restore(position):
+            if position >= len(SOURCES):
                 return
+            s = SOURCES[position]
+            t = s % TILES
+            first = P * (t % GROUP) + s // TILES
             v_rows = psum_v.tile([P, D], F32, tag="v")
             for c in range(CHUNKS):
                 nc.tensor.transpose(
-                    v_rows[:, P * c : P * (c + 1)],
-                    projected[s // GROUP][:, c, P * (s % GROUP) : P * (s % GROUP + 1)],
-                    ident[:],
+                    v_rows[:, P * c : P * (c + 1)], projected[t // GROUP][:, c, first : first + P], ident[:]
                 )
             v_src[s] = v_rows
 
         sums = {}
         pairs = {}
 
-        def spread(s):
+        def spread(position):
+            s = SOURCES[position]
             for j in range(TAPS - 1, -1, -1):
-                t = s - j
+                t = s + NB - j
                 if t < 0 or t >= TILES:
                     continue
-                if j == 0:
-                    fresh = stage.tile([P, D], F32, tag="sums", bufs=TAPS + 1)
+                begins = s == max(t - NB, 0)
+                ends = s == (t + NB if t >= NB else -1)
+                if begins:
+                    if t < NB:
+                        fresh = const.tile([P, D], F32, name="sums_%d" % t)
+                    else:
+                        fresh = stage.tile([P, D], F32, tag="sums", bufs=TAPS)
                     sums[t] = fresh
-                if j == TAPS - 1 and t % PAIR == 0:
-                    mixed = result.tile([P, PAIR, D], F32, bufs=6, tag="mixed")
+                if ends and t % PAIR == 0:
+                    mixed = result.tile([P, PAIR, D], F32, tag="mixed")
                     row_sum = small.tile([P, PAIR], F32, tag="row_sum")
                     pairs[t // PAIR] = (mixed, row_sum)
                 e = t % PAIR
                 nc.vector.scalar_tensor_tensor(
-                    out=pairs[t // PAIR][0][:, e, :] if j == TAPS - 1 else sums[t][:],
+                    out=pairs[t // PAIR][0][:, e, :] if ends else sums[t][:],
                     in0=v_src[s][:],
                     scalar=band[:, TAPS * t + j : TAPS * t + j + 1],
-                    in1=x_src[(t + NB) // GROUP][:, (t + NB) % GROUP, :] if j == 0 else sums[t][:],
+                    in1=x_src[t // GROUP][:, t % GROUP, :] if begins else sums[t][:],
                     op0=ALU.mult,
                     op1=ALU.add,
-                    accum_out=pairs[t // PAIR][1][:, e : e + 1] if j == TAPS - 1 else None,
+                    accum_out=pairs[t // PAIR][1][:, e : e + 1] if ends else None,
                 )
-            restore(s + V_BANKS)
+            restore(position + V_BANKS)
 
         def store_pair(pair):
             def store(normed):
@@ -329,107 +355,122 @@ def tile_crosssliceattention_pb_t_kernel(tc, x, Wv_words, Wv_scales, bv, attn_ba
 
             return store
 
-        def statistics(mixed, row_sum, n):
+        def centre(row_sum, n):
             neg_mean = small.tile([P, PAIR], F32, tag="neg_mean")
             nc.scalar.mul(out=neg_mean[:, 0:n], in_=row_sum[:, 0:n], mul=-1.0 / D)
-            normed = result.tile([P, PAIR, D], F32, bufs=5, tag="normed")
+            return neg_mean
+
+        def spread_of(mixed, row_sum, n):
             square_sum = small.tile([P, PAIR], F32, tag="square_sum")
             for e in range(n):
+                squares = small.tile([P, D], BF16, tag="squares", bufs=4)
                 nc.scalar.activation(
-                    out=normed[:, e, :],
+                    out=squares[:],
                     in_=mixed[:, e, :],
                     func=ACT.Square,
-                    bias=neg_mean[:, e : e + 1],
-                    scale=1.0,
+                    bias=row_sum[:, e : e + 1],
+                    scale=-float(D),
                     accum_out=square_sum[:, e : e + 1],
                 )
+            return square_sum
+
+        def invert(square_sum, n):
             rstd = small.tile([P, PAIR], F32, tag="rstd")
             nc.scalar.activation(
-                out=rstd[:, 0:n], in_=square_sum[:, 0:n], func=ACT.Abs_reciprocal_sqrt, bias=eps_col[:, 0:1], scale=1.0 / D
+                out=rstd[:, 0:n],
+                in_=square_sum[:, 0:n],
+                func=ACT.Abs_reciprocal_sqrt,
+                bias=eps_col[:, 0:1],
+                scale=1.0 / D**3,
             )
-            return neg_mean, rstd, normed
+            return rstd
 
-        def finish_on_gpsimd(mixed, row_sum, n, store):
-            neg_mean, rstd, normed = statistics(mixed, row_sum, n)
-            shift = small.tile([P, PAIR], F32, tag="shift")
+        def normalise(mixed, neg_mean, rstd, n):
             for e in range(n):
-                nc.scalar.activation(
-                    out=shift[:, e : e + 1], in_=neg_mean[:, e : e + 1], func=ACT.Copy, scale=rstd[:, e : e + 1]
+                nc.gpsimd.tensor_scalar(
+                    out=mixed[:, e, :],
+                    in0=mixed[:, e, :],
+                    scalar1=neg_mean[:, e : e + 1],
+                    scalar2=rstd[:, e : e + 1],
+                    op0=ALU.add,
+                    op1=ALU.mult,
                 )
-            for e in range(n):
-                nc.scalar.activation(
-                    out=normed[:, e, :],
-                    in_=mixed[:, e, :],
-                    func=ACT.Identity,
-                    bias=shift[:, e : e + 1],
-                    scale=rstd[:, e : e + 1],
-                )
+
+        def finish_on_gpsimd(normed, n, store):
             nc.gpsimd.tensor_mul(out=normed[:, 0:n, :], in0=normed[:, 0:n, :], in1=gamma_pair[:, 0:n, :])
             nc.gpsimd.tensor_add(out=normed[:, 0:n, :], in0=normed[:, 0:n, :], in1=beta_pair[:, 0:n, :])
             store(normed)
 
-        affine = psum_const.tile([P, 2, D], BF16)
+        affine_col = const.tile([P, 2, CHUNKS], F32)
 
         def fill_affine():
             turned = psum_front.tile([P, 2, D], BF16, tag="front")
             for i, rows in enumerate((gamma_pair, beta_pair)):
                 for c in range(CHUNKS):
                     nc.tensor.transpose(turned[:, i, P * c : P * (c + 1)], rows[:, 0, P * c : P * (c + 1)], ident_bf[:])
-            columns = stage.tile([P, 2, D], BF16, tag="columns", bufs=1)
-            nc.scalar.copy(out=columns[:], in_=turned[:])
-            for i in range(2):
-                for c in range(CHUNKS):
-                    nc.tensor.transpose(affine[:, i, P * c : P * (c + 1)], columns[:, i, P * c : P * (c + 1)], ident_bf[:])
+            nc.scalar.copy(out=affine_col[:], in_=turned[:].rearrange("n i (c p) -> n i c p", c=CHUNKS)[:, :, :, 0])
 
-        def finish_on_vector(mixed, n, store, neg_mean, rstd, normed):
+        thirds = []
+        turned = []
+
+        def turn(normed, n, store):
+            if not thirds:
+                by_feature = stage.tile([P, 3, CHUNKS, PAIR * P], F32, tag="weights", bufs=1)
+                thirds.extend([by_feature[:, k, :, :] for k in range(3)])
+            half = thirds[len(turned) % 3]
+            turned.append(half)
+            for c0 in range(0, CHUNKS, 2):
+                bank = psum_front.tile([P, 2, PAIR * P], F32, tag="front")
+                for c in range(2):
+                    for e in range(n):
+                        nc.tensor.transpose(
+                            bank[:, c, P * e : P * (e + 1)], normed[:, e, P * (c0 + c) : P * (c0 + c + 1)], ident[:]
+                        )
+                for c in range(2):
+                    nc.scalar.activation(
+                        out=half[:, c0 + c, 0 : n * P],
+                        in_=bank[:, c, 0 : n * P],
+                        func=ACT.Identity,
+                        bias=affine_col[:, 1, c0 + c : c0 + c + 1],
+                        scale=affine_col[:, 0, c0 + c : c0 + c + 1],
+                    )
+            return half, normed, n, store
+
+        def turn_back(half, normed, n, store):
+            for e in range(n):
+                bank = psum_front.tile([P, D], F32, tag="front")
+                for c in range(CHUNKS):
+                    nc.tensor.transpose(bank[:, P * c : P * (c + 1)], half[:, c, P * e : P * (e + 1)], ident[:])
+                nc.scalar.copy(out=normed[:, e, :], in_=bank[:])
+            store(normed)
+
+        def finish_on_vector(mixed, neg_mean, rstd, n, store):
             for e in range(n):
                 nc.vector.scalar_tensor_tensor(
-                    out=normed[:, e, :],
+                    out=mixed[:, e, :],
                     in0=mixed[:, e, :],
                     scalar=neg_mean[:, e : e + 1],
-                    in1=affine[:, 0, :],
+                    in1=gamma_pair[:, e, :],
                     op0=ALU.add,
                     op1=ALU.mult,
                 )
-            final = result.tile([P, PAIR, D], F32, bufs=5, tag="normed")
             for e in range(n):
                 nc.vector.scalar_tensor_tensor(
-                    out=final[:, e, :],
-                    in0=normed[:, e, :],
+                    out=mixed[:, e, :],
+                    in0=mixed[:, e, :],
                     scalar=rstd[:, e : e + 1],
-                    in1=affine[:, 1, :],
+                    in1=beta_pair[:, e, :],
                     op0=ALU.mult,
                     op1=ALU.add,
                 )
-            store(final)
-
-        lone = {}
-
-        def lone_front():
-            columns = stage.tile([P, P * 4], BF16, align_bytes=64, bufs=1, tag="lone_grouped")
-            lone["grouped"] = columns
-            transpose_tiles([x_band[BAND_TILES - 1][:]], columns[:].bitcast(F32))
-
-        def lone_quantise():
-            codes = stage.tile([P, P], U32, align_bytes=64, bufs=1, tag="lone_codes")
-            scales = stage.tile([P, P], U8, align_bytes=64, bufs=1, tag="lone_scales")
-            nc.vector.quantize_mx(out=codes[:].bitcast(FP8X4), scales=scales[:], in_=lone["grouped"][:])
-            lone["quantised"] = (codes, scales)
+            store(mixed)
 
         def band_project(i):
-            if i >= BAND_TILES:
-                return
-            if i == BAND_TILES - 1:
-                codes, scales = lone["quantised"]
-                at = 0
-            else:
-                codes, scales = quantised[i // GROUP + FIRST_JOINT]
-                at = P * (GROUP + i % GROUP)
             product = psum_front.tile([P, D], F32, tag="front")
             nc.tensor.matmul_mx(
                 out=product[:],
-                lhsT=codes[:, at : at + P].bitcast(FP8X4),
-                lhsT_scale=scales[:, at : at + P],
+                lhsT=band_codes[:, P * i : P * (i + 1)].bitcast(FP8X4),
+                lhsT_scale=band_scales[:, P * i : P * (i + 1)],
                 rhs=w_words[:].bitcast(FP4X4),
                 rhs_scale=w_scales[:],
                 start=True,
@@ -466,17 +507,6 @@ def tile_crosssliceattention_pb_t_kernel(tc, x, Wv_words, Wv_scales, bv, attn_ba
 
             return store
 
-        def band_due(slot):
-            span = LAST_BAND_SLOT - FIRST_BAND_SLOT + 1
-
-            def upto(k):
-                return min(BAND_TILES, max(0, ((k - FIRST_BAND_SLOT + 1) * BAND_TILES + span - 1) // span))
-
-            return list(range(upto(slot - 1), upto(slot)))
-
-        def joined_before(i, slot):
-            return 2 * (i // GROUP + FIRST_JOINT) - 3 < slot
-
         front(0, True)
         quantise(0)
         front(1, True)
@@ -490,62 +520,82 @@ def tile_crosssliceattention_pb_t_kernel(tc, x, Wv_words, Wv_scales, bv, attn_ba
 
         band_open = None
         summed = []
-        for_vector = []
+        to_turn = {}
+        to_turn_back = {}
+        on_vector = []
+        order = []
+
+        def hand_over(slot, job):
+            order.append(job)
+            if slot >= VECTOR_FROM:
+                how = "vector"
+            elif slot >= TURN_FROM or len(order) % ALPHA_OF >= ALPHA:
+                how = "turn"
+            else:
+                how = "gpsimd"
+            summed.append((how,) + job)
+
+        def layer_norms(step):
+            for job in to_turn_back.get(step, []):
+                turn_back(*job)
+            to_turn_back[step + 1] = [turn(*job) for job in to_turn.get(step, [])]
+            on_gpsimd = []
+            to_turn[step + LAG] = []
+            for how, mixed, row_sum, n, store in summed:
+                square_sum = spread_of(mixed, row_sum, n)
+                neg_mean = centre(row_sum, n)
+                rstd = invert(square_sum, n)
+                if how == "vector":
+                    on_vector.append((mixed, neg_mean, rstd, n, store))
+                    continue
+                normalise(mixed, neg_mean, rstd, n)
+                if how == "gpsimd":
+                    on_gpsimd.append((mixed, n, store))
+                else:
+                    to_turn[step + LAG].append((mixed, n, store))
+            summed.clear()
+            for job in on_gpsimd:
+                finish_on_gpsimd(*job)
+
         for slot in range(SLOTS):
-            due = band_due(slot)
-            g = (slot + 3) // 2
+            due = [i for i in range(BAND_TILES) if band_slot(i) == slot]
             for i in due:
                 band_matmul(i)
-            for mixed, row_sum, n, store, on_vector in summed:
-                if on_vector:
-                    for_vector.append((mixed, n, store) + statistics(mixed, row_sum, n))
-                else:
-                    finish_on_gpsimd(mixed, row_sum, n, store)
-            summed = []
-            for i in due:
-                if joined_before(i + AHEAD, slot):
-                    band_project(i + AHEAD)
-            if slot % 2 == 0 and slot > 0:
-                front(g + 1)
-            if slot == LONE_SLOT - 1:
-                lone_front()
+            for i in range(BAND_TILES):
+                if project_slot(i) == slot:
+                    band_project(i)
+            if slot % 2 == 0 and 0 < slot and slot // 2 + 2 < SRC_GROUPS:
+                front(slot // 2 + 2)
+            for h in range(BAND_GROUPS):
+                if h // BAND_FRONTS == slot:
+                    band_front(h)
             if slot == 1:
                 fill_affine()
             spread(PAIR * slot)
-            if slot % 2 == 1:
+            g = (slot + 3) // 2
+            if slot % 2 == 1 and g < SRC_GROUPS:
                 quantise(g)
-            if slot == LONE_SLOT:
-                lone_quantise()
-            for i in due:
-                if not joined_before(i + AHEAD, slot):
-                    band_project(i + AHEAD)
-            if slot == FIRST_BAND_SLOT - 1:
-                for i in range(AHEAD):
-                    band_project(i)
-            if slot % 2 == 1:
+            for h in range(BAND_GROUPS):
+                if h // BAND_FRONTS == slot - 1:
+                    band_quantise(h)
+            if slot % 2 == 1 and g < SRC_GROUPS:
                 project(g)
             spread(PAIR * slot + 1)
-            ready_for_vector = for_vector
-            for_vector = []
-            pair = slot - NB
-            if pair >= 0:
-                mixed, row_sum = pairs[pair]
-                if pair >= TILES // PAIR - LAST_ON_VECTOR:
-                    for_vector.append((mixed, PAIR, store_pair(pair)) + statistics(mixed, row_sum, PAIR))
-                else:
-                    finish_on_gpsimd(mixed, row_sum, PAIR, store_pair(pair))
+            layer_norms(slot)
             for i in due:
                 if i % PAIR == 0:
-                    mixed = result.tile([P, PAIR, D], F32, bufs=6, tag="mixed")
+                    mixed = result.tile([P, PAIR, D], F32, tag="mixed")
                     row_sum = small.tile([P, PAIR], F32, tag="row_sum")
                     band_open = (mixed, row_sum)
                 band_add(i, *band_open)
                 if i % PAIR == PAIR - 1 or i == BAND_TILES - 1:
                     n = i % PAIR + 1
-                    on_vector = (i // PAIR) % VECTOR_EVERY == VECTOR_EVERY - 1
-                    summed.append(band_open + (n, band_store(i + 1 - n, n), on_vector))
-            for job in ready_for_vector:
-                finish_on_vector(*job)
-        assert not summed
-        for job in for_vector:
-            finish_on_vector(*job)
+                    hand_over(slot, band_open + (n, band_store(i + 1 - n, n)))
+            if slot > 1:
+                pair = slot - 1 if slot < SLOTS - 1 else 0
+                hand_over(slot, pairs[pair] + (PAIR, store_pair(pair)))
+        for step in range(SLOTS, SLOTS + 3):
+            layer_norms(step)
+            if step == SLOTS:
+                for job in on_vector:
+                    finish_on_vector(*job)

@@ -41,16 +41,17 @@ V_BANKS = 3
 SLOTS = len(SOURCES) // PAIR
 FIRST_BAND_SLOT = 3
 LAST_BAND_SLOT = 19
-SHARED = 5
-MIXED_BUFS = 16
+SHARED = 4
+MIXED_BUFS = 14
 LAG = 2
 VECTOR_FROM = 18
 TURN_FROM = 17
 ALPHA = 2
 ALPHA_OF = 5
 FRONT_BUFS = 5
-CODES_BUFS = 2
-BAND_FRONTS = 2
+CODES_BUFS = 5
+BAND_FRONTS = 1
+SRC_LATE = 3
 
 FLOPS = 2 * ROWS * D * D
 
@@ -63,8 +64,12 @@ def project_slot(i):
     return FIRST_BAND_SLOT - 1 if i < AHEAD else band_slot(i - AHEAD)
 
 
-def quantise_slot(g):
-    return 2 * g - 3
+def front_slot(g):
+    return min(2 * g - 4, max(0, g - SRC_LATE))
+
+
+def band_front_slot(h):
+    return h // BAND_FRONTS
 
 
 def tile_crosssliceattention_pb_t_kernel(tc, x, Wv_words, Wv_scales, bv, attn_band, gamma, beta, out):
@@ -194,9 +199,10 @@ def tile_crosssliceattention_pb_t_kernel(tc, x, Wv_words, Wv_scales, bv, attn_ba
         v_band = [const.tile([P, D], F32, name="v_band%d" % k) for k in range(V_BUFS)]
         for k in range(V_BUFS):
             gpsimd_copy(v_band[k][96:P, :], bv_stage[96:P, :])
-        for i in range(8, 16):
-            load_band(i)
         load_src(4)
+        for i in range(8, 12):
+            load_band(i)
+        load_src(5)
         band_t = const.tile([P, BAND_TILES, P], F32)
         whole = BAND_TILES - 1
         for i0, i1 in ((0, GROUP), (GROUP, BAND_TILES)):
@@ -207,8 +213,10 @@ def tile_crosssliceattention_pb_t_kernel(tc, x, Wv_words, Wv_scales, bv, attn_ba
                     in_=scratch[start : start + P * WIDTH].rearrange("(c w) -> c w", w=WIDTH)[:, 0:P],
                 )
             if i0 == 0:
-                for i in range(16, BAND_TILES):
-                    load_band(i)
+                for g in range(6, 8):
+                    for i in range(4 * g - 12, 4 * g - 8):
+                        load_band(i)
+                    load_src(g)
             i1 = min(i1, whole)
             nc.sync.dma_start(
                 out=band_t[P - 1 : P, i0:i1, NB : NB + BAND_STEP],
@@ -220,7 +228,9 @@ def tile_crosssliceattention_pb_t_kernel(tc, x, Wv_words, Wv_scales, bv, attn_ba
             out=band_t[P - 1 : P, whole, NB : NB + BAND_ROWS - whole * BAND_STEP],
             in_=scratch[SUMS_AT + whole * BAND_STEP : SUMS_AT + BAND_ROWS].rearrange("(o m) -> o m", o=1),
         )
-        for g in range(5, SRC_GROUPS):
+        for i in range(20, BAND_TILES):
+            load_band(i)
+        for g in range(8, SRC_GROUPS):
             load_src(g)
 
         def transpose_tiles(sources, grouped_words, vector_helps=False):
@@ -401,6 +411,7 @@ def tile_crosssliceattention_pb_t_kernel(tc, x, Wv_words, Wv_scales, bv, attn_ba
             nc.gpsimd.tensor_add(out=normed[:, 0:n, :], in0=normed[:, 0:n, :], in1=beta_pair[:, 0:n, :])
             store(normed)
 
+        columns = const.tile([P, 2, D], BF16)
         affine_col = const.tile([P, 2, CHUNKS], F32)
 
         def fill_affine():
@@ -408,7 +419,17 @@ def tile_crosssliceattention_pb_t_kernel(tc, x, Wv_words, Wv_scales, bv, attn_ba
             for i, rows in enumerate((gamma_pair, beta_pair)):
                 for c in range(CHUNKS):
                     nc.tensor.transpose(turned[:, i, P * c : P * (c + 1)], rows[:, 0, P * c : P * (c + 1)], ident_bf[:])
-            nc.scalar.copy(out=affine_col[:], in_=turned[:].rearrange("n i (c p) -> n i c p", c=CHUNKS)[:, :, :, 0])
+            nc.scalar.copy(out=columns[:], in_=turned[:])
+            nc.scalar.copy(out=affine_col[:], in_=columns[:].rearrange("n i (c p) -> n i c p", c=CHUNKS)[:, :, :, 0])
+
+        affine = []
+
+        def affine_rows():
+            bank = psum_front.tile([P, 2, D], BF16, tag="front")
+            for i in range(2):
+                for c in range(CHUNKS):
+                    nc.tensor.transpose(bank[:, i, P * c : P * (c + 1)], columns[:, i, P * c : P * (c + 1)], ident_bf[:])
+            affine.append(bank)
 
         thirds = []
         turned = []
@@ -450,7 +471,7 @@ def tile_crosssliceattention_pb_t_kernel(tc, x, Wv_words, Wv_scales, bv, attn_ba
                     out=mixed[:, e, :],
                     in0=mixed[:, e, :],
                     scalar=neg_mean[:, e : e + 1],
-                    in1=gamma_pair[:, e, :],
+                    in1=affine[0][:, 0, :],
                     op0=ALU.add,
                     op1=ALU.mult,
                 )
@@ -459,7 +480,7 @@ def tile_crosssliceattention_pb_t_kernel(tc, x, Wv_words, Wv_scales, bv, attn_ba
                     out=mixed[:, e, :],
                     in0=mixed[:, e, :],
                     scalar=rstd[:, e : e + 1],
-                    in1=beta_pair[:, e, :],
+                    in1=affine[0][:, 1, :],
                     op0=ALU.mult,
                     op1=ALU.add,
                 )
@@ -564,20 +585,24 @@ def tile_crosssliceattention_pb_t_kernel(tc, x, Wv_words, Wv_scales, bv, attn_ba
             for i in range(BAND_TILES):
                 if project_slot(i) == slot:
                     band_project(i)
-            if slot % 2 == 0 and 0 < slot and slot // 2 + 2 < SRC_GROUPS:
-                front(slot // 2 + 2)
+            for g in range(3, SRC_GROUPS):
+                if front_slot(g) == slot:
+                    front(g)
             for h in range(BAND_GROUPS):
-                if h // BAND_FRONTS == slot:
+                if band_front_slot(h) == slot:
                     band_front(h)
             if slot == 1:
                 fill_affine()
+            if slot == SLOTS - 1:
+                affine_rows()
             spread(PAIR * slot)
-            g = (slot + 3) // 2
-            if slot % 2 == 1 and g < SRC_GROUPS:
-                quantise(g)
+            for g in range(2, SRC_GROUPS):
+                if front_slot(g) + 1 == slot:
+                    quantise(g)
             for h in range(BAND_GROUPS):
-                if h // BAND_FRONTS == slot - 1:
+                if band_front_slot(h) + 1 == slot:
                     band_quantise(h)
+            g = (slot + 3) // 2
             if slot % 2 == 1 and g < SRC_GROUPS:
                 project(g)
             spread(PAIR * slot + 1)

@@ -39,19 +39,19 @@ SRC_GROUPS = TILES // GROUP
 SOURCES = list(range(TILES + NB)) + list(range(-NB, 0))
 V_BANKS = 3
 SLOTS = len(SOURCES) // PAIR
-FIRST_BAND_SLOT = 3
-LAST_BAND_SLOT = 19
+FIRST_BAND_SLOT = 4
+LAST_BAND_SLOT = 20
 SHARED = 4
 MIXED_BUFS = 14
 LAG = 2
+STORE_LAG = 2
 VECTOR_FROM = 18
-TURN_FROM = 17
-ALPHA = 2
-ALPHA_OF = 5
+TURN_FROM = 15
+LATE = (1,)
 FRONT_BUFS = 5
 CODES_BUFS = 5
 BAND_FRONTS = 1
-SRC_LATE = 3
+SRC_LATE = 2
 
 FLOPS = 2 * ROWS * D * D
 
@@ -142,7 +142,6 @@ def tile_crosssliceattention_pb_t_kernel(tc, x, Wv_words, Wv_scales, bv, attn_ba
         with nc.allow_non_contiguous_dma(reason="512 bias values, one to a partition for each chunk of n"):
             nc.sync.dma_start(out=bv_bf[:], in_=bv.rearrange("(c n) -> n c", n=P))
         bv_col = const.tile([P, CHUNKS], F32)
-        nc.scalar.copy(out=bv_col[:], in_=bv_bf[:])
         load_src(1)
         band_bf = const.tile([P, TILES * TAPS], BF16)
         nc.sync.dma_start(out=band_bf[:], in_=band_rows)
@@ -243,7 +242,7 @@ def tile_crosssliceattention_pb_t_kernel(tc, x, Wv_words, Wv_scales, bv, attn_ba
                     for u in range(2):
                         col = (2 * i + u) * P
                         nc.tensor.transpose(planes[:, col : col + P], words[:, u : D // 2 : 2], ident[:])
-                copy = nc.vector.tensor_copy if vector_helps and first > 0 else nc.scalar.copy
+                copy = nc.vector.tensor_copy if vector_helps else nc.scalar.copy
                 copy(
                     out=grouped_words[:, first * 2 * P : (first + n) * 2 * P].rearrange(
                         "q (i p u) -> q i p u", i=n, u=2
@@ -256,10 +255,67 @@ def tile_crosssliceattention_pb_t_kernel(tc, x, Wv_words, Wv_scales, bv, attn_ba
         band_codes = const.tile([P, BAND_TILES * P], U32, align_bytes=64)
         band_scales = const.tile([P, BAND_TILES * P], U8, align_bytes=64)
 
-        def front(g, vector_helps=False):
+        projected = {}
+
+        def front(g):
             columns = stage.tile([P, GROUP * P * 4], BF16, align_bytes=64, bufs=4, tag="grouped")
             grouped[g] = columns
-            transpose_tiles([x_src[g][:, i, :] for i in range(GROUP)], columns[:].bitcast(F32), vector_helps)
+            transpose_tiles([x_src[g][:, i, :] for i in range(GROUP)], columns[:].bitcast(F32))
+
+        def begin_first_group():
+            columns = stage.tile([P, GROUP * P * 4], BF16, align_bytes=64, bufs=4, tag="grouped")
+            codes = stage.tile([P, GROUP * P], U32, align_bytes=64, bufs=CODES_BUFS, tag="codes")
+            scales = stage.tile([P, GROUP * P], U8, align_bytes=64, bufs=CODES_BUFS, tag="scales")
+            words = columns[:].bitcast(F32)
+
+            def quantise_half(h):
+                lo, hi = h * PAIR * P, (h + 1) * PAIR * P
+                nc.vector.quantize_mx(
+                    out=codes[:, lo:hi].bitcast(FP8X4), scales=scales[:, lo:hi], in_=columns[:, 4 * lo : 4 * hi]
+                )
+
+            def project_half(h):
+                lo, hi = h * PAIR * P, (h + 1) * PAIR * P
+                for c in range(CHUNKS):
+                    product = psum_front.tile([P, PAIR * P], F32, tag="front")
+                    nc.tensor.matmul_mx(
+                        out=product[:],
+                        lhsT=w_words[:, 2 * P * c : 2 * P * (c + 1)].bitcast(FP4X4),
+                        lhsT_scale=w_scales[:, P * c : P * (c + 1)],
+                        rhs=codes[:, lo:hi].bitcast(FP8X4),
+                        rhs_scale=scales[:, lo:hi],
+                        start=True,
+                        stop=True,
+                    )
+                    if h == 0 and c % 2 == 1:
+                        nc.vector.tensor_scalar(
+                            out=v_first[:, c, lo:hi],
+                            in0=product[:],
+                            scalar1=bv_col[:, c : c + 1],
+                            scalar2=None,
+                            op0=ALU.add,
+                        )
+                    else:
+                        nc.scalar.activation(
+                            out=v_first[:, c, lo:hi],
+                            in_=product[:],
+                            func=ACT.Identity,
+                            bias=bv_col[:, c : c + 1],
+                            scale=1.0,
+                        )
+
+            v_first = const.tile([P, CHUNKS, GROUP * P], F32)
+            projected[0] = v_first
+            transpose_tiles([x_src[0][:, i, :] for i in range(PAIR)], words[:, 0 : PAIR * 2 * P])
+            nc.scalar.copy(out=bv_col[:], in_=bv_bf[:])
+            quantise_half(0)
+            transpose_tiles([x_src[0][:, i, :] for i in range(PAIR, GROUP)], words[:, PAIR * 2 * P :], True)
+            quantise_half(1)
+            project_half(0)
+            for position in range(PAIR):
+                restore(position)
+            nc.scalar.copy(out=band[:], in_=band_bf[:])
+            project_half(1)
 
         def quantise(g):
             codes = stage.tile([P, GROUP * P], U32, align_bytes=64, bufs=CODES_BUFS, tag="codes")
@@ -279,15 +335,11 @@ def tile_crosssliceattention_pb_t_kernel(tc, x, Wv_words, Wv_scales, bv, attn_ba
                 out=band_codes[:, lo:hi].bitcast(FP8X4), scales=band_scales[:, lo:hi], in_=grouped[-1 - h]
             )
 
-        projected = {}
         v_src = {}
 
-        def project(g, vector_helps=False):
+        def project(g):
             codes, scales = quantised[g]
-            if g == 0:
-                v_by_feature = const.tile([P, CHUNKS, GROUP * P], F32, name="v_by_feature_0")
-            else:
-                v_by_feature = stage.tile([P, CHUNKS, GROUP * P], F32, tag="v_by_feature")
+            v_by_feature = stage.tile([P, CHUNKS, GROUP * P], F32, tag="v_by_feature")
             for c in range(CHUNKS):
                 product = psum_front.tile([P, GROUP * P], F32, tag="front")
                 nc.tensor.matmul_mx(
@@ -299,18 +351,13 @@ def tile_crosssliceattention_pb_t_kernel(tc, x, Wv_words, Wv_scales, bv, attn_ba
                     start=True,
                     stop=True,
                 )
-                if vector_helps and c % 2 == 1:
-                    nc.vector.tensor_scalar(
-                        out=v_by_feature[:, c, :], in0=product[:], scalar1=bv_col[:, c : c + 1], scalar2=None, op0=ALU.add
-                    )
-                else:
-                    nc.scalar.activation(
-                        out=v_by_feature[:, c, :],
-                        in_=product[:],
-                        func=ACT.Identity,
-                        bias=bv_col[:, c : c + 1],
-                        scale=1.0,
-                    )
+                nc.scalar.activation(
+                    out=v_by_feature[:, c, :],
+                    in_=product[:],
+                    func=ACT.Identity,
+                    bias=bv_col[:, c : c + 1],
+                    scale=1.0,
+                )
             projected[g] = v_by_feature
 
         def restore(position):
@@ -360,8 +407,9 @@ def tile_crosssliceattention_pb_t_kernel(tc, x, Wv_words, Wv_scales, bv, attn_ba
             restore(position + V_BANKS)
 
         def store_pair(pair):
-            def store(normed):
-                nc.sync.dma_start(out=out_rows[:, PAIR * pair : PAIR * (pair + 1), :], in_=normed[:])
+            def store(normed, e=None):
+                lo, hi = (0, PAIR) if e is None else (e, e + 1)
+                nc.sync.dma_start(out=out_rows[:, PAIR * pair + lo : PAIR * pair + hi, :], in_=normed[:, lo:hi, :])
 
             return store
 
@@ -409,7 +457,6 @@ def tile_crosssliceattention_pb_t_kernel(tc, x, Wv_words, Wv_scales, bv, attn_ba
         def finish_on_gpsimd(normed, n, store):
             nc.gpsimd.tensor_mul(out=normed[:, 0:n, :], in0=normed[:, 0:n, :], in1=gamma_pair[:, 0:n, :])
             nc.gpsimd.tensor_add(out=normed[:, 0:n, :], in0=normed[:, 0:n, :], in1=beta_pair[:, 0:n, :])
-            store(normed)
 
         columns = const.tile([P, 2, D], BF16)
         affine_col = const.tile([P, 2, CHUNKS], F32)
@@ -465,7 +512,7 @@ def tile_crosssliceattention_pb_t_kernel(tc, x, Wv_words, Wv_scales, bv, attn_ba
                 nc.scalar.copy(out=normed[:, e, :], in_=bank[:])
             store(normed)
 
-        def finish_on_vector(mixed, neg_mean, rstd, n, store):
+        def finish_on_vector(mixed, neg_mean, rstd, n, store, by_tile):
             for e in range(n):
                 nc.vector.scalar_tensor_tensor(
                     out=mixed[:, e, :],
@@ -484,7 +531,10 @@ def tile_crosssliceattention_pb_t_kernel(tc, x, Wv_words, Wv_scales, bv, attn_ba
                     op0=ALU.mult,
                     op1=ALU.add,
                 )
-            store(mixed)
+                if by_tile:
+                    store(mixed, e)
+            if not by_tile:
+                store(mixed)
 
         def band_project(i):
             product = psum_front.tile([P, D], F32, tag="front")
@@ -528,35 +578,32 @@ def tile_crosssliceattention_pb_t_kernel(tc, x, Wv_words, Wv_scales, bv, attn_ba
 
             return store
 
-        front(0, True)
-        quantise(0)
-        front(1, True)
-        project(0, True)
-        quantise(1)
-        nc.scalar.copy(out=band[:], in_=band_bf[:])
-        for s in range(V_BANKS):
-            restore(s)
-        project(1)
-        front(2)
+        begin_first_group()
+        front(1)
+        for position in range(PAIR, V_BANKS):
+            restore(position)
 
         band_open = None
         summed = []
         to_turn = {}
         to_turn_back = {}
+        to_store = {}
         on_vector = []
-        order = []
+        late = []
 
         def hand_over(slot, job):
-            order.append(job)
             if slot >= VECTOR_FROM:
-                how = "vector"
-            elif slot >= TURN_FROM or len(order) % ALPHA_OF >= ALPHA:
+                late.append(job)
+                how = "gpsimd" if len(late) in LATE else "vector"
+            elif slot >= TURN_FROM or job[4] == "vector":
                 how = "turn"
             else:
                 how = "gpsimd"
-            summed.append((how,) + job)
+            summed.append((how,) + job[0:4])
 
         def layer_norms(step):
+            for normed, n, store in to_store.get(step, []):
+                store(normed)
             for job in to_turn_back.get(step, []):
                 turn_back(*job)
             to_turn_back[step + 1] = [turn(*job) for job in to_turn.get(step, [])]
@@ -577,6 +624,15 @@ def tile_crosssliceattention_pb_t_kernel(tc, x, Wv_words, Wv_scales, bv, attn_ba
             summed.clear()
             for job in on_gpsimd:
                 finish_on_gpsimd(*job)
+            to_store[step + STORE_LAG] = on_gpsimd
+
+        def fronts(slot):
+            for g in range(2, SRC_GROUPS):
+                if front_slot(g) == slot:
+                    front(g)
+            for h in range(BAND_GROUPS):
+                if band_front_slot(h) == slot:
+                    band_front(h)
 
         for slot in range(SLOTS):
             due = [i for i in range(BAND_TILES) if band_slot(i) == slot]
@@ -585,27 +641,32 @@ def tile_crosssliceattention_pb_t_kernel(tc, x, Wv_words, Wv_scales, bv, attn_ba
             for i in range(BAND_TILES):
                 if project_slot(i) == slot:
                     band_project(i)
-            for g in range(3, SRC_GROUPS):
-                if front_slot(g) == slot:
-                    front(g)
-            for h in range(BAND_GROUPS):
-                if band_front_slot(h) == slot:
-                    band_front(h)
+            if slot > 0:
+                fronts(slot)
             if slot == 1:
                 fill_affine()
-            if slot == SLOTS - 1:
+            if slot == VECTOR_FROM:
                 affine_rows()
             spread(PAIR * slot)
-            for g in range(2, SRC_GROUPS):
+            if slot == 0:
+                quantise(1)
+                project(1)
+                fronts(0)
+            if slot == 1:
+                quantise(2)
+            g = (slot + 3) // 2
+            if slot % 2 == 1 and g < SRC_GROUPS:
+                project(g)
+            spread(PAIR * slot + 1)
+            for g in range(3, SRC_GROUPS):
                 if front_slot(g) + 1 == slot:
                     quantise(g)
             for h in range(BAND_GROUPS):
                 if band_front_slot(h) + 1 == slot:
                     band_quantise(h)
-            g = (slot + 3) // 2
-            if slot % 2 == 1 and g < SRC_GROUPS:
-                project(g)
-            spread(PAIR * slot + 1)
+            if slot > 1:
+                pair = slot - 1 if slot < SLOTS - 1 else 0
+                hand_over(slot, pairs[pair] + (PAIR, store_pair(pair), "vector"))
             layer_norms(slot)
             for i in due:
                 if i % PAIR == 0:
@@ -615,12 +676,9 @@ def tile_crosssliceattention_pb_t_kernel(tc, x, Wv_words, Wv_scales, bv, attn_ba
                 band_add(i, *band_open)
                 if i % PAIR == PAIR - 1 or i == BAND_TILES - 1:
                     n = i % PAIR + 1
-                    hand_over(slot, band_open + (n, band_store(i + 1 - n, n)))
-            if slot > 1:
-                pair = slot - 1 if slot < SLOTS - 1 else 0
-                hand_over(slot, pairs[pair] + (PAIR, store_pair(pair)))
+                    hand_over(slot, band_open + (n, band_store(i + 1 - n, n), "band"))
         for step in range(SLOTS, SLOTS + 3):
             layer_norms(step)
             if step == SLOTS:
                 for job in on_vector:
-                    finish_on_vector(*job)
+                    finish_on_vector(*job, by_tile=job is on_vector[-1])

@@ -39,15 +39,17 @@ SRC_GROUPS = TILES // GROUP
 SOURCES = list(range(TILES + NB)) + list(range(-NB, 0))
 V_BANKS = 3
 SLOTS = len(SOURCES) // PAIR
-FIRST_BAND_SLOT = 4
+FIRST_BAND_SLOT = 3
 LAST_BAND_SLOT = 20
 SHARED = 4
 MIXED_BUFS = 14
 LAG = 2
 STORE_LAG = 2
 VECTOR_FROM = 18
-TURN_FROM = 15
+TURN_FROM = 16
 LATE = (1,)
+LATE_TURN = ()
+FINAL = 2
 FRONT_BUFS = 5
 CODES_BUFS = 5
 BAND_FRONTS = 1
@@ -418,19 +420,16 @@ def tile_crosssliceattention_pb_t_kernel(tc, x, Wv_words, Wv_scales, bv, attn_ba
             nc.scalar.mul(out=neg_mean[:, 0:n], in_=row_sum[:, 0:n], mul=-1.0 / D)
             return neg_mean
 
-        def spread_of(mixed, row_sum, n):
-            square_sum = small.tile([P, PAIR], F32, tag="square_sum")
-            for e in range(n):
-                squares = small.tile([P, D], BF16, tag="squares", bufs=4)
-                nc.scalar.activation(
-                    out=squares[:],
-                    in_=mixed[:, e, :],
-                    func=ACT.Square,
-                    bias=row_sum[:, e : e + 1],
-                    scale=-float(D),
-                    accum_out=square_sum[:, e : e + 1],
-                )
-            return square_sum
+        def square(mixed, row_sum, square_sum, e):
+            squares = small.tile([P, D], BF16, tag="squares", bufs=4)
+            nc.scalar.activation(
+                out=squares[:],
+                in_=mixed[:, e, :],
+                func=ACT.Square,
+                bias=row_sum[:, e : e + 1],
+                scale=-float(D),
+                accum_out=square_sum[:, e : e + 1],
+            )
 
         def invert(square_sum, n):
             rstd = small.tile([P, PAIR], F32, tag="rstd")
@@ -504,12 +503,13 @@ def tile_crosssliceattention_pb_t_kernel(tc, x, Wv_words, Wv_scales, bv, attn_ba
                     )
             return half, normed, n, store
 
-        def turn_back(half, normed, n, store):
+        def turn_back(half, normed, n, store, between):
             for e in range(n):
                 bank = psum_front.tile([P, D], F32, tag="front")
                 for c in range(CHUNKS):
                     nc.tensor.transpose(bank[:, P * c : P * (c + 1)], half[:, c, P * e : P * (e + 1)], ident[:])
                 nc.scalar.copy(out=normed[:, e, :], in_=bank[:])
+                between()
             store(normed)
 
         def finish_on_vector(mixed, neg_mean, rstd, n, store, by_tile):
@@ -594,7 +594,7 @@ def tile_crosssliceattention_pb_t_kernel(tc, x, Wv_words, Wv_scales, bv, attn_ba
         def hand_over(slot, job):
             if slot >= VECTOR_FROM:
                 late.append(job)
-                how = "gpsimd" if len(late) in LATE else "vector"
+                how = "gpsimd" if len(late) in LATE else ("turn" if len(late) in LATE_TURN else "vector")
             elif slot >= TURN_FROM or job[4] == "vector":
                 how = "turn"
             else:
@@ -604,27 +604,42 @@ def tile_crosssliceattention_pb_t_kernel(tc, x, Wv_words, Wv_scales, bv, attn_ba
         def layer_norms(step):
             for normed, n, store in to_store.get(step, []):
                 store(normed)
-            for job in to_turn_back.get(step, []):
-                turn_back(*job)
-            to_turn_back[step + 1] = [turn(*job) for job in to_turn.get(step, [])]
             on_gpsimd = []
             to_turn[step + LAG] = []
-            for how, mixed, row_sum, n, store in summed:
-                square_sum = spread_of(mixed, row_sum, n)
-                neg_mean = centre(row_sum, n)
+            late_rstd = []
+
+            def conclude(job):
+                how, mixed, neg_mean, square_sum, n, store = job
                 rstd = invert(square_sum, n)
                 if how == "vector":
                     on_vector.append((mixed, neg_mean, rstd, n, store))
-                    continue
+                    return
                 normalise(mixed, neg_mean, rstd, n)
                 if how == "gpsimd":
                     on_gpsimd.append((mixed, n, store))
                 else:
                     to_turn[step + LAG].append((mixed, n, store))
+
+            def conclude_waiting():
+                for job in late_rstd:
+                    conclude(job)
+                late_rstd.clear()
+
+            for how, mixed, row_sum, n, store in summed:
+                square_sum = small.tile([P, PAIR], F32, tag="square_sum")
+                for e in range(n):
+                    square(mixed, row_sum, square_sum, e)
+                    conclude_waiting()
+                late_rstd.append((how, mixed, centre(row_sum, n), square_sum, n, store))
             summed.clear()
+            for job in to_turn_back.get(step, []):
+                turn_back(*job, between=conclude_waiting)
+            conclude_waiting()
+            to_turn_back[step + 1] = [turn(*job) for job in to_turn.get(step, [])]
             for job in on_gpsimd:
                 finish_on_gpsimd(*job)
-            to_store[step + STORE_LAG] = on_gpsimd
+            when = step + STORE_LAG if step < VECTOR_FROM else SLOTS + 2
+            to_store[when] = to_store.get(when, []) + on_gpsimd
 
         def fronts(slot):
             for g in range(2, SRC_GROUPS):
@@ -677,8 +692,10 @@ def tile_crosssliceattention_pb_t_kernel(tc, x, Wv_words, Wv_scales, bv, attn_ba
                 if i % PAIR == PAIR - 1 or i == BAND_TILES - 1:
                     n = i % PAIR + 1
                     hand_over(slot, band_open + (n, band_store(i + 1 - n, n), "band"))
-        for step in range(SLOTS, SLOTS + 3):
+        layer_norms(SLOTS)
+        for job in on_vector[:-FINAL]:
+            finish_on_vector(*job, by_tile=False)
+        for step in range(SLOTS + 1, SLOTS + 3):
             layer_norms(step)
-            if step == SLOTS:
-                for job in on_vector:
-                    finish_on_vector(*job, by_tile=job is on_vector[-1])
+        for job in on_vector[-FINAL:]:
+            finish_on_vector(*job, by_tile=job is on_vector[-1])

import concourse.mybir as mybir
from concourse.masks import make_identity

F32 = mybir.dt.float32
BF16 = mybir.dt.bfloat16
I32 = mybir.dt.int32
U32 = mybir.dt.uint32
U8 = mybir.dt.uint8
FP8X4 = mybir.dt.float8_e4m3fn_x4
FP4X4 = mybir.dt.float4_e2m1fn_x4
ACT = mybir.ActivationFunctionType
ALU = mybir.AluOpType

P = 128
D = 512
ROWS = 32 * 256
NB = 2
TAPS = 2 * NB + 1
GROUP = 4
PAIR = 2
CHUNKS = D // P
LN_EPS = 1e-5

BAND_TILES = 25
BAND_GROUPS = (BAND_TILES + GROUP - 1) // GROUP
BAND_STEP = P - 2 * NB - 1
BAND_ROWS = 24 * P
COEF = BAND_ROWS // P
PITCH = 136
WIDTH = PITCH - 1
SCRATCH_ROWS = 832
SUMS_AT = 820 * D
TAIL = 8
AHEAD = 2
V_BUFS = 2 * AHEAD

TILES = (ROWS - BAND_ROWS) // P
SRC_GROUPS = TILES // GROUP
SOURCES = list(range(TILES + NB)) + list(range(-NB, 0))
V_BANKS = 3
SLOTS = len(SOURCES) // PAIR
FIRST_BAND_SLOT = 3
LAST_BAND_SLOT = 20
SHARED = 4
MIXED_BUFS = 14
LAG = 2
STORE_LAG = 2
VECTOR_FROM = 18
TURN_FROM = 16
LATE = (1,)
LATE_TURN = ()
FINAL = 2
FRONT_BUFS = 5
CODES_BUFS = 5
BAND_FRONTS = 1
SRC_LATE = 2

FLOPS = 2 * ROWS * D * D


def band_slot(i):
    return FIRST_BAND_SLOT + i * (LAST_BAND_SLOT - FIRST_BAND_SLOT + 1) // BAND_TILES


def project_slot(i):
    return FIRST_BAND_SLOT - 1 if i < AHEAD else band_slot(i - AHEAD)


def front_slot(g):
    return min(2 * g - 4, max(0, g - SRC_LATE))


def band_front_slot(h):
    return h // BAND_FRONTS


def tile_crosssliceattention_pb_t_kernel(tc, x, Wv_words, Wv_scales, bv, attn_band, gamma, beta, out):
    nc = tc.nc
    x_all = x.flatten_outer_dims()
    out_all = out.flatten_outer_dims()
    band_all = attn_band.flatten_outer_dims()
    x_rows = x_all[BAND_ROWS:ROWS, :].rearrange("(p t) d -> p t d", t=TILES)
    out_rows = out_all[BAND_ROWS:ROWS, :].rearrange("(p t) d -> p t d", t=TILES)
    band_rows = band_all[BAND_ROWS:ROWS, :].rearrange("(p t) j -> p (t j)", t=TILES)
    scratch = out_all[BAND_ROWS - SCRATCH_ROWS : BAND_ROWS, :].rearrange("r d -> (r d)")

    with (
        tc.tile_pool(name="const", bufs=1) as const,
        tc.tile_pool(name="stage", bufs=2) as stage,
        tc.tile_pool(name="result", bufs=MIXED_BUFS) as result,
        tc.tile_pool(name="small", bufs=8) as small,
        tc.psum_pool(name="psum_front", bufs=FRONT_BUFS) as psum_front,
        tc.psum_pool(name="psum_v", bufs=V_BANKS) as psum_v,
        tc.manual_schedule(),
    ):
        ident = const.tile([P, P], F32)
        make_identity(nc, ident[:])
        ident_bf = const.tile([P, P], BF16)
        make_identity(nc, ident_bf[:])
        w_words = const.tile([P, 2 * D], U8, align_bytes=64)
        w_scales = const.tile([P, D], U8, align_bytes=64)
        nc.vector.memset(w_scales[:].bitcast(I32), 0)
        weights = stage.tile([P, COEF, PITCH], F32, tag="weights", bufs=1)
        nc.vector.memset(weights[:], 0.0)
        eps_col = const.tile([P, 1], F32)
        nc.vector.memset(eps_col[:], LN_EPS)
        zero = const.tile([TAIL, PITCH], F32)
        nc.vector.memset(zero[:], 0.0)
        coef_before = const.tile([P, NB, TAPS], BF16)
        nc.gpsimd.memset(coef_before[:], 0.0)

        x_src = []
        for g in range(SRC_GROUPS):
            if g < SHARED:
                early_tile = result.tile([P, GROUP, D], BF16, tag="mixed")
                x_src.append(early_tile)
            else:
                late_tile = const.tile([P, GROUP, D], BF16, name="x_src%d" % g)
                x_src.append(late_tile)
        x_band = [const.tile([P, D], BF16, name="x_band%d" % i) for i in range(BAND_TILES)]
        nc.vector.memset(x_band[0][0:NB, :], 0.0)

        def gpsimd_copy(target, source):
            nc.gpsimd.tensor_scalar(out=target, in0=source, scalar1=1.0, scalar2=0.0, op0=ALU.mult, op1=ALU.add)

        def load_src(g):
            nc.sync.dma_start(out=x_src[g][:], in_=x_rows[:, GROUP * g : GROUP * (g + 1), :])

        def load_band(i):
            if i == 0:
                nc.sync.dma_start(out=x_band[0][NB:P, :], in_=x_all[0 : P - NB, :])
            else:
                nc.sync.dma_start(out=x_band[i][:], in_=x_all[BAND_STEP * i - NB : BAND_STEP * i - NB + P, :])

        nc.sync.dma_start(out=x_src[0][:, 0:PAIR, :], in_=x_rows[:, 0:PAIR, :])
        nc.sync.dma_start(out=x_src[0][:, PAIR:GROUP, :], in_=x_rows[:, PAIR:GROUP, :])
        nc.sync.dma_start(out=w_words[:].bitcast(I32), in_=Wv_words[0].bitcast(I32))
        for quadrant in range(4):
            nc.sync.dma_start(
                out=w_scales[32 * quadrant : 32 * quadrant + 4, :].bitcast(I32),
                in_=Wv_scales[0, 4 * quadrant : 4 * quadrant + 4, :].bitcast(I32),
            )
        bv_bf = const.tile([P, CHUNKS], BF16)
        with nc.allow_non_contiguous_dma(reason="512 bias values, one to a partition for each chunk of n"):
            nc.sync.dma_start(out=bv_bf[:], in_=bv.rearrange("(c n) -> n c", n=P))
        bv_col = const.tile([P, CHUNKS], F32)
        load_src(1)
        band_bf = const.tile([P, TILES * TAPS], BF16)
        nc.sync.dma_start(out=band_bf[:], in_=band_rows)
        band = const.tile([P, TILES * TAPS], F32)

        coef_main = const.tile([P, COEF, TAPS], BF16)
        coef_after = const.tile([P, NB, TAPS], BF16)
        nc.sync.dma_start(out=coef_main[:], in_=band_all[0:BAND_ROWS, :].rearrange("(p l) j -> p l j", l=COEF))
        before = band_all[COEF - NB : COEF - NB + COEF * (P - 1), :].rearrange("(p l) j -> p l j", l=COEF)
        for lo, hi in ((1, 65), (65, P)):
            nc.sync.dma_start(out=coef_before[lo:hi, :, :], in_=before[lo - 1 : hi - 1, 0:NB, :])
        nc.sync.dma_start(
            out=coef_after[:],
            in_=band_all[COEF : COEF + BAND_ROWS, :].rearrange("(p l) j -> p l j", l=COEF)[:, 0:NB, :],
        )
        nc.sync.dma_start(out=scratch[0 : NB * PITCH].rearrange("(o z) -> o z", o=NB), in_=zero[0:NB, :])
        nc.sync.dma_start(
            out=scratch[(NB + BAND_ROWS) * PITCH : (NB + BAND_ROWS + TAIL) * PITCH].rearrange("(o z) -> o z", o=TAIL),
            in_=zero[:],
        )
        load_src(2)
        gamma_pair = const.tile([P, PAIR, D], BF16)
        nc.sync.dma_start(out=gamma_pair[:, 0, :], in_=gamma.partition_broadcast(P))
        beta_pair = const.tile([P, PAIR, D], BF16)
        nc.sync.dma_start(out=beta_pair[:, 0, :], in_=beta.partition_broadcast(P))
        for i in range(8):
            load_band(i)
        load_src(3)

        coef = const.tile([P, COEF + 2 * NB, TAPS], F32)
        nc.gpsimd.tensor_copy(out=coef[:, NB : NB + COEF, :], in_=coef_main[:])
        nc.gpsimd.tensor_copy(out=coef[:, 0:NB, :], in_=coef_before[:])
        nc.gpsimd.tensor_copy(out=coef[:, NB + COEF : 2 * NB + COEF, :], in_=coef_after[:])
        for i in range(TAPS):
            nc.gpsimd.tensor_copy(out=weights[:, :, i], in_=coef[:, i : i + COEF, TAPS - 1 - i])
        weight_sum = const.tile([P, COEF], F32)
        nc.gpsimd.tensor_tensor(
            out=weight_sum[:], in0=coef[:, NB : NB + COEF, 0], in1=coef[:, NB : NB + COEF, 1], op=ALU.add
        )
        for j in range(2, TAPS):
            nc.gpsimd.tensor_tensor(out=weight_sum[:], in0=weight_sum[:], in1=coef[:, NB : NB + COEF, j], op=ALU.add)
        for rows in (gamma_pair, beta_pair):
            gpsimd_copy(rows[:, 1, :], rows[:, 0, :])

        nc.sync.dma_start(
            out=scratch[NB * PITCH : (NB + BAND_ROWS) * PITCH].rearrange("(p l w) -> p l w", l=COEF, w=PITCH),
            in_=weights[:],
        )
        nc.sync.dma_start(
            out=scratch[SUMS_AT : SUMS_AT + BAND_ROWS].rearrange("(p l) -> p l", l=COEF), in_=weight_sum[:]
        )
        bv_stage = const.tile([P, D], BF16)
        nc.sync.dma_start(out=bv_stage[96:P, :], in_=bv.partition_broadcast(32))
        v_band = [const.tile([P, D], F32, name="v_band%d" % k) for k in range(V_BUFS)]
        for k in range(V_BUFS):
            gpsimd_copy(v_band[k][96:P, :], bv_stage[96:P, :])
        load_src(4)
        for i in range(8, 12):
            load_band(i)
        load_src(5)
        band_t = const.tile([P, BAND_TILES, P], F32)
        whole = BAND_TILES - 1
        for i0, i1 in ((0, GROUP), (GROUP, BAND_TILES)):
            for i in range(i0, i1):
                start = BAND_STEP * i * PITCH + NB
                nc.sync.dma_start(
                    out=band_t[:, i, :],
                    in_=scratch[start : start + P * WIDTH].rearrange("(c w) -> c w", w=WIDTH)[:, 0:P],
                )
            if i0 == 0:
                for g in range(6, 8):
                    for i in range(4 * g - 12, 4 * g - 8):
                        load_band(i)
                    load_src(g)
            i1 = min(i1, whole)
            nc.sync.dma_start(
                out=band_t[P - 1 : P, i0:i1, NB : NB + BAND_STEP],
                in_=scratch[SUMS_AT + i0 * BAND_STEP : SUMS_AT + i1 * BAND_STEP].rearrange(
                    "(o i m) -> o i m", o=1, m=BAND_STEP
                ),
            )
        nc.sync.dma_start(
            out=band_t[P - 1 : P, whole, NB : NB + BAND_ROWS - whole * BAND_STEP],
            in_=scratch[SUMS_AT + whole * BAND_STEP : SUMS_AT + BAND_ROWS].rearrange("(o m) -> o m", o=1),
        )
        for i in range(20, BAND_TILES):
            load_band(i)
        for g in range(8, SRC_GROUPS):
            load_src(g)

        def transpose_tiles(sources, grouped_words, vector_helps=False):
            for first in range(0, len(sources), 2):
                some = sources[first : first + 2]
                n = len(some)
                planes = psum_front.tile([P, D], F32, tag="front")
                for i in range(n):
                    words = some[i].bitcast(F32)
                    for u in range(2):
                        col = (2 * i + u) * P
                        nc.tensor.transpose(planes[:, col : col + P], words[:, u : D // 2 : 2], ident[:])
                copy = nc.vector.tensor_copy if vector_helps else nc.scalar.copy
                copy(
                    out=grouped_words[:, first * 2 * P : (first + n) * 2 * P].rearrange(
                        "q (i p u) -> q i p u", i=n, u=2
                    ),
                    in_=planes[:, 0 : n * 2 * P].rearrange("q (i u p) -> q i p u", i=n, u=2),
                )

        grouped = {}
        quantised = {}
        band_codes = const.tile([P, BAND_TILES * P], U32, align_bytes=64)
        band_scales = const.tile([P, BAND_TILES * P], U8, align_bytes=64)

        projected = {}

        def front(g):
            columns = stage.tile([P, GROUP * P * 4], BF16, align_bytes=64, bufs=4, tag="grouped")
            grouped[g] = columns
            transpose_tiles([x_src[g][:, i, :] for i in range(GROUP)], columns[:].bitcast(F32))

        def begin_first_group():
            columns = stage.tile([P, GROUP * P * 4], BF16, align_bytes=64, bufs=4, tag="grouped")
            codes = stage.tile([P, GROUP * P], U32, align_bytes=64, bufs=CODES_BUFS, tag="codes")
            scales = stage.tile([P, GROUP * P], U8, align_bytes=64, bufs=CODES_BUFS, tag="scales")
            words = columns[:].bitcast(F32)

            def quantise_half(h):
                lo, hi = h * PAIR * P, (h + 1) * PAIR * P
                nc.vector.quantize_mx(
                    out=codes[:, lo:hi].bitcast(FP8X4), scales=scales[:, lo:hi], in_=columns[:, 4 * lo : 4 * hi]
                )

            def project_half(h):
                lo, hi = h * PAIR * P, (h + 1) * PAIR * P
                for c in range(CHUNKS):
                    product = psum_front.tile([P, PAIR * P], F32, tag="front")
                    nc.tensor.matmul_mx(
                        out=product[:],
                        lhsT=w_words[:, 2 * P * c : 2 * P * (c + 1)].bitcast(FP4X4),
                        lhsT_scale=w_scales[:, P * c : P * (c + 1)],
                        rhs=codes[:, lo:hi].bitcast(FP8X4),
                        rhs_scale=scales[:, lo:hi],
                        start=True,
                        stop=True,
                    )
                    if h == 0 and c % 2 == 1:
                        nc.vector.tensor_scalar(
                            out=v_first[:, c, lo:hi],
                            in0=product[:],
                            scalar1=bv_col[:, c : c + 1],
                            scalar2=None,
                            op0=ALU.add,
                        )
                    else:
                        nc.scalar.activation(
                            out=v_first[:, c, lo:hi],
                            in_=product[:],
                            func=ACT.Identity,
                            bias=bv_col[:, c : c + 1],
                            scale=1.0,
                        )

            v_first = const.tile([P, CHUNKS, GROUP * P], F32)
            projected[0] = v_first
            transpose_tiles([x_src[0][:, i, :] for i in range(PAIR)], words[:, 0 : PAIR * 2 * P])
            nc.scalar.copy(out=bv_col[:], in_=bv_bf[:])
            quantise_half(0)
            transpose_tiles([x_src[0][:, i, :] for i in range(PAIR, GROUP)], words[:, PAIR * 2 * P :], True)
            quantise_half(1)
            project_half(0)
            for position in range(PAIR):
                restore(position)
            nc.scalar.copy(out=band[:], in_=band_bf[:])
            project_half(1)

        def quantise(g):
            codes = stage.tile([P, GROUP * P], U32, align_bytes=64, bufs=CODES_BUFS, tag="codes")
            scales = stage.tile([P, GROUP * P], U8, align_bytes=64, bufs=CODES_BUFS, tag="scales")
            nc.vector.quantize_mx(out=codes[:].bitcast(FP8X4), scales=scales[:], in_=grouped[g][:])
            quantised[g] = (codes, scales)

        def band_front(h):
            tiles = range(GROUP * h, min(GROUP * (h + 1), BAND_TILES))
            columns = stage.tile([P, GROUP * P * 4], BF16, align_bytes=64, bufs=4, tag="grouped")
            grouped[-1 - h] = columns[:, 0 : len(tiles) * P * 4]
            transpose_tiles([x_band[i][:] for i in tiles], grouped[-1 - h].bitcast(F32))

        def band_quantise(h):
            lo, hi = P * GROUP * h, P * min(GROUP * (h + 1), BAND_TILES)
            nc.vector.quantize_mx(
                out=band_codes[:, lo:hi].bitcast(FP8X4), scales=band_scales[:, lo:hi], in_=grouped[-1 - h]
            )

        v_src = {}

        def project(g):
            codes, scales = quantised[g]
            v_by_feature = stage.tile([P, CHUNKS, GROUP * P], F32, tag="v_by_feature")
            for c in range(CHUNKS):
                product = psum_front.tile([P, GROUP * P], F32, tag="front")
                nc.tensor.matmul_mx(
                    out=product[:],
                    lhsT=w_words[:, 2 * P * c : 2 * P * (c + 1)].bitcast(FP4X4),
                    lhsT_scale=w_scales[:, P * c : P * (c + 1)],
                    rhs=codes[:, 0 : GROUP * P].bitcast(FP8X4),
                    rhs_scale=scales[:, 0 : GROUP * P],
                    start=True,
                    stop=True,
                )
                nc.scalar.activation(
                    out=v_by_feature[:, c, :],
                    in_=product[:],
                    func=ACT.Identity,
                    bias=bv_col[:, c : c + 1],
                    scale=1.0,
                )
            projected[g] = v_by_feature

        def restore(position):
            if position >= len(SOURCES):
                return
            s = SOURCES[position]
            t = s % TILES
            first = P * (t % GROUP) + s // TILES
            v_rows = psum_v.tile([P, D], F32, tag="v")
            for c in range(CHUNKS):
                nc.tensor.transpose(
                    v_rows[:, P * c : P * (c + 1)], projected[t // GROUP][:, c, first : first + P], ident[:]
                )
            v_src[s] = v_rows

        sums = {}
        pairs = {}

        def spread(position):
            s = SOURCES[position]
            for j in range(TAPS - 1, -1, -1):
                t = s + NB - j
                if t < 0 or t >= TILES:
                    continue
                begins = s == max(t - NB, 0)
                ends = s == (t + NB if t >= NB else -1)
                if begins:
                    if t < NB:
                        fresh = const.tile([P, D], F32, name="sums_%d" % t)
                    else:
                        fresh = stage.tile([P, D], F32, tag="sums", bufs=TAPS)
                    sums[t] = fresh
                if ends and t % PAIR == 0:
                    mixed = result.tile([P, PAIR, D], F32, tag="mixed")
                    row_sum = small.tile([P, PAIR], F32, tag="row_sum")
                    pairs[t // PAIR] = (mixed, row_sum)
                e = t % PAIR
                nc.vector.scalar_tensor_tensor(
                    out=pairs[t // PAIR][0][:, e, :] if ends else sums[t][:],
                    in0=v_src[s][:],
                    scalar=band[:, TAPS * t + j : TAPS * t + j + 1],
                    in1=x_src[t // GROUP][:, t % GROUP, :] if begins else sums[t][:],
                    op0=ALU.mult,
                    op1=ALU.add,
                    accum_out=pairs[t // PAIR][1][:, e : e + 1] if ends else None,
                )
            restore(position + V_BANKS)

        def store_pair(pair):
            def store(normed, e=None):
                lo, hi = (0, PAIR) if e is None else (e, e + 1)
                nc.sync.dma_start(out=out_rows[:, PAIR * pair + lo : PAIR * pair + hi, :], in_=normed[:, lo:hi, :])

            return store

        def centre(row_sum, n):
            neg_mean = small.tile([P, PAIR], F32, tag="neg_mean")
            nc.scalar.mul(out=neg_mean[:, 0:n], in_=row_sum[:, 0:n], mul=-1.0 / D)
            return neg_mean

        def square(mixed, row_sum, square_sum, e):
            squares = small.tile([P, D], BF16, tag="squares", bufs=4)
            nc.scalar.activation(
                out=squares[:],
                in_=mixed[:, e, :],
                func=ACT.Square,
                bias=row_sum[:, e : e + 1],
                scale=-float(D),
                accum_out=square_sum[:, e : e + 1],
            )

        def invert(square_sum, n):
            rstd = small.tile([P, PAIR], F32, tag="rstd")
            nc.scalar.activation(
                out=rstd[:, 0:n],
                in_=square_sum[:, 0:n],
                func=ACT.Abs_reciprocal_sqrt,
                bias=eps_col[:, 0:1],
                scale=1.0 / D**3,
            )
            return rstd

        def normalise(mixed, neg_mean, rstd, n):
            for e in range(n):
                nc.gpsimd.tensor_scalar(
                    out=mixed[:, e, :],
                    in0=mixed[:, e, :],
                    scalar1=neg_mean[:, e : e + 1],
                    scalar2=rstd[:, e : e + 1],
                    op0=ALU.add,
                    op1=ALU.mult,
                )

        def finish_on_gpsimd(normed, n, store):
            nc.gpsimd.tensor_mul(out=normed[:, 0:n, :], in0=normed[:, 0:n, :], in1=gamma_pair[:, 0:n, :])
            nc.gpsimd.tensor_add(out=normed[:, 0:n, :], in0=normed[:, 0:n, :], in1=beta_pair[:, 0:n, :])

        columns = const.tile([P, 2, D], BF16)
        affine_col = const.tile([P, 2, CHUNKS], F32)

        def fill_affine():
            turned = psum_front.tile([P, 2, D], BF16, tag="front")
            for i, rows in enumerate((gamma_pair, beta_pair)):
                for c in range(CHUNKS):
                    nc.tensor.transpose(turned[:, i, P * c : P * (c + 1)], rows[:, 0, P * c : P * (c + 1)], ident_bf[:])
            nc.scalar.copy(out=columns[:], in_=turned[:])
            nc.scalar.copy(out=affine_col[:], in_=columns[:].rearrange("n i (c p) -> n i c p", c=CHUNKS)[:, :, :, 0])

        affine = []

        def affine_rows():
            bank = psum_front.tile([P, 2, D], BF16, tag="front")
            for i in range(2):
                for c in range(CHUNKS):
                    nc.tensor.transpose(bank[:, i, P * c : P * (c + 1)], columns[:, i, P * c : P * (c + 1)], ident_bf[:])
            affine.append(bank)

        thirds = []
        turned = []

        def turn(normed, n, store):
            if not thirds:
                by_feature = stage.tile([P, 3, CHUNKS, PAIR * P], F32, tag="weights", bufs=1)
                thirds.extend([by_feature[:, k, :, :] for k in range(3)])
            half = thirds[len(turned) % 3]
            turned.append(half)
            for c0 in range(0, CHUNKS, 2):
                bank = psum_front.tile([P, 2, PAIR * P], F32, tag="front")
                for c in range(2):
                    for e in range(n):
                        nc.tensor.transpose(
                            bank[:, c, P * e : P * (e + 1)], normed[:, e, P * (c0 + c) : P * (c0 + c + 1)], ident[:]
                        )
                for c in range(2):
                    nc.scalar.activation(
                        out=half[:, c0 + c, 0 : n * P],
                        in_=bank[:, c, 0 : n * P],
                        func=ACT.Identity,
                        bias=affine_col[:, 1, c0 + c : c0 + c + 1],
                        scale=affine_col[:, 0, c0 + c : c0 + c + 1],
                    )
            return half, normed, n, store

        def turn_back(half, normed, n, store, between):
            for e in range(n):
                bank = psum_front.tile([P, D], F32, tag="front")
                for c in range(CHUNKS):
                    nc.tensor.transpose(bank[:, P * c : P * (c + 1)], half[:, c, P * e : P * (e + 1)], ident[:])
                nc.scalar.copy(out=normed[:, e, :], in_=bank[:])
                between()
            store(normed)

        def finish_on_vector(mixed, neg_mean, rstd, n, store, by_tile):
            for e in range(n):
                nc.vector.scalar_tensor_tensor(
                    out=mixed[:, e, :],
                    in0=mixed[:, e, :],
                    scalar=neg_mean[:, e : e + 1],
                    in1=affine[0][:, 0, :],
                    op0=ALU.add,
                    op1=ALU.mult,
                )
            for e in range(n):
                nc.vector.scalar_tensor_tensor(
                    out=mixed[:, e, :],
                    in0=mixed[:, e, :],
                    scalar=rstd[:, e : e + 1],
                    in1=affine[0][:, 1, :],
                    op0=ALU.mult,
                    op1=ALU.add,
                )
                if by_tile:
                    store(mixed, e)
            if not by_tile:
                store(mixed)

        def band_project(i):
            product = psum_front.tile([P, D], F32, tag="front")
            nc.tensor.matmul_mx(
                out=product[:],
                lhsT=band_codes[:, P * i : P * (i + 1)].bitcast(FP8X4),
                lhsT_scale=band_scales[:, P * i : P * (i + 1)],
                rhs=w_words[:].bitcast(FP4X4),
                rhs_scale=w_scales[:],
                start=True,
                stop=True,
            )
            nc.scalar.copy(out=v_band[i % V_BUFS][0 : P - 1, :], in_=product[0 : P - 1, :])

        band_sums = {}

        def band_matmul(i):
            summed = psum_front.tile([P, D], F32, tag="front")
            nc.tensor.matmul(out=summed[:], lhsT=band_t[:, i, :], rhs=v_band[i % V_BUFS][:], start=True, stop=True)
            band_sums[i] = summed

        def band_add(i, mixed, row_sum):
            e = i % PAIR
            nc.vector.scalar_tensor_tensor(
                out=mixed[:, e, :],
                in0=band_sums[i][:],
                scalar=1.0,
                in1=x_band[i][:],
                op0=ALU.mult,
                op1=ALU.add,
                accum_out=row_sum[:, e : e + 1],
            )

        def band_store(i0, n):
            rows = min(BAND_STEP, BAND_ROWS - BAND_STEP * (i0 + n - 1))
            target = out_all[BAND_STEP * i0 : BAND_STEP * (i0 + n - 1) + rows, :].rearrange("(e m) d -> m e d", e=n)

            def store(normed):
                for lo, hi in ((0, 64), (64, 112), (112, rows)):
                    nc.sync.dma_start(out=target[lo:hi, :, :], in_=normed[NB + lo : NB + hi, 0:n, :])

            return store

        begin_first_group()
        front(1)
        for position in range(PAIR, V_BANKS):
            restore(position)

        band_open = None
        summed = []
        to_turn = {}
        to_turn_back = {}
        to_store = {}
        on_vector = []
        late = []

        def hand_over(slot, job):
            if slot >= VECTOR_FROM:
                late.append(job)
                how = "gpsimd" if len(late) in LATE else ("turn" if len(late) in LATE_TURN else "vector")
            elif slot >= TURN_FROM or job[4] == "vector":
                how = "turn"
            else:
                how = "gpsimd"
            summed.append((how,) + job[0:4])

        def layer_norms(step):
            for normed, n, store in to_store.get(step, []):
                store(normed)
            on_gpsimd = []
            to_turn[step + LAG] = []
            late_rstd = []

            def conclude(job):
                how, mixed, neg_mean, square_sum, n, store = job
                rstd = invert(square_sum, n)
                if how == "vector":
                    on_vector.append((mixed, neg_mean, rstd, n, store))
                    return
                normalise(mixed, neg_mean, rstd, n)
                if how == "gpsimd":
                    on_gpsimd.append((mixed, n, store))
                else:
                    to_turn[step + LAG].append((mixed, n, store))

            def conclude_waiting():
                for job in late_rstd:
                    conclude(job)
                late_rstd.clear()

            for how, mixed, row_sum, n, store in summed:
                square_sum = small.tile([P, PAIR], F32, tag="square_sum")
                for e in range(n):
                    square(mixed, row_sum, square_sum, e)
                    conclude_waiting()
                late_rstd.append((how, mixed, centre(row_sum, n), square_sum, n, store))
            summed.clear()
            for job in to_turn_back.get(step, []):
                turn_back(*job, between=conclude_waiting)
            conclude_waiting()
            to_turn_back[step + 1] = [turn(*job) for job in to_turn.get(step, [])]
            for job in on_gpsimd:
                finish_on_gpsimd(*job)
            when = step + STORE_LAG if step < VECTOR_FROM else SLOTS + 2
            to_store[when] = to_store.get(when, []) + on_gpsimd

        def fronts(slot):
            for g in range(2, SRC_GROUPS):
                if front_slot(g) == slot:
                    front(g)
            for h in range(BAND_GROUPS):
                if band_front_slot(h) == slot:
                    band_front(h)

        for slot in range(SLOTS):
            due = [i for i in range(BAND_TILES) if band_slot(i) == slot]
            for i in due:
                band_matmul(i)
            for i in range(BAND_TILES):
                if project_slot(i) == slot:
                    band_project(i)
            if slot > 0:
                fronts(slot)
            if slot == 1:
                fill_affine()
            if slot == VECTOR_FROM:
                affine_rows()
            spread(PAIR * slot)
            if slot == 0:
                quantise(1)
                project(1)
                fronts(0)
            if slot == 1:
                quantise(2)
            g = (slot + 3) // 2
            if slot % 2 == 1 and g < SRC_GROUPS:
                project(g)
            spread(PAIR * slot + 1)
            for g in range(3, SRC_GROUPS):
                if front_slot(g) + 1 == slot:
                    quantise(g)
            for h in range(BAND_GROUPS):
                if band_front_slot(h) + 1 == slot:
                    band_quantise(h)
            if slot > 1:
                pair = slot - 1 if slot < SLOTS - 1 else 0
                hand_over(slot, pairs[pair] + (PAIR, store_pair(pair), "vector"))
            layer_norms(slot)
            for i in due:
                if i % PAIR == 0:
                    mixed = result.tile([P, PAIR, D], F32, tag="mixed")
                    row_sum = small.tile([P, PAIR], F32, tag="row_sum")
                    band_open = (mixed, row_sum)
                band_add(i, *band_open)
                if i % PAIR == PAIR - 1 or i == BAND_TILES - 1:
                    n = i % PAIR + 1
                    hand_over(slot, band_open + (n, band_store(i + 1 - n, n), "band"))
        layer_norms(SLOTS)
        for job in on_vector[:-FINAL]:
            finish_on_vector(*job, by_tile=False)
        for step in range(SLOTS + 1, SLOTS + 3):
            layer_norms(step)
        for job in on_vector[-FINAL:]:
            finish_on_vector(*job, by_tile=job is on_vector[-1])
